import numpy as np
import ml_dtypes


def mxq(x, axis, fmt="e4m3"):
    dtype, down = {"e4m3": (ml_dtypes.float8_e4m3fn, 7), "e5m2": (ml_dtypes.float8_e5m2, 14)}[fmt]
    v = np.moveaxis(np.asarray(x, np.float32).astype(ml_dtypes.bfloat16).astype(np.float64), axis, -1)
    blocks = v.reshape(v.shape[:-1] + (-1, 32))
    amax = np.abs(blocks).max(-1, keepdims=True)
    byte = np.maximum(np.where(amax > 0, np.frexp(amax)[1] - 1 + 127, 0) - down, 1)
    scale = np.exp2(byte - 127.0)
    codes = (blocks / scale).astype(np.float32).astype(dtype).astype(np.float64)
    return np.moveaxis((codes * scale).reshape(v.shape), -1, axis)


WIDE = False


def mx_kscale(k):
    if not WIDE:
        return np.ones(k)
    levels = np.array([18, -18])
    if k % 512:
        return np.exp2(np.random.permutation(np.resize(levels, k // 32))).repeat(32)
    a = np.empty((k // 512, 16))
    for p in range(k // 512):
        a[p, :8] = np.random.permutation(np.resize(levels, 8))
        for g in range(8):
            far = levels[np.abs(levels - a[p, g]) >= 10]
            a[p, g + 8] = far[np.random.randint(len(far))]
    return np.exp2(a.ravel()).repeat(32)


BF16 = ml_dtypes.bfloat16


def bf(x):
    return np.asarray(x, np.float32).astype(BF16)


def f64(x):
    return np.asarray(x).astype(np.float64)


SL, BS, DM, H, NH, DO = 4, 512, 1024, 16, 64, 1024
DP = H * NH
T = BS * SL


def setup_inputs():
    s = mx_kscale(T).reshape(BS, SL)
    u = mx_kscale(DO)
    v = mx_kscale(DP)
    g = np.random.standard_normal((SL, BS, H)) * 2.0
    x0 = bf(np.random.standard_normal((SL, BS, DM)))
    logw = bf(g - np.log(np.exp(g).sum(0, keepdims=True)))
    wv0 = bf(np.random.standard_normal((DP, DM)) / np.sqrt(DM * SL))
    wo0 = bf(np.random.standard_normal((DO, DP)) * 0.5 / np.sqrt(DP))
    go = bf(np.random.standard_normal((BS, DO)) * np.exp2(np.random.randint(-6, 1, (BS, 1))) * 2.0 / s[:, :1] * u)
    pool_w = f64(logw)
    return {"values": bf(f64(x0) * s.T[:, :, None]),
            "logw": logw,
            "Wv": bf(f64(wv0) / v[:, None]),
            "Wo": bf(f64(wo0) * v[None, :] / u[:, None]),
            "pool_w": np.asarray(pool_w, np.float32),
            "grad_out": go}


def reference(values, logw, Wv, Wo, pool_w, grad_out):
    dattn = mxq(f64(grad_out), 1, "e5m2") @ mxq(f64(Wo), 0, "e4m3")
    pw = f64(pool_w).transpose(1, 0, 2)
    dvp = (pw[..., None] * dattn.reshape(BS, 1, H, NH)).reshape(T, DP)
    dx = mxq(dvp, 1, "e5m2") @ mxq(f64(Wv), 0, "e4m3")
    dvalues = dx.reshape(BS, SL, DM).transpose(1, 0, 2)
    xt = f64(values).transpose(1, 0, 2).reshape(T, DM)
    dWv = mxq(dvp, 0, "e5m2").T @ mxq(xt, 0, "e4m3")
    return dvalues, dWv

@@ -1,0 +1,277 @@
+from contextlib import ExitStack
+
+import concourse.mybir as mybir
+from concourse.masks import make_identity
+
+FLOPS = 2 * 512 * 1024 * 1024 + 2 * 2 * 2048 * 1024 * 1024
+BYTES = 2 * (4 * 512 * 1024 + 2 * 1024 * 1024 + 512 * 1024) + 4 * 4 * 512 * 16 + 4 * (2048 * 1024 + 1024 * 1024)
+
+F32 = mybir.dt.float32
+BF16 = mybir.dt.bfloat16
+U32 = mybir.dt.uint32
+U8 = mybir.dt.uint8
+E4 = mybir.dt.float8_e4m3fn_x4
+E5 = mybir.dt.float8_e5m2_x4
+MULT = mybir.AluOpType.mult
+P = 128
+SPAN = {"0": (0, 256), "1": (256, 256), "2": (512, 256), "3": (768, 256), "a": (0, 512), "b": (512, 512)}
+
+ORDER = """
+LWo00:D LWo10:D WoI000:V WoI001:S Lgo0:D WoI011:V WoI010:S Lgo1:D GT0:P WoQ00:V LWo01:D GT1:P GC0:S WoQ01:V
+Lpw:D GC1:S GQ0:V LWo11:D WoI100:S WoI101:V DA00:P GQ1:V LWv0:D M00:V WoI11a:S LWv1:D WoQ10:V WvI0a:S TT000:P
+WoQ11:V TT001:P DQ00:V DA01:P LX0:D WvI11:V WvI10:S M01:V TC000:S Lgo2:D Lgo3:D TC001:S LX1:D WvQ00:V DA10:P
+WvQ10:V GT2:P WvI13:S WvI0b:V TT010:P GC2:S M10:V TC010:S TT011:P TC011:S TQ00:V XI01:S TT100:P TQ01:V DA11:P
+WvQ01:V TC100:S GT3:P M11:V O0_000:P XI10:S O0_010:P O0_020:P GC3:S O0_030:P WvI12:V XI11:S TT101:P GQ2:V
+WvQ11:V E0_000:S DA20:P DQ01:V O0_001:P E0_010:S S0_000:D E0_030:V O0_011:P TC101:S S0_010:D M20:V TT110:P
+LX2:D E0_020:S O0_021:P TC110:S TT111:P XI00:V TC111:S DA21:P S0_020:D TQ10:V O0_031:P S0_030:D DQ10:V E0_001:S
+TT200:P E0_011:S TQ11:V S0_001:D E0_021:S DQ11:V LX3:D O0_100:P E0_031:S GQ3:V O0_110:P M21:V XI21:S O0_120:P
+O0_130:P TC200:S S0_011:D O0_101:P S0_021:D TT201:P XQ00:V E0_100:S S0_031:D TT210:P XI20:V E0_110:S S0_100:D
+DA30:P XQ10:V E0_120:S S0_110:D O0_111:P TC201:S DQ20:V S0_120:D O1_0000:P O1_0001:P XQ20:V TC210:S M30:V
+TT211:P O0_121:P E0_130:S TC211:S O0_131:P DQ21:V O1_0002:P XI31:S TT300:P XI30:V TT301:P DQ30:V E0_101:S
+DA31:P XQ30:V E0_111:S TQ20:V E0_121:S O1_0003:P O1_0100:P TQ21:V O1_0101:P E1_000:S O1_0102:P XI0b:V O1_0103:P
+E0_131:S O1_0200:P S1_000:D O1_0201:P XI22:S O1_0202:P S0_130:D O1_0203:P XI1b:V O0_200:P S0_101:D E1_010:S
+O1_0300:P O0_210:P E1_020:S XI23:V S1_010:D O1_0301:P E0_200:S O1_0302:P XQ01:V S0_111:D O0_220:P E0_210:S
+XQ11:V O1_0303:P S1_020:D O0_230:P XI3b:V E1_030:S S0_121:D O0_201:P E0_220:S S0_131:D O0_211:P E0_230:S XQ21:V
+S0_200:D O1_0010:P O0_221:P TC300:S XQ31:V S1_030:D O1_0011:P O1_0012:P M31:V O1_0013:P E0_201:S O1_0110:P
+O1_0111:P E0_211:S O1_0112:P O1_0113:P E1_001:S O1_0210:P O1_0211:P E1_011:S O1_0212:P S1_001:D O1_0213:P
+DQ31:V O1_0310:P S1_011:D E1_021:S O1_0311:P E0_221:V O1_0312:P S0_210:D O1_0313:P TC301:S O1_1000:P O1_1001:P
+S0_220:D O1_1002:P O1_1003:P E1_031:S S1_021:D O1_1100:P TQ30:V O1_1101:P E1_100:S O1_1102:P S1_031:D O1_1103:P
+O1_1200:P S0_230:D E1_110:S O1_1201:P O1_1202:P S0_201:D O1_1203:P O1_1300:P S0_211:D TT310:P S1_100:D TT311:P
+TC310:V S1_110:D O1_1301:P TC311:S O1_1302:P S0_221:D O1_1303:P O0_231:P E1_120:S O1_1010:P TQ31:V O1_1011:P
+E0_231:S O1_1012:P S1_120:D O1_1013:P E1_130:S O1_1110:P O1_1111:P E1_101:S O1_1112:P S1_130:D O0_300:P
+S1_101:D O0_310:P E0_300:S O1_1113:P S0_231:D E0_310:V O0_320:P E1_111:S S0_300:D O0_330:P E0_320:S S0_310:D
+O0_301:P E0_330:S O0_311:P S0_320:D E0_301:V O0_321:P S0_330:D E0_311:S O0_331:P S0_301:D E0_321:S O1_1210:P
+S1_111:D O1_1211:P E0_331:S O1_1212:P S0_311:D O1_1213:P O1_1310:P E1_121:S S0_321:D O1_1311:P O1_1312:P
+O1_1313:P S0_331:D E1_131:S S1_121:D S1_131:D
+"""
+
+
+def tile_multiheadattention_pb_v_kernel(tc, values, logw, Wv, Wo, pool_w, grad_out, out_0, out_1):
+    nc = tc.nc
+    with ExitStack() as ctx:
+        keep = ctx.enter_context(tc.tile_pool(name="keep", bufs=1))
+        work = ctx.enter_context(tc.tile_pool(name="work", bufs=1))
+        psum = ctx.enter_context(tc.psum_pool(name="psum", bufs=1))
+
+        ident = keep.tile([P, P], F32, name="ident")
+        make_identity(nc, ident[:])
+        pw = keep.tile([P, 4, 4, 16], F32, name="pw")
+        go_raw = [keep.tile([P, 1024], BF16, name="go_raw%d" % i) for i in range(4)]
+        goq = keep.tile([P, 4, 2, P], U32, name="goq", align_bytes=64)
+        gos = keep.tile([P, 4, 2, P], U8, name="gos", align_bytes=64)
+        woq = keep.tile([P, 2, 1024], U32, name="woq", align_bytes=64)
+        wos = keep.tile([P, 2, 1024], U8, name="wos", align_bytes=64)
+        wvq = keep.tile([P, 2, 1024], U32, name="wvq", align_bytes=64)
+        wvs = keep.tile([P, 2, 1024], U8, name="wvs", align_bytes=64)
+        xq = keep.tile([P, 4, 1024], U32, name="xq", align_bytes=64)
+        xs = keep.tile([P, 4, 1024], U8, name="xs", align_bytes=64)
+        dq = keep.tile([P, 4, 2, 512], U32, name="dq", align_bytes=64)
+        ds = keep.tile([P, 4, 2, 512], U8, name="ds", align_bytes=64)
+        tq = keep.tile([P, 4, 2, 512], U32, name="tq", align_bytes=64)
+        ts = keep.tile([P, 4, 2, 512], U8, name="ts", align_bytes=64)
+
+        live = {}
+
+        def move(e, out, in_):
+            if e == "V":
+                nc.vector.tensor_copy(out=out, in_=in_)
+            else:
+                nc.scalar.copy(out=out, in_=in_)
+
+        def big(key):
+            if key not in live:
+                live[key] = work.tile([P, 4, 1024], BF16, name="raw", bufs=6, align_bytes=64)
+            return live[key]
+
+        def stage(key):
+            if key not in live:
+                live[key] = work.tile([P, 512, 4], BF16, name="sx" if key[1] == "x" else "sw", bufs=4 if key[1] == "x" else 3, align_bytes=64)
+            return live[key]
+
+        def interleave(e, dst, src):
+            move(
+                e,
+                dst.rearrange("p (c i) t -> p c t i", i=4),
+                src.rearrange("p t (c i) -> p c t i", i=4),
+            )
+
+        def quant(codes, scales, src, fmt):
+            nc.vector.quantize_mx(out=codes.bitcast(fmt), scales=scales, in_=src)
+
+        def emit(name, e):
+            k = name[:2]
+            if name[0] == "L":
+                if name == "Lpw":
+                    for i in range(4):
+                        nc.scalar.dma_start(out=pw[:, i], in_=pool_w[:, P * i : P * (i + 1), :].rearrange("s p h -> p s h"))
+                elif name[1:3] == "go":
+                    i = int(name[3])
+                    nc.sync.dma_start(out=go_raw[i][:], in_=grad_out[P * i : P * (i + 1), :])
+                elif name[1:3] == "Wo":
+                    b, g = int(name[3]), int(name[4])
+                    nc.sync.dma_start(
+                        out=big("Wo%d" % b)[:, :, 512 * g : 512 * g + 512],
+                        in_=Wo[512 * b : 512 * b + 512, 512 * g : 512 * g + 512].rearrange("(p j) c -> p j c", j=4),
+                    )
+                elif name[1:3] == "Wv":
+                    g = int(name[3])
+                    nc.sync.dma_start(out=big("Wv%d" % g)[:], in_=Wv[512 * g : 512 * g + 512, :].rearrange("(p j) c -> p j c", j=4))
+                else:
+                    i = int(name[2])
+                    nc.sync.dma_start(out=big("X%d" % i)[:], in_=values[:, P * i : P * (i + 1), :].rearrange("s p d -> p s d"))
+            elif k == "GT":
+                i = int(name[2])
+                ps = psum.tile([P, 4, P], F32, name="tt", bufs=2)
+                live["tg%d" % i] = ps
+                words = go_raw[i][:].bitcast(F32)
+                for b in range(2):
+                    for u in range(2):
+                        nc.tensor.transpose(ps[:, 2 * b + u, :], words[:, 256 * b + u : 256 * b + 256 : 2], ident[:])
+            elif k == "GC":
+                i = int(name[2])
+                ps = live["tg%d" % i]
+                gt = work.tile([P, 2, P, 4], BF16, name="got", bufs=2, align_bytes=64)
+                live["got%d" % i] = gt
+                out = gt[:].rearrange("p g b t -> p (g b t)").bitcast(F32).rearrange("p (g b u) -> p g b u", g=2, b=P)
+                move(e, out, ps[:].rearrange("p (g u) b -> p g b u", g=2))
+            elif k == "GQ":
+                i = int(name[2])
+                gt = live["got%d" % i]
+                quant(
+                    goq[:, i].rearrange("p g b -> p (g b)"),
+                    gos[:, i].rearrange("p g b -> p (g b)"),
+                    gt[:].rearrange("p g b t -> p (g b t)"),
+                    E5,
+                )
+            elif name[:3] == "WoI":
+                g, b = int(name[3]), int(name[4])
+                c0, n = SPAN[name[5]]
+                st = stage("so%d%d" % (b, g))
+                interleave(e, st[:, c0 : c0 + n, :], big("Wo%d" % b)[:, :, 512 * g + c0 : 512 * g + c0 + n])
+            elif name[:3] == "WoQ":
+                g, b = int(name[3]), int(name[4])
+                cols = slice(512 * g, 512 * g + 512)
+                quant(woq[:, b, cols], wos[:, b, cols], stage("so%d%d" % (b, g))[:].rearrange("p c t -> p (c t)"), E4)
+            elif name[:3] == "WvI":
+                g = int(name[3])
+                c0, n = SPAN[name[4]]
+                st = stage("sv%d%d" % (g, c0 // 512))
+                interleave(e, st[:, c0 % 512 : c0 % 512 + n, :], big("Wv%d" % g)[:, :, c0 : c0 + n])
+            elif name[:3] == "WvQ":
+                g, h = int(name[3]), int(name[4])
+                cols = slice(512 * h, 512 * h + 512)
+                quant(wvq[:, g, cols], wvs[:, g, cols], stage("sv%d%d" % (g, h))[:].rearrange("p c t -> p (c t)"), E4)
+            elif k == "XI":
+                i = int(name[2])
+                c0, n = SPAN[name[3]]
+                st = stage("sx%d%d" % (i, c0 // 512))
+                interleave(e, st[:, c0 % 512 : c0 % 512 + n, :], big("X%d" % i)[:, :, c0 : c0 + n])
+            elif k == "XQ":
+                i, h = int(name[2]), int(name[3])
+                cols = slice(512 * h, 512 * h + 512)
+                quant(xq[:, i, cols], xs[:, i, cols], stage("sx%d%d" % (i, h))[:].rearrange("p c t -> p (c t)"), E4)
+            elif k == "DA":
+                i, g = int(name[2]), int(name[3])
+                ps = psum.tile([P, 512], F32, name="da", bufs=1)
+                live["da%d%d" % (i, g)] = ps
+                cols = slice(512 * g, 512 * g + 512)
+                for b in range(2):
+                    nc.tensor.matmul_mx(
+                        out=ps[:],
+                        lhsT=goq[:, i, b, :].bitcast(E5),
+                        lhsT_scale=gos[:, i, b, :],
+                        rhs=woq[:, b, cols].bitcast(E4),
+                        rhs_scale=wos[:, b, cols],
+                        start=(b == 0),
+                        stop=(b == 1),
+                    )
+            elif name[0] == "M":
+                i, g = int(name[1]), int(name[2])
+                ps = live["da%d%d" % (i, g)]
+                d = work.tile([P, 4, P, 4], BF16, name="dvp", bufs=5, align_bytes=64)
+                live["d%d%d" % (i, g)] = d
+                factor = pw[:, i, :, 8 * g : 8 * g + 8].rearrange("p s h -> p h s").unsqueeze(2).to_broadcast([P, 8, 16, 4])
+                for t in range(4):
+                    nc.vector.tensor_tensor(
+                        out=d[:, t].rearrange("p (h j) s -> p h j s", h=8),
+                        in0=ps[:].rearrange("p (h j t) -> p t h j", h=8, j=16)[:, t].unsqueeze(3).to_broadcast([P, 8, 16, 4]),
+                        in1=factor,
+                        op=MULT,
+                    )
+            elif k == "DQ":
+                i, g = int(name[2]), int(name[3])
+                quant(dq[:, i, g], ds[:, i, g], live["d%d%d" % (i, g)][:].rearrange("p t c s -> p (t c s)"), E5)
+            elif k == "TT":
+                i, g, u = int(name[2]), int(name[3]), int(name[4])
+                ps = psum.tile([P, 4, P], F32, name="tt", bufs=2)
+                live["tt%d%d%d" % (i, g, u)] = ps
+                words = live["d%d%d" % (i, g)][:].rearrange("p t c s -> p (t c s)").bitcast(F32)
+                for t in range(4):
+                    nc.tensor.transpose(ps[:, t, :], words[:, 256 * t + u : 256 * t + 256 : 2], ident[:])
+            elif k == "TC":
+                i, g, u = int(name[2]), int(name[3]), int(name[4])
+                ps = live["tt%d%d%d" % (i, g, u)]
+                key = "t%d%d" % (i, g)
+                if key not in live:
+                    live[key] = work.tile([P, 4, P, 4], BF16, name="dvt", bufs=3, align_bytes=64)
+                move(
+                    e,
+                    live[key][:, 2 * u : 2 * u + 2],
+                    ps[:].rearrange("p t b -> p (t b)").bitcast(BF16).rearrange("p (t b e) -> p e b t", t=4, b=P),
+                )
+            elif k == "TQ":
+                i, g = int(name[2]), int(name[3])
+                quant(tq[:, i, g], ts[:, i, g], live["t%d%d" % (i, g)][:].rearrange("p s b t -> p (s b t)"), E5)
+            elif k == "O1":
+                g, t, h, i = int(name[3]), int(name[4]), int(name[5]), int(name[6])
+                key = "a1%d%d%d" % (g, t, h)
+                if i == 0:
+                    live[key] = psum.tile([P, 512], F32, name="acc", bufs=5)
+                cols = slice(512 * h, 512 * h + 512)
+                m = slice(P * t, P * t + P)
+                nc.tensor.matmul_mx(
+                    out=live[key][:],
+                    lhsT=dq[:, i, g, m].bitcast(E5),
+                    lhsT_scale=ds[:, i, g, m],
+                    rhs=xq[:, i, cols].bitcast(E4),
+                    rhs_scale=xs[:, i, cols],
+                    start=(i == 0),
+                    stop=(i == 3),
+                )
+            elif k == "O0":
+                i, s, h = int(name[3]), int(name[4]), int(name[5])
+                ps = psum.tile([P, 512], F32, name="acc", bufs=5)
+                live["a0%d%d%d" % (i, s, h)] = ps
+                cols = slice(512 * h, 512 * h + 512)
+                m = slice(P * s, P * s + P)
+                for g in range(2):
+                    nc.tensor.matmul_mx(
+                        out=ps[:],
+                        lhsT=tq[:, i, g, m].bitcast(E5),
+                        lhsT_scale=ts[:, i, g, m],
+                        rhs=wvq[:, g, cols].bitcast(E4),
+                        rhs_scale=wvs[:, g, cols],
+                        start=(g == 0),
+                        stop=(g == 1),
+                    )
+            elif k == "E0" or k == "E1":
+                a, b, h = int(name[3]), int(name[4]), int(name[5])
+                r = work.tile([P, 512], F32, name="r0" if k == "E0" else "r1", bufs=8 if k == "E0" else 4)
+                live["r%s%d%d%d" % (k[1], a, b, h)] = r
+                move(e, r[:], live["a%s%d%d%d" % (k[1], a, b, h)][:])
+            elif k == "S0":
+                i, s, h = int(name[3]), int(name[4]), int(name[5])
+                nc.sync.dma_start(
+                    out=out_0[s, P * i : P * (i + 1), 512 * h : 512 * h + 512],
+                    in_=live["r0%d%d%d" % (i, s, h)][:],
+                )
+            elif k == "S1":
+                g, t, h = int(name[3]), int(name[4]), int(name[5])
+                nc.sync.dma_start(
+                    out=out_1[512 * g : 512 * g + 512, 512 * h : 512 * h + 512].rearrange("(p t) d -> p t d", t=4)[:, t, :],
+                    in_=live["r1%d%d%d" % (g, t, h)][:],
+                )
+
+        with tc.manual_schedule():
+            for token in ORDER.split():
+                emit(token[:-2], token[-1])

@@ -14,36 +14,11 @@ E4 = mybir.dt.float8_e4m3fn_x4
 E5 = mybir.dt.float8_e5m2_x4
 MULT = mybir.AluOpType.mult
 P = 128
-SPAN = {"0": (0, 256), "1": (256, 256), "2": (512, 256), "3": (768, 256), "a": (0, 512), "b": (512, 512)}
-
-ORDER = """
-LWo00:D LWo10:D WoI000:V WoI001:S Lgo0:D WoI011:V WoI010:S Lgo1:D GT0:P WoQ00:V LWo01:D GT1:P GC0:S WoQ01:V
-Lpw:D GC1:S GQ0:V LWo11:D WoI100:S WoI101:V DA00:P GQ1:V LWv0:D M00:V WoI11a:S LWv1:D WoQ10:V WvI0a:S TT000:P
-WoQ11:V TT001:P DQ00:V DA01:P LX0:D WvI11:V WvI10:S M01:V TC000:S Lgo2:D Lgo3:D TC001:S LX1:D WvQ00:V DA10:P
-WvQ10:V GT2:P WvI13:S WvI0b:V TT010:P GC2:S M10:V TC010:S TT011:P TC011:S TQ00:V XI01:S TT100:P TQ01:V DA11:P
-WvQ01:V TC100:S GT3:P M11:V O0_000:P XI10:S O0_010:P O0_020:P GC3:S O0_030:P WvI12:V XI11:S TT101:P GQ2:V
-WvQ11:V E0_000:S DA20:P DQ01:V O0_001:P E0_010:S S0_000:D E0_030:V O0_011:P TC101:S S0_010:D M20:V TT110:P
-LX2:D E0_020:S O0_021:P TC110:S TT111:P XI00:V TC111:S DA21:P S0_020:D TQ10:V O0_031:P S0_030:D DQ10:V E0_001:S
-TT200:P E0_011:S TQ11:V S0_001:D E0_021:S DQ11:V LX3:D O0_100:P E0_031:S GQ3:V O0_110:P M21:V XI21:S O0_120:P
-O0_130:P TC200:S S0_011:D O0_101:P S0_021:D TT201:P XQ00:V E0_100:S S0_031:D TT210:P XI20:V E0_110:S S0_100:D
-DA30:P XQ10:V E0_120:S S0_110:D O0_111:P TC201:S DQ20:V S0_120:D O1_0000:P O1_0001:P XQ20:V TC210:S M30:V
-TT211:P O0_121:P E0_130:S TC211:S O0_131:P DQ21:V O1_0002:P XI31:S TT300:P XI30:V TT301:P DQ30:V E0_101:S
-DA31:P XQ30:V E0_111:S TQ20:V E0_121:S O1_0003:P O1_0100:P TQ21:V O1_0101:P E1_000:S O1_0102:P XI0b:V O1_0103:P
-E0_131:S O1_0200:P S1_000:D O1_0201:P XI22:S O1_0202:P S0_130:D O1_0203:P XI1b:V O0_200:P S0_101:D E1_010:S
-O1_0300:P O0_210:P E1_020:S XI23:V S1_010:D O1_0301:P E0_200:S O1_0302:P XQ01:V S0_111:D O0_220:P E0_210:S
-XQ11:V O1_0303:P S1_020:D O0_230:P XI3b:V E1_030:S S0_121:D O0_201:P E0_220:S S0_131:D O0_211:P E0_230:S XQ21:V
-S0_200:D O1_0010:P O0_221:P TC300:S XQ31:V S1_030:D O1_0011:P O1_0012:P M31:V O1_0013:P E0_201:S O1_0110:P
-O1_0111:P E0_211:S O1_0112:P O1_0113:P E1_001:S O1_0210:P O1_0211:P E1_011:S O1_0212:P S1_001:D O1_0213:P
-DQ31:V O1_0310:P S1_011:D E1_021:S O1_0311:P E0_221:V O1_0312:P S0_210:D O1_0313:P TC301:S O1_1000:P O1_1001:P
-S0_220:D O1_1002:P O1_1003:P E1_031:S S1_021:D O1_1100:P TQ30:V O1_1101:P E1_100:S O1_1102:P S1_031:D O1_1103:P
-O1_1200:P S0_230:D E1_110:S O1_1201:P O1_1202:P S0_201:D O1_1203:P O1_1300:P S0_211:D TT310:P S1_100:D TT311:P
-TC310:V S1_110:D O1_1301:P TC311:S O1_1302:P S0_221:D O1_1303:P O0_231:P E1_120:S O1_1010:P TQ31:V O1_1011:P
-E0_231:S O1_1012:P S1_120:D O1_1013:P E1_130:S O1_1110:P O1_1111:P E1_101:S O1_1112:P S1_130:D O0_300:P
-S1_101:D O0_310:P E0_300:S O1_1113:P S0_231:D E0_310:V O0_320:P E1_111:S S0_300:D O0_330:P E0_320:S S0_310:D
-O0_301:P E0_330:S O0_311:P S0_320:D E0_301:V O0_321:P S0_330:D E0_311:S O0_331:P S0_301:D E0_321:S O1_1210:P
-S1_111:D O1_1211:P E0_331:S O1_1212:P S0_311:D O1_1213:P O1_1310:P E1_121:S S0_321:D O1_1311:P O1_1312:P
-O1_1313:P S0_331:D E1_131:S S1_121:D S1_131:D
-"""
+HALF = 512
+STAGES = 5
+TURNED = 3
+ROWS = 6
+CODES = 6
 
 
 def tile_multiheadattention_pb_v_kernel(tc, values, logw, Wv, Wo, pool_w, grad_out, out_0, out_1):
@@ -55,223 +30,375 @@ def tile_multiheadattention_pb_v_kernel(tc, values, logw, Wv, Wo, pool_w, grad_o
 
         ident = keep.tile([P, P], F32, name="ident")
         make_identity(nc, ident[:])
-        pw = keep.tile([P, 4, 4, 16], F32, name="pw")
+        pw = [keep.tile([P, 4, 16], F32, name="pw%d" % i) for i in range(4)]
         go_raw = [keep.tile([P, 1024], BF16, name="go_raw%d" % i) for i in range(4)]
-        goq = keep.tile([P, 4, 2, P], U32, name="goq", align_bytes=64)
-        gos = keep.tile([P, 4, 2, P], U8, name="gos", align_bytes=64)
-        woq = keep.tile([P, 2, 1024], U32, name="woq", align_bytes=64)
-        wos = keep.tile([P, 2, 1024], U8, name="wos", align_bytes=64)
-        wvq = keep.tile([P, 2, 1024], U32, name="wvq", align_bytes=64)
-        wvs = keep.tile([P, 2, 1024], U8, name="wvs", align_bytes=64)
-        xq = keep.tile([P, 4, 1024], U32, name="xq", align_bytes=64)
-        xs = keep.tile([P, 4, 1024], U8, name="xs", align_bytes=64)
-        dq = keep.tile([P, 4, 2, 512], U32, name="dq", align_bytes=64)
-        ds = keep.tile([P, 4, 2, 512], U8, name="ds", align_bytes=64)
-        tq = keep.tile([P, 4, 2, 512], U32, name="tq", align_bytes=64)
-        ts = keep.tile([P, 4, 2, 512], U8, name="ts", align_bytes=64)
+        goq = [keep.tile([P, 2 * P], U32, name="goq%d" % i, align_bytes=64) for i in range(4)]
+        gos = [keep.tile([P, 2 * P], U8, name="gos%d" % i, align_bytes=64) for i in range(4)]
+        dvp = [keep.tile([P, 4 * 4 * HALF], BF16, name="dvp%d" % g, align_bytes=64) for g in range(2)]
+        raw = {}
+        codes = {}
+        scales = {}
+        staged = {}
+        banks = {}
+        rows = {}
 
-        live = {}
-
-        def move(e, out, in_):
-            if e == "V":
+        def copy_on(engine, out, in_):
+            if engine == "V":
                 nc.vector.tensor_copy(out=out, in_=in_)
             else:
                 nc.scalar.copy(out=out, in_=in_)
 
-        def big(key):
-            if key not in live:
-                live[key] = work.tile([P, 4, 1024], BF16, name="raw", bufs=6, align_bytes=64)
-            return live[key]
+        def quantise(key, src, fmt):
+            width = src.shape[1] // 4
+            if key[0] in ("t", "d"):
+                codes[key] = work.tile([P, width], U32, name="q_dvp", bufs=CODES, align_bytes=64)
+                scales[key] = work.tile([P, width], U8, name="s_dvp", bufs=CODES, align_bytes=64)
+            else:
+                codes[key] = keep.tile([P, width], U32, name="q_%s%d%d" % key, align_bytes=64)
+                scales[key] = keep.tile([P, width], U8, name="s_%s%d%d" % key, align_bytes=64)
+            nc.vector.quantize_mx(out=codes[key][:].bitcast(fmt), scales=scales[key][:], in_=src)
+
+        def bank(n, shape):
+            return psum.tile(shape, F32, name="bank%d" % n)
 
         def stage(key):
-            if key not in live:
-                live[key] = work.tile([P, 512, 4], BF16, name="sx" if key[1] == "x" else "sw", bufs=4 if key[1] == "x" else 3, align_bytes=64)
-            return live[key]
+            if key not in staged:
+                staged[key] = work.tile([P, HALF, 4], BF16, name="stage", bufs=STAGES, align_bytes=64)
+            return staged[key]
 
-        def interleave(e, dst, src):
-            move(
-                e,
-                dst.rearrange("p (c i) t -> p c t i", i=4),
-                src.rearrange("p t (c i) -> p c t i", i=4),
+        def load_pw(i, queue):
+            queue.dma_start(out=pw[i][:], in_=pool_w[:, P * i : P * (i + 1), :].rearrange("s p h -> p s h"))
+
+        def load_go(i):
+            nc.sync.dma_start(out=go_raw[i][:], in_=grad_out[P * i : P * (i + 1), :])
+
+        def load_w(name, a, h):
+            weight = Wo if name == "wo" else Wv
+            raw[name, a, h] = keep.tile([P, 4, HALF], BF16, name="raw_%s%d%d" % (name, a, h))
+            nc.sync.dma_start(
+                out=raw[name, a, h][:],
+                in_=weight[HALF * a : HALF * (a + 1), HALF * h : HALF * (h + 1)].rearrange("(p j) c -> p j c", j=4),
             )
 
-        def quant(codes, scales, src, fmt):
-            nc.vector.quantize_mx(out=codes.bitcast(fmt), scales=scales, in_=src)
+        def load_w_whole(name, a):
+            weight = Wo if name == "wo" else Wv
+            whole = keep.tile([P, 4, 2 * HALF], BF16, name="raw_%s%d" % (name, a))
+            nc.sync.dma_start(out=whole[:], in_=weight[HALF * a : HALF * (a + 1), :].rearrange("(p j) c -> p j c", j=4))
+            for h in range(2):
+                raw[name, a, h] = whole[:, :, HALF * h : HALF * (h + 1)]
 
-        def emit(name, e):
-            k = name[:2]
-            if name[0] == "L":
-                if name == "Lpw":
-                    for i in range(4):
-                        nc.scalar.dma_start(out=pw[:, i], in_=pool_w[:, P * i : P * (i + 1), :].rearrange("s p h -> p s h"))
-                elif name[1:3] == "go":
-                    i = int(name[3])
-                    nc.sync.dma_start(out=go_raw[i][:], in_=grad_out[P * i : P * (i + 1), :])
-                elif name[1:3] == "Wo":
-                    b, g = int(name[3]), int(name[4])
-                    nc.sync.dma_start(
-                        out=big("Wo%d" % b)[:, :, 512 * g : 512 * g + 512],
-                        in_=Wo[512 * b : 512 * b + 512, 512 * g : 512 * g + 512].rearrange("(p j) c -> p j c", j=4),
-                    )
-                elif name[1:3] == "Wv":
-                    g = int(name[3])
-                    nc.sync.dma_start(out=big("Wv%d" % g)[:], in_=Wv[512 * g : 512 * g + 512, :].rearrange("(p j) c -> p j c", j=4))
-                else:
-                    i = int(name[2])
-                    nc.sync.dma_start(out=big("X%d" % i)[:], in_=values[:, P * i : P * (i + 1), :].rearrange("s p d -> p s d"))
-            elif k == "GT":
-                i = int(name[2])
-                ps = psum.tile([P, 4, P], F32, name="tt", bufs=2)
-                live["tg%d" % i] = ps
-                words = go_raw[i][:].bitcast(F32)
-                for b in range(2):
-                    for u in range(2):
-                        nc.tensor.transpose(ps[:, 2 * b + u, :], words[:, 256 * b + u : 256 * b + 256 : 2], ident[:])
-            elif k == "GC":
-                i = int(name[2])
-                ps = live["tg%d" % i]
-                gt = work.tile([P, 2, P, 4], BF16, name="got", bufs=2, align_bytes=64)
-                live["got%d" % i] = gt
-                out = gt[:].rearrange("p g b t -> p (g b t)").bitcast(F32).rearrange("p (g b u) -> p g b u", g=2, b=P)
-                move(e, out, ps[:].rearrange("p (g u) b -> p g b u", g=2))
-            elif k == "GQ":
-                i = int(name[2])
-                gt = live["got%d" % i]
-                quant(
-                    goq[:, i].rearrange("p g b -> p (g b)"),
-                    gos[:, i].rearrange("p g b -> p (g b)"),
-                    gt[:].rearrange("p g b t -> p (g b t)"),
-                    E5,
+        def load_x(i):
+            whole = keep.tile([P, 4, 2 * HALF], BF16, name="raw_x%d" % i)
+            nc.sync.dma_start(out=whole[:], in_=values[:, P * i : P * (i + 1), :].rearrange("s p d -> p s d"))
+            for h in range(2):
+                raw["x", i, h] = whole[:, :, HALF * h : HALF * (h + 1)]
+
+        def weave(engine, name, a, h, part=0, parts=1):
+            n = HALF // parts
+            src = raw[name, a, h][:, :, n * part : n * (part + 1)]
+            dst = stage((name, a, h))
+            if name == "wo":
+                dst = dst[:].rearrange("p (u r) t -> p u r t", u=2)[:, :, n // 2 * part : n // 2 * (part + 1), :]
+                copy_on(
+                    engine,
+                    dst.rearrange("p u (r l) t -> p r t l u", l=2),
+                    src.rearrange("p t (r l u) -> p r t l u", l=2, u=2),
                 )
-            elif name[:3] == "WoI":
-                g, b = int(name[3]), int(name[4])
-                c0, n = SPAN[name[5]]
-                st = stage("so%d%d" % (b, g))
-                interleave(e, st[:, c0 : c0 + n, :], big("Wo%d" % b)[:, :, 512 * g + c0 : 512 * g + c0 + n])
-            elif name[:3] == "WoQ":
-                g, b = int(name[3]), int(name[4])
-                cols = slice(512 * g, 512 * g + 512)
-                quant(woq[:, b, cols], wos[:, b, cols], stage("so%d%d" % (b, g))[:].rearrange("p c t -> p (c t)"), E4)
-            elif name[:3] == "WvI":
-                g = int(name[3])
-                c0, n = SPAN[name[4]]
-                st = stage("sv%d%d" % (g, c0 // 512))
-                interleave(e, st[:, c0 % 512 : c0 % 512 + n, :], big("Wv%d" % g)[:, :, c0 : c0 + n])
-            elif name[:3] == "WvQ":
-                g, h = int(name[3]), int(name[4])
-                cols = slice(512 * h, 512 * h + 512)
-                quant(wvq[:, g, cols], wvs[:, g, cols], stage("sv%d%d" % (g, h))[:].rearrange("p c t -> p (c t)"), E4)
-            elif k == "XI":
-                i = int(name[2])
-                c0, n = SPAN[name[3]]
-                st = stage("sx%d%d" % (i, c0 // 512))
-                interleave(e, st[:, c0 % 512 : c0 % 512 + n, :], big("X%d" % i)[:, :, c0 : c0 + n])
-            elif k == "XQ":
-                i, h = int(name[2]), int(name[3])
-                cols = slice(512 * h, 512 * h + 512)
-                quant(xq[:, i, cols], xs[:, i, cols], stage("sx%d%d" % (i, h))[:].rearrange("p c t -> p (c t)"), E4)
-            elif k == "DA":
-                i, g = int(name[2]), int(name[3])
-                ps = psum.tile([P, 512], F32, name="da", bufs=1)
-                live["da%d%d" % (i, g)] = ps
-                cols = slice(512 * g, 512 * g + 512)
-                for b in range(2):
-                    nc.tensor.matmul_mx(
-                        out=ps[:],
-                        lhsT=goq[:, i, b, :].bitcast(E5),
-                        lhsT_scale=gos[:, i, b, :],
-                        rhs=woq[:, b, cols].bitcast(E4),
-                        rhs_scale=wos[:, b, cols],
-                        start=(b == 0),
-                        stop=(b == 1),
-                    )
-            elif name[0] == "M":
-                i, g = int(name[1]), int(name[2])
-                ps = live["da%d%d" % (i, g)]
-                d = work.tile([P, 4, P, 4], BF16, name="dvp", bufs=5, align_bytes=64)
-                live["d%d%d" % (i, g)] = d
-                factor = pw[:, i, :, 8 * g : 8 * g + 8].rearrange("p s h -> p h s").unsqueeze(2).to_broadcast([P, 8, 16, 4])
-                for t in range(4):
-                    nc.vector.tensor_tensor(
-                        out=d[:, t].rearrange("p (h j) s -> p h j s", h=8),
-                        in0=ps[:].rearrange("p (h j t) -> p t h j", h=8, j=16)[:, t].unsqueeze(3).to_broadcast([P, 8, 16, 4]),
-                        in1=factor,
-                        op=MULT,
-                    )
-            elif k == "DQ":
-                i, g = int(name[2]), int(name[3])
-                quant(dq[:, i, g], ds[:, i, g], live["d%d%d" % (i, g)][:].rearrange("p t c s -> p (t c s)"), E5)
-            elif k == "TT":
-                i, g, u = int(name[2]), int(name[3]), int(name[4])
-                ps = psum.tile([P, 4, P], F32, name="tt", bufs=2)
-                live["tt%d%d%d" % (i, g, u)] = ps
-                words = live["d%d%d" % (i, g)][:].rearrange("p t c s -> p (t c s)").bitcast(F32)
-                for t in range(4):
-                    nc.tensor.transpose(ps[:, t, :], words[:, 256 * t + u : 256 * t + 256 : 2], ident[:])
-            elif k == "TC":
-                i, g, u = int(name[2]), int(name[3]), int(name[4])
-                ps = live["tt%d%d%d" % (i, g, u)]
-                key = "t%d%d" % (i, g)
-                if key not in live:
-                    live[key] = work.tile([P, 4, P, 4], BF16, name="dvt", bufs=3, align_bytes=64)
-                move(
-                    e,
-                    live[key][:, 2 * u : 2 * u + 2],
-                    ps[:].rearrange("p t b -> p (t b)").bitcast(BF16).rearrange("p (t b e) -> p e b t", t=4, b=P),
+            elif name == "wv":
+                copy_on(
+                    engine,
+                    dst[:, n * part : n * (part + 1), :].rearrange("p (c i) (u e) -> p c u e i", i=4, u=2),
+                    src.rearrange("p (e u) (c i) -> p c u e i", i=4, u=2),
                 )
-            elif k == "TQ":
-                i, g = int(name[2]), int(name[3])
-                quant(tq[:, i, g], ts[:, i, g], live["t%d%d" % (i, g)][:].rearrange("p s b t -> p (s b t)"), E5)
-            elif k == "O1":
-                g, t, h, i = int(name[3]), int(name[4]), int(name[5]), int(name[6])
-                key = "a1%d%d%d" % (g, t, h)
-                if i == 0:
-                    live[key] = psum.tile([P, 512], F32, name="acc", bufs=5)
-                cols = slice(512 * h, 512 * h + 512)
-                m = slice(P * t, P * t + P)
+            else:
+                copy_on(
+                    engine,
+                    dst[:, n * part : n * (part + 1), :].rearrange("p (c i) t -> p c t i", i=4),
+                    src.rearrange("p t (c i) -> p c t i", i=4),
+                )
+
+        def quant_staged(name, a, h):
+            quantise((name, a, h), staged[name, a, h][:].rearrange("p c t -> p (c t)"), E5 if name == "d" else E4)
+
+        def turn_go(i, n):
+            banks["go", i] = bank(n, [P, 4, P])
+            words = go_raw[i][:].bitcast(F32)
+            for a in range(2):
+                for u in range(2):
+                    nc.tensor.transpose(banks["go", i][:, 2 * a + u, :], words[:, 256 * a + u : 256 * a + 256 : 2], ident[:])
+
+        def copy_go(engine, i):
+            staged["go", i] = work.tile([P, 2 * P * 2], F32, name="go_t", bufs=2, align_bytes=64)
+            copy_on(
+                engine,
+                staged["go", i][:].rearrange("p (a b u) -> p a b u", a=2, u=2),
+                banks["go", i][:].rearrange("p (a u) b -> p a b u", u=2),
+            )
+
+        def quant_go(i):
+            nc.vector.quantize_mx(out=goq[i][:].bitcast(E5), scales=gos[i][:], in_=staged["go", i][:].bitcast(BF16))
+
+        def dattn(i, g, n):
+            banks["da", i, g] = bank(n, [P, HALF])
+            for a in range(2):
                 nc.tensor.matmul_mx(
-                    out=live[key][:],
-                    lhsT=dq[:, i, g, m].bitcast(E5),
-                    lhsT_scale=ds[:, i, g, m],
-                    rhs=xq[:, i, cols].bitcast(E4),
-                    rhs_scale=xs[:, i, cols],
-                    start=(i == 0),
-                    stop=(i == 3),
+                    out=banks["da", i, g][:],
+                    lhsT=goq[i][:, P * a : P * (a + 1)].bitcast(E5),
+                    lhsT_scale=gos[i][:, P * a : P * (a + 1)],
+                    rhs=codes["wo", a, g][:].bitcast(E4),
+                    rhs_scale=scales["wo", a, g][:],
+                    start=(a == 0),
+                    stop=(a == 1),
                 )
-            elif k == "O0":
-                i, s, h = int(name[3]), int(name[4]), int(name[5])
-                ps = psum.tile([P, 512], F32, name="acc", bufs=5)
-                live["a0%d%d%d" % (i, s, h)] = ps
-                cols = slice(512 * h, 512 * h + 512)
-                m = slice(P * s, P * s + P)
-                for g in range(2):
-                    nc.tensor.matmul_mx(
-                        out=ps[:],
-                        lhsT=tq[:, i, g, m].bitcast(E5),
-                        lhsT_scale=ts[:, i, g, m],
-                        rhs=wvq[:, g, cols].bitcast(E4),
-                        rhs_scale=wvs[:, g, cols],
-                        start=(g == 0),
-                        stop=(g == 1),
-                    )
-            elif k == "E0" or k == "E1":
-                a, b, h = int(name[3]), int(name[4]), int(name[5])
-                r = work.tile([P, 512], F32, name="r0" if k == "E0" else "r1", bufs=8 if k == "E0" else 4)
-                live["r%s%d%d%d" % (k[1], a, b, h)] = r
-                move(e, r[:], live["a%s%d%d%d" % (k[1], a, b, h)][:])
-            elif k == "S0":
-                i, s, h = int(name[3]), int(name[4]), int(name[5])
-                nc.sync.dma_start(
-                    out=out_0[s, P * i : P * (i + 1), 512 * h : 512 * h + 512],
-                    in_=live["r0%d%d%d" % (i, s, h)][:],
+
+        def plane(i, g, s):
+            return dvp[g][:, HALF * (4 * i + s) : HALF * (4 * i + s + 1)]
+
+        def weigh(k, g):
+            i = k // 2
+            for s in (2 * (k % 2), 2 * (k % 2) + 1):
+                nc.vector.tensor_tensor(
+                    out=plane(i, g, s).rearrange("p (u h j) -> p u h j", u=2, h=8),
+                    in0=banks["da", i, g][:].rearrange("p (u h j) -> p u h j", u=2, h=8),
+                    in1=pw[i][:, s, 8 * g : 8 * g + 8].unsqueeze(1).unsqueeze(3).to_broadcast([P, 2, 8, 32]),
+                    op=MULT,
                 )
-            elif k == "S1":
-                g, t, h = int(name[3]), int(name[4]), int(name[5])
-                nc.sync.dma_start(
-                    out=out_1[512 * g : 512 * g + 512, 512 * h : 512 * h + 512].rearrange("(p t) d -> p t d", t=4)[:, t, :],
-                    in_=live["r1%d%d%d" % (g, t, h)][:],
+
+        def turn(k, g, n):
+            banks["t", k, g] = bank(n, [P, 4, P])
+            for e in range(2):
+                words = plane(k // 2, g, 2 * (k % 2) + e).bitcast(F32)
+                for u in range(2):
+                    nc.tensor.transpose(banks["t", k, g][:, 2 * e + u, :], words[:, P * u : P * (u + 1)], ident[:])
+
+        def copy_turned(engine, k, g):
+            if ("t", k) not in staged:
+                staged["t", k] = work.tile([P, 2 * HALF], F32, name="turned", bufs=TURNED, align_bytes=64)
+            copy_on(
+                engine,
+                staged["t", k][:, HALF * g : HALF * (g + 1)].rearrange("p (e b u) -> p e b u", e=2, u=2),
+                banks["t", k, g][:].rearrange("p (e u) b -> p e b u", u=2),
+            )
+
+        def quant_turned(k):
+            quantise(("t", k, 0), staged["t", k][:].bitcast(BF16), E5)
+
+        def product0(k, e, h, n):
+            banks["o0", k, e, h] = bank(n, [P, HALF])
+            for g in range(2):
+                m = slice(P * (2 * g + e), P * (2 * g + e + 1))
+                nc.tensor.matmul_mx(
+                    out=banks["o0", k, e, h][:],
+                    lhsT=codes["t", k, 0][:, m].bitcast(E5),
+                    lhsT_scale=scales["t", k, 0][:, m],
+                    rhs=codes["wv", g, h][:].bitcast(E4),
+                    rhs_scale=scales["wv", g, h][:],
+                    start=(g == 0),
+                    stop=(g == 1),
                 )
+
+        def weave_d(engine, g, q, part=0, parts=1):
+            n = 4 // parts
+            src = dvp[g][:].rearrange("p (i s j) -> p i s j", i=4, s=4)[:, n * part : n * (part + 1), :, P * q : P * (q + 1)]
+            dst = stage(("d", g, q))[:].rearrange("p (i j) s -> p i j s", i=4)[:, n * part : n * (part + 1)]
+            copy_on(engine, dst.rearrange("p i (c l) s -> p i c s l", l=4), src.rearrange("p i s (c l) -> p i c s l", l=4))
+
+        def pass1(g, q, h, i, n):
+            if i == 0:
+                banks["o1", g, q, h] = bank(n, [P, HALF])
+            nc.tensor.matmul_mx(
+                out=banks["o1", g, q, h][:],
+                lhsT=codes["d", g, q][:, P * i : P * (i + 1)].bitcast(E5),
+                lhsT_scale=scales["d", g, q][:, P * i : P * (i + 1)],
+                rhs=codes["x", i, h][:].bitcast(E4),
+                rhs_scale=scales["x", i, h][:],
+                start=(i == 0),
+                stop=(i == 3),
+            )
+
+        def product1(g, q, h, n):
+            for i in range(4):
+                pass1(g, q, h, i, n)
+
+        def empty(engine, name, a, b, h):
+            if (name, a, b) not in rows:
+                rows[name, a, b] = work.tile([P, 2 * HALF], F32, name="rows", bufs=ROWS)
+            copy_on(engine, rows[name, a, b][:, HALF * h : HALF * (h + 1)], banks[name, a, b, h][:])
+
+        def store(name, a, b, lo=0, hi=2):
+            cols = slice(HALF * lo, HALF * hi)
+            if name == "o0":
+                dst = out_0[2 * (a % 2) + b, P * (a // 2) : P * (a // 2 + 1), cols]
+            else:
+                first = HALF * a + 256 * (b % 2)
+                dst = out_1[first : first + 256, cols].rearrange("(r u) d -> u r d", u=2)[b // 2]
+            nc.sync.dma_start(out=dst, in_=rows[name, a, b][:, cols])
 
         with tc.manual_schedule():
-            for token in ORDER.split():
-                emit(token[:-2], token[-1])
+            load_w("wo", 0, 0)
+            load_go(0)
+            load_w("wo", 1, 0)
+            load_w("wo", 0, 1)
+            load_w("wo", 1, 1)
+            load_pw(0, nc.sync)
+            load_w("wv", 0, 0)
+            load_w("wv", 1, 0)
+            load_go(1)
+            load_w("wv", 0, 1)
+            load_w("wv", 1, 1)
+            load_pw(1, nc.sync)
+            load_go(2)
+            load_x(0)
+            load_go(3)
+            load_pw(2, nc.sync)
+            load_x(1)
+            load_pw(3, nc.sync)
+            load_x(2)
+            load_x(3)
+            turn_go(0, 7)
+            weave("V", "wo", 0, 0, 0, 2)
+            weave("S", "wo", 0, 0, 1, 2)
+            copy_go("S", 0)
+            quant_staged("wo", 0, 0)
+            weave("V", "wo", 1, 0, 0, 2)
+            weave("S", "wo", 1, 0, 1, 2)
+            quant_go(0)
+            weave("V", "wo", 0, 1, 0, 2)
+            weave("S", "wo", 0, 1, 1, 2)
+            quant_staged("wo", 1, 0)
+            dattn(0, 0, 0)
+            weave("V", "wo", 1, 1, 0, 2)
+            weave("S", "wo", 1, 1, 1, 2)
+            quant_staged("wo", 0, 1)
+            weave("S", "wv", 0, 0)
+            quant_staged("wo", 1, 1)
+            dattn(0, 1, 1)
+            weigh(0, 0)
+            weigh(0, 1)
+            turn(0, 0, 2)
+            turn(0, 1, 3)
+            turn_go(1, 7)
+            weave("V", "wv", 1, 0, 0, 2)
+            copy_turned("S", 0, 0)
+            weave("S", "wv", 1, 0, 1, 2)
+            copy_turned("S", 0, 1)
+            quant_staged("wv", 0, 0)
+            quant_staged("wv", 1, 0)
+            quant_turned(0)
+            copy_go("S", 1)
+            weave("S", "wv", 0, 1)
+            weigh(1, 0)
+            weigh(1, 1)
+            quant_go(1)
+            product0(0, 0, 0, 4)
+            product0(0, 1, 0, 5)
+            turn(1, 0, 2)
+            turn(1, 1, 3)
+            dattn(1, 0, 0)
+            dattn(1, 1, 1)
+            turn_go(2, 6)
+            copy_turned("S", 1, 0)
+            copy_turned("S", 1, 1)
+            weave("V", "wv", 1, 1)
+            quant_turned(1)
+            quant_staged("wv", 0, 1)
+            quant_staged("wv", 1, 1)
+            empty("S", "o0", 0, 0, 0)
+            empty("S", "o0", 0, 1, 0)
+            copy_go("S", 2)
+            weigh(2, 0)
+            weigh(2, 1)
+            acc = 3
+            for k, e, h in ((1, 0, 0), (1, 1, 0), (0, 0, 1), (0, 1, 1)):
+                product0(k, e, h, 4 + acc % 4)
+                acc = acc + 1
+                empty("S", "o0", k, e, h)
+                if h == 1:
+                    store("o0", k, e)
+            for k in range(1, 8):
+                if k < 7:
+                    turn(k + 1, 0, 2)
+                    turn(k + 1, 1, 3)
+                if k == 1:
+                    turn_go(3, 4 + acc % 4)
+                    acc = acc + 1
+                if k in (2, 4):
+                    dattn(k // 2 + 1, 0, 0)
+                    dattn(k // 2 + 1, 1, 1)
+                if k < 7:
+                    copy_turned("S", k + 1, 0)
+                    copy_turned("S", k + 1, 1)
+                if k == 1:
+                    copy_go("S", 3)
+                    quant_go(2)
+                if k == 2:
+                    quant_go(3)
+                    weave("V", "x", 0, 0)
+                    weave("S", "x", 1, 0, 0, 2)
+                if k == 4:
+                    weave("V", "x", 2, 0)
+                if k < 6:
+                    weigh(k + 2, 0)
+                    weigh(k + 2, 1)
+                if k == 5:
+                    weave("V", "x", 1, 0, 1, 2)
+                    quant_staged("x", 0, 0)
+                if k < 7:
+                    quant_turned(k + 1)
+                if k == 5:
+                    weave("V", "x", 3, 0)
+                    quant_staged("x", 1, 0)
+                    quant_staged("x", 2, 0)
+                if k == 6:
+                    weave_d("V", 0, 0)
+                    quant_staged("x", 3, 0)
+                    quant_staged("d", 0, 0)
+                    weave_d("V", 0, 1)
+                if k == 7:
+                    quant_staged("d", 0, 1)
+                    weave_d("V", 0, 2)
+                for e, h in ((0, 0), (1, 0), (0, 1), (1, 1)):
+                    if k > 1 or h == 1:
+                        product0(k, e, h, 4 + acc % 4)
+                        acc = acc + 1
+                        empty("S", "o0", k, e, h)
+                        if h == 1:
+                            store("o0", k, e)
+            weave("S", "x", 0, 1)
+            quant_staged("d", 0, 2)
+            weave_d("V", 0, 3)
+            weave("S", "x", 1, 1)
+            quant_staged("d", 0, 3)
+            for q in range(4):
+                product1(0, q, 0, q)
+            quant_staged("x", 0, 1)
+            weave("S", "x", 2, 1)
+            weave("V", "x", 3, 1)
+            quant_staged("x", 1, 1)
+            weave_d("V", 1, 0)
+            for q in range(4):
+                empty("S", "o1", 0, q, 0)
+            quant_staged("x", 2, 1)
+            quant_staged("x", 3, 1)
+            quant_staged("d", 1, 0)
+            for i in range(4):
+                for q in range(4):
+                    pass1(0, q, 1, i, 4 + q)
+            weave_d("V", 1, 1)
+            weave_d("S", 1, 2, 0, 2)
+            quant_staged("d", 1, 1)
+            weave_d("V", 1, 2, 1, 2)
+            weave_d("V", 1, 3)
+            quant_staged("d", 1, 2)
+            quant_staged("d", 1, 3)
+            for q in range(4):
+                empty("S", "o1", 0, q, 1)
+                store("o1", 0, q)
+            for q in range(4):
+                for h in range(2):
+                    product1(1, q, h, 2 * q + h)
+                    empty("V" if h == 0 and q > 1 else "S", "o1", 1, q, h)
+                    if q == 3:
+                        store("o1", 1, q, h, h + 1)
+                if q < 3:
+                    store("o1", 1, q)

@@ -15,7 +15,7 @@ E5 = mybir.dt.float8_e5m2_x4
 MULT = mybir.AluOpType.mult
 P = 128
 HALF = 512
-STAGES = 5
+STAGES = 6
 TURNED = 3
 ROWS = 6
 CODES = 6
@@ -74,18 +74,12 @@ def tile_multiheadattention_pb_v_kernel(tc, values, logw, Wv, Wo, pool_w, grad_o
 
         def load_w(name, a, h):
             weight = Wo if name == "wo" else Wv
-            raw[name, a, h] = keep.tile([P, 4, HALF], BF16, name="raw_%s%d%d" % (name, a, h))
+            half = keep.tile([P, 4, HALF], BF16, name="raw_%s%d%d" % (name, a, h))
+            raw[name, a, h] = half[:]
             nc.sync.dma_start(
-                out=raw[name, a, h][:],
+                out=half[:],
                 in_=weight[HALF * a : HALF * (a + 1), HALF * h : HALF * (h + 1)].rearrange("(p j) c -> p j c", j=4),
             )
-
-        def load_w_whole(name, a):
-            weight = Wo if name == "wo" else Wv
-            whole = keep.tile([P, 4, 2 * HALF], BF16, name="raw_%s%d" % (name, a))
-            nc.sync.dma_start(out=whole[:], in_=weight[HALF * a : HALF * (a + 1), :].rearrange("(p j) c -> p j c", j=4))
-            for h in range(2):
-                raw[name, a, h] = whole[:, :, HALF * h : HALF * (h + 1)]
 
         def load_x(i):
             whole = keep.tile([P, 4, 2 * HALF], BF16, name="raw_x%d" % i)
@@ -116,6 +110,29 @@ def tile_multiheadattention_pb_v_kernel(tc, values, logw, Wv, Wo, pool_w, grad_o
                     dst[:, n * part : n * (part + 1), :].rearrange("p (c i) t -> p c t i", i=4),
                     src.rearrange("p t (c i) -> p c t i", i=4),
                 )
+
+        def side_weave(k, i, h, part, parts):
+            n = HALF // parts
+            staged["side", i, h, part] = work.tile([P, n, 4], BF16, name="swap%d" % (k % TURNED), align_bytes=64)
+            nc.gpsimd.tensor_scalar(
+                out=staged["side", i, h, part][:],
+                in0=raw["x", i, h][:, :, n * part : n * (part + 1)].rearrange("p t c -> p c t"),
+                scalar1=1.0,
+                scalar2=0.0,
+                op0=MULT,
+                op1=mybir.AluOpType.add,
+            )
+
+        def quant_side(i, h, part, parts):
+            n = HALF // parts
+            if part == 0:
+                codes["x", i, h] = keep.tile([P, HALF], U32, name="q_x%d%d" % (i, h), align_bytes=64)
+                scales["x", i, h] = keep.tile([P, HALF], U8, name="s_x%d%d" % (i, h), align_bytes=64)
+            nc.vector.quantize_mx(
+                out=codes["x", i, h][:, n * part : n * (part + 1)].bitcast(E4),
+                scales=scales["x", i, h][:, n * part : n * (part + 1)],
+                in_=staged["side", i, h, part][:].rearrange("p c t -> p (c t)"),
+            )
 
         def quant_staged(name, a, h):
             quantise((name, a, h), staged[name, a, h][:].rearrange("p c t -> p (c t)"), E5 if name == "d" else E4)
@@ -173,7 +190,7 @@ def tile_multiheadattention_pb_v_kernel(tc, values, logw, Wv, Wo, pool_w, grad_o
 
         def copy_turned(engine, k, g):
             if ("t", k) not in staged:
-                staged["t", k] = work.tile([P, 2 * HALF], F32, name="turned", bufs=TURNED, align_bytes=64)
+                staged["t", k] = work.tile([P, 2 * HALF], F32, name="swap%d" % (k % TURNED), align_bytes=64)
             copy_on(
                 engine,
                 staged["t", k][:, HALF * g : HALF * (g + 1)].rearrange("p (e b u) -> p e b u", e=2, u=2),
@@ -203,7 +220,7 @@ def tile_multiheadattention_pb_v_kernel(tc, values, logw, Wv, Wo, pool_w, grad_o
             dst = stage(("d", g, q))[:].rearrange("p (i j) s -> p i j s", i=4)[:, n * part : n * (part + 1)]
             copy_on(engine, dst.rearrange("p i (c l) s -> p i c s l", l=4), src.rearrange("p i s (c l) -> p i c s l", l=4))
 
-        def pass1(g, q, h, i, n):
+        def pass1(g, q, h, i, n, last=3):
             if i == 0:
                 banks["o1", g, q, h] = bank(n, [P, HALF])
             nc.tensor.matmul_mx(
@@ -213,7 +230,7 @@ def tile_multiheadattention_pb_v_kernel(tc, values, logw, Wv, Wo, pool_w, grad_o
                 rhs=codes["x", i, h][:].bitcast(E4),
                 rhs_scale=scales["x", i, h][:],
                 start=(i == 0),
-                stop=(i == 3),
+                stop=(i == last),
             )
 
         def product1(g, q, h, n):
@@ -253,8 +270,8 @@ def tile_multiheadattention_pb_v_kernel(tc, values, logw, Wv, Wo, pool_w, grad_o
             load_pw(2, nc.sync)
             load_x(1)
             load_pw(3, nc.sync)
-            load_x(2)
             load_x(3)
+            load_x(2)
             turn_go(0, 7)
             weave("V", "wo", 0, 0, 0, 2)
             weave("S", "wo", 0, 0, 1, 2)
@@ -300,22 +317,27 @@ def tile_multiheadattention_pb_v_kernel(tc, values, logw, Wv, Wo, pool_w, grad_o
             copy_turned("S", 1, 0)
             copy_turned("S", 1, 1)
             weave("V", "wv", 1, 1)
-            quant_turned(1)
-            quant_staged("wv", 0, 1)
-            quant_staged("wv", 1, 1)
             empty("S", "o0", 0, 0, 0)
             empty("S", "o0", 0, 1, 0)
             copy_go("S", 2)
+            quant_staged("wv", 0, 1)
+            quant_staged("wv", 1, 1)
+            quant_turned(1)
+            side_weave(1, 0, 0, 0, 1)
             weigh(2, 0)
             weigh(2, 1)
             acc = 3
-            for k, e, h in ((1, 0, 0), (1, 1, 0), (0, 0, 1), (0, 1, 1)):
-                product0(k, e, h, 4 + acc % 4)
+            for e in range(2):
+                product0(0, e, 1, 4 + acc % 4)
                 acc = acc + 1
-                empty("S", "o0", k, e, h)
-                if h == 1:
-                    store("o0", k, e)
+                empty("S", "o0", 0, e, 1)
+                store("o0", 0, e)
             for k in range(1, 8):
+                if k == 1:
+                    for e in range(2):
+                        product0(k, e, 0, 4 + acc % 4)
+                        acc = acc + 1
+                        empty("S", "o0", k, e, 0)
                 if k < 7:
                     turn(k + 1, 0, 2)
                     turn(k + 1, 1, 3)
@@ -330,33 +352,41 @@ def tile_multiheadattention_pb_v_kernel(tc, values, logw, Wv, Wo, pool_w, grad_o
                     copy_turned("S", k + 1, 1)
                 if k == 1:
                     copy_go("S", 3)
-                    quant_go(2)
                 if k == 2:
+                    weave("S", "x", 3, 0, 0, 2)
                     quant_go(3)
-                    weave("V", "x", 0, 0)
-                    weave("S", "x", 1, 0, 0, 2)
+                    quant_side(0, 0, 0, 1)
+                    quant_turned(2)
+                    side_weave(2, 1, 0, 0, 2)
                 if k == 4:
-                    weave("V", "x", 2, 0)
+                    weave("V", "x", 3, 0, 1, 2)
+                    quant_turned(4)
+                    side_weave(4, 2, 0, 0, 2)
                 if k < 6:
                     weigh(k + 2, 0)
                     weigh(k + 2, 1)
-                if k == 5:
-                    weave("V", "x", 1, 0, 1, 2)
-                    quant_staged("x", 0, 0)
-                if k < 7:
+                if k == 1:
+                    quant_go(2)
+                if k in (2, 4):
+                    quant_side(k // 2, 0, 0, 2)
                     quant_turned(k + 1)
+                    side_weave(k + 1, k // 2, 0, 1, 2)
+                if k in (3, 5):
+                    quant_side(k // 2, 0, 1, 2)
                 if k == 5:
-                    weave("V", "x", 3, 0)
-                    quant_staged("x", 1, 0)
-                    quant_staged("x", 2, 0)
-                if k == 6:
-                    weave_d("V", 0, 0)
                     quant_staged("x", 3, 0)
+                    quant_turned(6)
+                    weave_d("V", 0, 0)
+                if k == 6:
+                    quant_turned(7)
                     quant_staged("d", 0, 0)
                     weave_d("V", 0, 1)
-                if k == 7:
-                    quant_staged("d", 0, 1)
                     weave_d("V", 0, 2)
+                    quant_staged("d", 0, 1)
+                if k == 7:
+                    weave_d("V", 0, 3)
+                    quant_staged("d", 0, 2)
+                    quant_staged("d", 0, 3)
                 for e, h in ((0, 0), (1, 0), (0, 1), (1, 1)):
                     if k > 1 or h == 1:
                         product0(k, e, h, 4 + acc % 4)
@@ -365,25 +395,23 @@ def tile_multiheadattention_pb_v_kernel(tc, values, logw, Wv, Wo, pool_w, grad_o
                         if h == 1:
                             store("o0", k, e)
             weave("S", "x", 0, 1)
-            quant_staged("d", 0, 2)
-            weave_d("V", 0, 3)
+            weave("V", "x", 3, 1)
             weave("S", "x", 1, 1)
-            quant_staged("d", 0, 3)
+            quant_staged("x", 0, 1)
+            weave_d("V", 1, 0)
+            weave("S", "x", 2, 1)
             for q in range(4):
                 product1(0, q, 0, q)
-            quant_staged("x", 0, 1)
-            weave("S", "x", 2, 1)
-            weave("V", "x", 3, 1)
             quant_staged("x", 1, 1)
-            weave_d("V", 1, 0)
+            quant_staged("d", 1, 0)
+            quant_staged("x", 3, 1)
+            quant_staged("x", 2, 1)
             for q in range(4):
                 empty("S", "o1", 0, q, 0)
-            quant_staged("x", 2, 1)
-            quant_staged("x", 3, 1)
-            quant_staged("d", 1, 0)
-            for i in range(4):
+                store("o1", 0, q, 0, 1)
+            for i in (0, 1, 3, 2):
                 for q in range(4):
-                    pass1(0, q, 1, i, 4 + q)
+                    pass1(0, q, 1, i, 4 + q, 2)
             weave_d("V", 1, 1)
             weave_d("S", 1, 2, 0, 2)
             quant_staged("d", 1, 1)
@@ -393,7 +421,7 @@ def tile_multiheadattention_pb_v_kernel(tc, values, logw, Wv, Wo, pool_w, grad_o
             quant_staged("d", 1, 3)
             for q in range(4):
                 empty("S", "o1", 0, q, 1)
-                store("o1", 0, q)
+                store("o1", 0, q, 1, 2)
             for q in range(4):
                 for h in range(2):
                     product1(1, q, h, 2 * q + h)

@@ -31,9 +31,7 @@ def tile_multiheadattention_pb_v_kernel(tc, values, logw, Wv, Wo, pool_w, grad_o
         ident = keep.tile([P, P], F32, name="ident")
         make_identity(nc, ident[:])
         pw = [keep.tile([P, 4, 16], F32, name="pw%d" % i) for i in range(4)]
-        go_raw = [keep.tile([P, 1024], BF16, name="go_raw%d" % i) for i in range(4)]
-        goq = [keep.tile([P, 2 * P], U32, name="goq%d" % i, align_bytes=64) for i in range(4)]
-        gos = [keep.tile([P, 2 * P], U8, name="gos%d" % i, align_bytes=64) for i in range(4)]
+        go_raw = {}
         dvp = [keep.tile([P, 4 * 4 * HALF], BF16, name="dvp%d" % g, align_bytes=64) for g in range(2)]
         raw = {}
         codes = {}
@@ -61,16 +59,22 @@ def tile_multiheadattention_pb_v_kernel(tc, values, logw, Wv, Wo, pool_w, grad_o
         def bank(n, shape):
             return psum.tile(shape, F32, name="bank%d" % n)
 
-        def stage(key):
+        def stage(key, slot=None):
             if key not in staged:
-                staged[key] = work.tile([P, HALF, 4], BF16, name="stage", bufs=STAGES, align_bytes=64)
+                if slot is None:
+                    staged[key] = work.tile([P, HALF, 4], BF16, name="stage", bufs=STAGES, align_bytes=64)
+                else:
+                    staged[key] = work.tile([P, HALF, 4], BF16, name=slot, align_bytes=64)
             return staged[key]
 
         def load_pw(i, queue):
             queue.dma_start(out=pw[i][:], in_=pool_w[:, P * i : P * (i + 1), :].rearrange("s p h -> p s h"))
 
-        def load_go(i):
-            nc.sync.dma_start(out=go_raw[i][:], in_=grad_out[P * i : P * (i + 1), :])
+        def load_go(first, n):
+            both = keep.tile([P, n, 1024], BF16, name="go_raw%d" % first)
+            nc.sync.dma_start(out=both[:], in_=grad_out[P * first : P * (first + n), :].rearrange("(i p) o -> p i o", p=P))
+            for i in range(n):
+                go_raw[first + i] = both[:, i, :]
 
         def load_w(name, a, h):
             weight = Wo if name == "wo" else Wv
@@ -111,27 +115,28 @@ def tile_multiheadattention_pb_v_kernel(tc, values, logw, Wv, Wo, pool_w, grad_o
                     src.rearrange("p t (c i) -> p c t i", i=4),
                 )
 
-        def side_weave(k, i, h, part, parts):
+        def side_weave(slot, name, a, h, part, parts=2):
             n = HALF // parts
-            staged["side", i, h, part] = work.tile([P, n, 4], BF16, name="swap%d" % (k % TURNED), align_bytes=64)
-            nc.gpsimd.tensor_scalar(
-                out=staged["side", i, h, part][:],
-                in0=raw["x", i, h][:, :, n * part : n * (part + 1)].rearrange("p t c -> p c t"),
-                scalar1=1.0,
-                scalar2=0.0,
-                op0=MULT,
-                op1=mybir.AluOpType.add,
-            )
+            staged["side", name, a, h, part] = work.tile([P, n, 4], BF16, name=slot, align_bytes=64)
+            src = raw[name, a, h][:, :, n * part : n * (part + 1)]
+            dst = staged["side", name, a, h, part][:]
+            if name == "wv":
+                src = src.rearrange("p (e u) c -> p c u e", u=2)
+                dst = dst.rearrange("p c (u e) -> p c u e", u=2)
+            else:
+                src = src.rearrange("p t c -> p c t")
+            nc.gpsimd.tensor_scalar(out=dst, in0=src, scalar1=1.0, scalar2=0.0, op0=MULT, op1=mybir.AluOpType.add)
 
-        def quant_side(i, h, part, parts):
+        def quant_half(name, a, h, part, side, parts=2):
             n = HALF // parts
-            if part == 0:
-                codes["x", i, h] = keep.tile([P, HALF], U32, name="q_x%d%d" % (i, h), align_bytes=64)
-                scales["x", i, h] = keep.tile([P, HALF], U8, name="s_x%d%d" % (i, h), align_bytes=64)
+            if (name, a, h) not in codes:
+                codes[name, a, h] = keep.tile([P, HALF], U32, name="q_%s%d%d" % (name, a, h), align_bytes=64)
+                scales[name, a, h] = keep.tile([P, HALF], U8, name="s_%s%d%d" % (name, a, h), align_bytes=64)
+            src = staged["side", name, a, h, part][:] if side else staged[name, a, h][:, n * part : n * (part + 1), :]
             nc.vector.quantize_mx(
-                out=codes["x", i, h][:, n * part : n * (part + 1)].bitcast(E4),
-                scales=scales["x", i, h][:, n * part : n * (part + 1)],
-                in_=staged["side", i, h, part][:].rearrange("p c t -> p (c t)"),
+                out=codes[name, a, h][:, n * part : n * (part + 1)].bitcast(E4),
+                scales=scales[name, a, h][:, n * part : n * (part + 1)],
+                in_=src.rearrange("p c t -> p (c t)"),
             )
 
         def quant_staged(name, a, h):
@@ -139,13 +144,13 @@ def tile_multiheadattention_pb_v_kernel(tc, values, logw, Wv, Wo, pool_w, grad_o
 
         def turn_go(i, n):
             banks["go", i] = bank(n, [P, 4, P])
-            words = go_raw[i][:].bitcast(F32)
+            words = go_raw[i].bitcast(F32)
             for a in range(2):
                 for u in range(2):
                     nc.tensor.transpose(banks["go", i][:, 2 * a + u, :], words[:, 256 * a + u : 256 * a + 256 : 2], ident[:])
 
         def copy_go(engine, i):
-            staged["go", i] = work.tile([P, 2 * P * 2], F32, name="go_t", bufs=2, align_bytes=64)
+            staged["go", i] = work.tile([P, HALF], F32, name="go_turned", bufs=2, align_bytes=64)
             copy_on(
                 engine,
                 staged["go", i][:].rearrange("p (a b u) -> p a b u", a=2, u=2),
@@ -153,15 +158,16 @@ def tile_multiheadattention_pb_v_kernel(tc, values, logw, Wv, Wo, pool_w, grad_o
             )
 
         def quant_go(i):
-            nc.vector.quantize_mx(out=goq[i][:].bitcast(E5), scales=gos[i][:], in_=staged["go", i][:].bitcast(BF16))
+            quantise(("go", i, 0), staged["go", i][:].bitcast(BF16), E5)
 
         def dattn(i, g, n):
             banks["da", i, g] = bank(n, [P, HALF])
             for a in range(2):
+                m = slice(P * a, P * (a + 1))
                 nc.tensor.matmul_mx(
                     out=banks["da", i, g][:],
-                    lhsT=goq[i][:, P * a : P * (a + 1)].bitcast(E5),
-                    lhsT_scale=gos[i][:, P * a : P * (a + 1)],
+                    lhsT=codes["go", i, 0][:, m].bitcast(E5),
+                    lhsT_scale=scales["go", i, 0][:, m],
                     rhs=codes["wo", a, g][:].bitcast(E4),
                     rhs_scale=scales["wo", a, g][:],
                     start=(a == 0),
@@ -176,8 +182,8 @@ def tile_multiheadattention_pb_v_kernel(tc, values, logw, Wv, Wo, pool_w, grad_o
             for s in (2 * (k % 2), 2 * (k % 2) + 1):
                 nc.vector.tensor_tensor(
                     out=plane(i, g, s).rearrange("p (u h j) -> p u h j", u=2, h=8),
-                    in0=banks["da", i, g][:].rearrange("p (u h j) -> p u h j", u=2, h=8),
-                    in1=pw[i][:, s, 8 * g : 8 * g + 8].unsqueeze(1).unsqueeze(3).to_broadcast([P, 2, 8, 32]),
+                    in1=banks["da", i, g][:].rearrange("p (u h j) -> p u h j", u=2, h=8),
+                    in0=pw[i][:, s, 8 * g : 8 * g + 8].unsqueeze(1).unsqueeze(3).to_broadcast([P, 2, 8, 32]),
                     op=MULT,
                 )
 
@@ -253,25 +259,24 @@ def tile_multiheadattention_pb_v_kernel(tc, values, logw, Wv, Wo, pool_w, grad_o
 
         with tc.manual_schedule():
             load_w("wo", 0, 0)
-            load_go(0)
+            load_go(0, 1)
             load_w("wo", 1, 0)
             load_w("wo", 0, 1)
             load_w("wo", 1, 1)
             load_pw(0, nc.sync)
             load_w("wv", 0, 0)
             load_w("wv", 1, 0)
-            load_go(1)
+            load_go(1, 1)
             load_w("wv", 0, 1)
             load_w("wv", 1, 1)
             load_pw(1, nc.sync)
-            load_go(2)
+            load_go(2, 2)
             load_x(0)
-            load_go(3)
-            load_pw(2, nc.sync)
             load_x(1)
+            load_pw(2, nc.sync)
             load_pw(3, nc.sync)
-            load_x(3)
             load_x(2)
+            load_x(3)
             turn_go(0, 7)
             weave("V", "wo", 0, 0, 0, 2)
             weave("S", "wo", 0, 0, 1, 2)
@@ -284,24 +289,28 @@ def tile_multiheadattention_pb_v_kernel(tc, values, logw, Wv, Wo, pool_w, grad_o
             weave("S", "wo", 0, 1, 1, 2)
             quant_staged("wo", 1, 0)
             dattn(0, 0, 0)
+            stage(("wo", 1, 1), "swap2")
             weave("V", "wo", 1, 1, 0, 2)
             weave("S", "wo", 1, 1, 1, 2)
             quant_staged("wo", 0, 1)
-            weave("S", "wv", 0, 0)
             quant_staged("wo", 1, 1)
             dattn(0, 1, 1)
+            side_weave("swap2", "wv", 0, 0, 0)
+            weave("S", "wv", 0, 0, 1, 2)
             weigh(0, 0)
             weigh(0, 1)
             turn(0, 0, 2)
             turn(0, 1, 3)
             turn_go(1, 7)
+            weave("S", "wv", 1, 0, 1, 2)
             weave("V", "wv", 1, 0, 0, 2)
             copy_turned("S", 0, 0)
-            weave("S", "wv", 1, 0, 1, 2)
             copy_turned("S", 0, 1)
-            quant_staged("wv", 0, 0)
+            quant_half("wv", 0, 0, 0, True)
+            quant_half("wv", 0, 0, 1, False)
             quant_staged("wv", 1, 0)
             quant_turned(0)
+            side_weave("swap0", "wv", 1, 1, 0)
             copy_go("S", 1)
             weave("S", "wv", 0, 1)
             weigh(1, 0)
@@ -314,110 +323,92 @@ def tile_multiheadattention_pb_v_kernel(tc, values, logw, Wv, Wo, pool_w, grad_o
             dattn(1, 0, 0)
             dattn(1, 1, 1)
             turn_go(2, 6)
+            turn_go(3, 7)
+            weave("V", "wv", 1, 1, 1, 2)
+            quant_staged("wv", 0, 1)
+            quant_half("wv", 1, 1, 0, True)
+            quant_half("wv", 1, 1, 1, False)
             copy_turned("S", 1, 0)
             copy_turned("S", 1, 1)
-            weave("V", "wv", 1, 1)
             empty("S", "o0", 0, 0, 0)
             empty("S", "o0", 0, 1, 0)
-            copy_go("S", 2)
-            quant_staged("wv", 0, 1)
-            quant_staged("wv", 1, 1)
             quant_turned(1)
-            side_weave(1, 0, 0, 0, 1)
+            copy_go("S", 2)
+            copy_go("S", 3)
+            side_weave("swap1", "x", 0, 0, 0, 1)
             weigh(2, 0)
             weigh(2, 1)
-            acc = 3
-            for e in range(2):
-                product0(0, e, 1, 4 + acc % 4)
-                acc = acc + 1
-                empty("S", "o0", 0, e, 1)
-                store("o0", 0, e)
-            for k in range(1, 8):
-                if k == 1:
-                    for e in range(2):
-                        product0(k, e, 0, 4 + acc % 4)
-                        acc = acc + 1
-                        empty("S", "o0", k, e, 0)
-                if k < 7:
+            weigh(3, 0)
+            weigh(3, 1)
+            quant_go(2)
+            acc = 0
+            for k in range(8):
+                if 1 <= k < 7:
                     turn(k + 1, 0, 2)
                     turn(k + 1, 1, 3)
-                if k == 1:
-                    turn_go(3, 4 + acc % 4)
-                    acc = acc + 1
                 if k in (2, 4):
                     dattn(k // 2 + 1, 0, 0)
                     dattn(k // 2 + 1, 1, 1)
-                if k < 7:
+                if 1 <= k < 7:
                     copy_turned("S", k + 1, 0)
                     copy_turned("S", k + 1, 1)
-                if k == 1:
-                    copy_go("S", 3)
                 if k == 2:
-                    weave("S", "x", 3, 0, 0, 2)
                     quant_go(3)
-                    quant_side(0, 0, 0, 1)
-                    quant_turned(2)
-                    side_weave(2, 1, 0, 0, 2)
+                    quant_half("x", 0, 0, 0, True, 1)
+                if 3 <= k < 7:
+                    quant_half("x", (k - 1) // 2, 0, (k - 1) % 2, True)
                 if k == 4:
-                    weave("V", "x", 3, 0, 1, 2)
-                    quant_turned(4)
-                    side_weave(4, 2, 0, 0, 2)
-                if k < 6:
+                    quant_staged("x", 3, 0)
+                if 2 <= k < 7:
+                    quant_turned(k)
+                if 2 <= k < 6:
+                    side_weave("swap%d" % (k % 3), "x", k // 2, 0, k % 2)
                     weigh(k + 2, 0)
                     weigh(k + 2, 1)
-                if k == 1:
-                    quant_go(2)
-                if k in (2, 4):
-                    quant_side(k // 2, 0, 0, 2)
-                    quant_turned(k + 1)
-                    side_weave(k + 1, k // 2, 0, 1, 2)
-                if k in (3, 5):
-                    quant_side(k // 2, 0, 1, 2)
-                if k == 5:
-                    quant_staged("x", 3, 0)
-                    quant_turned(6)
-                    weave_d("V", 0, 0)
+                if k in (2, 3):
+                    weave("S", "x", 3, 0, k % 2, 2)
+                if k in (4, 5):
+                    weave("S", "x", 0, 1, k % 2, 2)
                 if k == 6:
+                    weave_d("V", 0, 0)
                     quant_turned(7)
                     quant_staged("d", 0, 0)
                     weave_d("V", 0, 1)
+                if k == 7:
                     weave_d("V", 0, 2)
                     quant_staged("d", 0, 1)
-                if k == 7:
-                    weave_d("V", 0, 3)
-                    quant_staged("d", 0, 2)
-                    quant_staged("d", 0, 3)
                 for e, h in ((0, 0), (1, 0), (0, 1), (1, 1)):
-                    if k > 1 or h == 1:
+                    if k > 0 or h == 1:
                         product0(k, e, h, 4 + acc % 4)
                         acc = acc + 1
-                        empty("S", "o0", k, e, h)
+                        empty("V" if (e, h) == (0, 0) and 2 <= k < 6 else "S", "o0", k, e, h)
                         if h == 1:
                             store("o0", k, e)
-            weave("S", "x", 0, 1)
-            weave("V", "x", 3, 1)
-            weave("S", "x", 1, 1)
+            weave_d("S", 0, 3, 1, 2)
+            weave_d("V", 0, 3, 0, 2)
+            quant_staged("d", 0, 2)
             quant_staged("x", 0, 1)
-            weave_d("V", 1, 0)
-            weave("S", "x", 2, 1)
-            for q in range(4):
-                product1(0, q, 0, q)
+            quant_staged("d", 0, 3)
+            weave("S", "x", 1, 1)
+            weave("V", "x", 2, 1)
+            weave("S", "x", 3, 1)
             quant_staged("x", 1, 1)
+            weave_d("V", 1, 0)
+            quant_staged("x", 2, 1)
             quant_staged("d", 1, 0)
             quant_staged("x", 3, 1)
-            quant_staged("x", 2, 1)
+            for q in range(4):
+                product1(0, q, 0, q)
             for q in range(4):
                 empty("S", "o1", 0, q, 0)
                 store("o1", 0, q, 0, 1)
-            for i in (0, 1, 3, 2):
+            for i in range(4):
                 for q in range(4):
-                    pass1(0, q, 1, i, 4 + q, 2)
-            weave_d("V", 1, 1)
-            weave_d("S", 1, 2, 0, 2)
-            quant_staged("d", 1, 1)
-            weave_d("V", 1, 2, 1, 2)
-            weave_d("V", 1, 3)
-            quant_staged("d", 1, 2)
+                    pass1(0, q, 1, i, 4 + q)
+            for q in range(1, 4):
+                weave_d("V", 1, q)
+                if q > 1:
+                    quant_staged("d", 1, q - 1)
             quant_staged("d", 1, 3)
             for q in range(4):
                 empty("S", "o1", 0, q, 1)

@@ -85,18 +85,26 @@ def tile_multiheadattention_pb_v_kernel(tc, values, logw, Wv, Wo, pool_w, grad_o
                 in_=weight[HALF * a : HALF * (a + 1), HALF * h : HALF * (h + 1)].rearrange("(p j) c -> p j c", j=4),
             )
 
-        def load_x(i):
-            whole = keep.tile([P, 4, 2 * HALF], BF16, name="raw_x%d" % i)
-            nc.sync.dma_start(out=whole[:], in_=values[:, P * i : P * (i + 1), :].rearrange("s p d -> p s d"))
+        def load_w_whole(name, a):
+            weight = Wo if name == "wo" else Wv
+            whole = keep.tile([P, 4, 2 * HALF], BF16, name="raw_%s%d" % (name, a))
+            nc.sync.dma_start(out=whole[:], in_=weight[HALF * a : HALF * (a + 1), :].rearrange("(p j) c -> p j c", j=4))
             for h in range(2):
-                raw["x", i, h] = whole[:, :, HALF * h : HALF * (h + 1)]
+                raw[name, a, h] = whole[:, :, HALF * h : HALF * (h + 1)]
 
-        def weave(engine, name, a, h, part=0, parts=1):
-            n = HALF // parts
-            src = raw[name, a, h][:, :, n * part : n * (part + 1)]
+        def load_x_half(i, h):
+            half = keep.tile([P, 4, HALF], BF16, name="raw_x%d%d" % (i, h))
+            raw["x", i, h] = half[:]
+            nc.sync.dma_start(
+                out=half[:], in_=values[:, P * i : P * (i + 1), HALF * h : HALF * (h + 1)].rearrange("s p d -> p s d")
+            )
+
+        def weave(engine, name, a, h, part=0, parts=1, count=1):
+            lo, hi = HALF // parts * part, HALF // parts * (part + count)
+            src = raw[name, a, h][:, :, lo:hi]
             dst = stage((name, a, h))
             if name == "wo":
-                dst = dst[:].rearrange("p (u r) t -> p u r t", u=2)[:, :, n // 2 * part : n // 2 * (part + 1), :]
+                dst = dst[:].rearrange("p (u r) t -> p u r t", u=2)[:, :, lo // 2 : hi // 2, :]
                 copy_on(
                     engine,
                     dst.rearrange("p u (r l) t -> p r t l u", l=2),
@@ -105,13 +113,13 @@ def tile_multiheadattention_pb_v_kernel(tc, values, logw, Wv, Wo, pool_w, grad_o
             elif name == "wv":
                 copy_on(
                     engine,
-                    dst[:, n * part : n * (part + 1), :].rearrange("p (c i) (u e) -> p c u e i", i=4, u=2),
+                    dst[:, lo:hi, :].rearrange("p (c i) (u e) -> p c u e i", i=4, u=2),
                     src.rearrange("p (e u) (c i) -> p c u e i", i=4, u=2),
                 )
             else:
                 copy_on(
                     engine,
-                    dst[:, n * part : n * (part + 1), :].rearrange("p (c i) t -> p c t i", i=4),
+                    dst[:, lo:hi, :].rearrange("p (c i) t -> p c t i", i=4),
                     src.rearrange("p t (c i) -> p c t i", i=4),
                 )
 
@@ -239,6 +247,25 @@ def tile_multiheadattention_pb_v_kernel(tc, values, logw, Wv, Wo, pool_w, grad_o
                 stop=(i == last),
             )
 
+        def last_product1(engine, g, q, quarter, n):
+            acc = bank(n, [P, HALF // 2])
+            h, cols = quarter // 2, slice(256 * (quarter % 2), 256 * (quarter % 2 + 1))
+            for i in range(4):
+                nc.tensor.matmul_mx(
+                    out=acc[:],
+                    lhsT=codes["d", g, q][:, P * i : P * (i + 1)].bitcast(E5),
+                    lhsT_scale=scales["d", g, q][:, P * i : P * (i + 1)],
+                    rhs=codes["x", i, h][:, cols].bitcast(E4),
+                    rhs_scale=scales["x", i, h][:, cols],
+                    start=(i == 0),
+                    stop=(i == 3),
+                )
+            part = work.tile([P, HALF // 2], F32, name="last%d" % quarter)
+            copy_on(engine, part[:], acc[:])
+            first = HALF * g + 256 * (q % 2)
+            dst = out_1[first : first + 256, 256 * quarter : 256 * (quarter + 1)]
+            nc.sync.dma_start(out=dst.rearrange("(r u) d -> u r d", u=2)[q // 2], in_=part[:])
+
         def product1(g, q, h, n):
             for i in range(4):
                 pass1(g, q, h, i, n)
@@ -258,59 +285,56 @@ def tile_multiheadattention_pb_v_kernel(tc, values, logw, Wv, Wo, pool_w, grad_o
             nc.sync.dma_start(out=dst, in_=rows[name, a, b][:, cols])
 
         with tc.manual_schedule():
-            load_w("wo", 0, 0)
+            load_w_whole("wo", 0)
             load_go(0, 1)
             load_w("wo", 1, 0)
-            load_w("wo", 0, 1)
             load_w("wo", 1, 1)
-            load_pw(0, nc.sync)
             load_w("wv", 0, 0)
+            load_pw(0, nc.sync)
             load_w("wv", 1, 0)
             load_go(1, 1)
             load_w("wv", 0, 1)
             load_w("wv", 1, 1)
             load_pw(1, nc.sync)
             load_go(2, 2)
-            load_x(0)
-            load_x(1)
+            load_x_half(0, 0)
+            load_x_half(1, 0)
             load_pw(2, nc.sync)
-            load_pw(3, nc.sync)
-            load_x(2)
-            load_x(3)
+            load_x_half(2, 0)
             turn_go(0, 7)
-            weave("V", "wo", 0, 0, 0, 2)
-            weave("S", "wo", 0, 0, 1, 2)
-            copy_go("S", 0)
+            weave("V", "wo", 0, 0, 0, 8, 5)
+            weave("S", "wo", 0, 0, 5, 8, 3)
+            weave("V", "wo", 0, 1, 0, 8, 3)
+            weave("S", "wo", 0, 1, 3, 8, 5)
             quant_staged("wo", 0, 0)
-            weave("V", "wo", 1, 0, 0, 2)
-            weave("S", "wo", 1, 0, 1, 2)
+            copy_go("S", 0)
+            weave("V", "wo", 1, 0, 0, 8, 5)
+            weave("S", "wo", 1, 0, 5, 8, 3)
             quant_go(0)
-            weave("V", "wo", 0, 1, 0, 2)
-            weave("S", "wo", 0, 1, 1, 2)
             quant_staged("wo", 1, 0)
             dattn(0, 0, 0)
-            stage(("wo", 1, 1), "swap2")
-            weave("V", "wo", 1, 1, 0, 2)
-            weave("S", "wo", 1, 1, 1, 2)
+            stage(("wo", 1, 1), "side")
+            weave("V", "wo", 1, 1, 0, 8, 3)
+            weave("S", "wo", 1, 1, 3, 8, 5)
             quant_staged("wo", 0, 1)
             quant_staged("wo", 1, 1)
             dattn(0, 1, 1)
-            side_weave("swap2", "wv", 0, 0, 0)
+            side_weave("side", "wv", 0, 0, 0)
             weave("S", "wv", 0, 0, 1, 2)
             weigh(0, 0)
             weigh(0, 1)
             turn(0, 0, 2)
             turn(0, 1, 3)
             turn_go(1, 7)
-            weave("S", "wv", 1, 0, 1, 2)
-            weave("V", "wv", 1, 0, 0, 2)
+            weave("S", "wv", 1, 0, 3, 8, 5)
+            weave("V", "wv", 1, 0, 0, 8, 3)
             copy_turned("S", 0, 0)
             copy_turned("S", 0, 1)
-            quant_half("wv", 0, 0, 0, True)
             quant_half("wv", 0, 0, 1, False)
             quant_staged("wv", 1, 0)
+            quant_half("wv", 0, 0, 0, True)
             quant_turned(0)
-            side_weave("swap0", "wv", 1, 1, 0)
+            side_weave("side", "wv", 1, 1, 0)
             copy_go("S", 1)
             weave("S", "wv", 0, 1)
             weigh(1, 0)
@@ -326,8 +350,8 @@ def tile_multiheadattention_pb_v_kernel(tc, values, logw, Wv, Wo, pool_w, grad_o
             turn_go(3, 7)
             weave("V", "wv", 1, 1, 1, 2)
             quant_staged("wv", 0, 1)
-            quant_half("wv", 1, 1, 0, True)
             quant_half("wv", 1, 1, 1, False)
+            quant_half("wv", 1, 1, 0, True)
             copy_turned("S", 1, 0)
             copy_turned("S", 1, 1)
             empty("S", "o0", 0, 0, 0)
@@ -335,7 +359,7 @@ def tile_multiheadattention_pb_v_kernel(tc, values, logw, Wv, Wo, pool_w, grad_o
             quant_turned(1)
             copy_go("S", 2)
             copy_go("S", 3)
-            side_weave("swap1", "x", 0, 0, 0, 1)
+            side_weave("side", "x", 0, 0, 0, 1)
             weigh(2, 0)
             weigh(2, 1)
             weigh(3, 0)
@@ -343,32 +367,41 @@ def tile_multiheadattention_pb_v_kernel(tc, values, logw, Wv, Wo, pool_w, grad_o
             quant_go(2)
             acc = 0
             for k in range(8):
-                if 1 <= k < 7:
-                    turn(k + 1, 0, 2)
-                    turn(k + 1, 1, 3)
+                if k == 1:
+                    load_x_half(3, 0)
+                    load_pw(3, nc.sync)
+                if 2 <= k < 6:
+                    load_x_half(k - 2, 1)
                 if k in (2, 4):
                     dattn(k // 2 + 1, 0, 0)
                     dattn(k // 2 + 1, 1, 1)
+                if 1 <= k < 7:
+                    turn(k + 1, 0, 2)
+                    turn(k + 1, 1, 3)
+                if k == 2:
+                    weave("S", "x", 1, 0, 0, 2)
+                if k == 4:
+                    weave("S", "x", 0, 1, 0, 2)
                 if 1 <= k < 7:
                     copy_turned("S", k + 1, 0)
                     copy_turned("S", k + 1, 1)
                 if k == 2:
                     quant_go(3)
                     quant_half("x", 0, 0, 0, True, 1)
-                if 3 <= k < 7:
-                    quant_half("x", (k - 1) // 2, 0, (k - 1) % 2, True)
                 if k == 4:
-                    quant_staged("x", 3, 0)
+                    quant_staged("x", 1, 0)
+                if 3 <= k < 7:
+                    quant_half("x", (k + 1) // 2, 0, (k - 1) % 2, True)
                 if 2 <= k < 7:
                     quant_turned(k)
                 if 2 <= k < 6:
-                    side_weave("swap%d" % (k % 3), "x", k // 2, 0, k % 2)
+                    side_weave("side", "x", k // 2 + 1, 0, k % 2)
                     weigh(k + 2, 0)
                     weigh(k + 2, 1)
-                if k in (2, 3):
-                    weave("S", "x", 3, 0, k % 2, 2)
-                if k in (4, 5):
-                    weave("S", "x", 0, 1, k % 2, 2)
+                if k == 3:
+                    weave("S", "x", 1, 0, 1, 2)
+                if k == 5:
+                    weave("S", "x", 0, 1, 1, 2)
                 if k == 6:
                     weave_d("V", 0, 0)
                     quant_turned(7)
@@ -413,11 +446,13 @@ def tile_multiheadattention_pb_v_kernel(tc, values, logw, Wv, Wo, pool_w, grad_o
             for q in range(4):
                 empty("S", "o1", 0, q, 1)
                 store("o1", 0, q, 1, 2)
-            for q in range(4):
+            for q in range(3):
                 for h in range(2):
                     product1(1, q, h, 2 * q + h)
-                    empty("V" if h == 0 and q > 1 else "S", "o1", 1, q, h)
-                    if q == 3:
-                        store("o1", 1, q, h, h + 1)
-                if q < 3:
-                    store("o1", 1, q)
+                    empty("S", "o1", 1, q, h)
+                store("o1", 1, q)
+            product1(1, 3, 0, 6)
+            empty("V", "o1", 1, 3, 0)
+            store("o1", 1, 3, 0, 1)
+            last_product1("S", 1, 3, 2, 7)
+            last_product1("V", 1, 3, 3, 0)

@@ -17,7 +17,7 @@ P = 128
 HALF = 512
 STAGES = 6
 TURNED = 3
-ROWS = 6
+ROWS = 7
 CODES = 6
 
 
@@ -313,13 +313,13 @@ def tile_multiheadattention_pb_v_kernel(tc, values, logw, Wv, Wo, pool_w, grad_o
             quant_go(0)
             quant_staged("wo", 1, 0)
             dattn(0, 0, 0)
-            stage(("wo", 1, 1), "side")
+            stage(("wo", 1, 1), "swap2")
             weave("V", "wo", 1, 1, 0, 8, 3)
             weave("S", "wo", 1, 1, 3, 8, 5)
             quant_staged("wo", 0, 1)
             quant_staged("wo", 1, 1)
             dattn(0, 1, 1)
-            side_weave("side", "wv", 0, 0, 0)
+            side_weave("swap2", "wv", 0, 0, 0)
             weave("S", "wv", 0, 0, 1, 2)
             weigh(0, 0)
             weigh(0, 1)
@@ -334,9 +334,10 @@ def tile_multiheadattention_pb_v_kernel(tc, values, logw, Wv, Wo, pool_w, grad_o
             quant_staged("wv", 1, 0)
             quant_half("wv", 0, 0, 0, True)
             quant_turned(0)
-            side_weave("side", "wv", 1, 1, 0)
+            side_weave("swap0", "wv", 0, 1, 0)
             copy_go("S", 1)
-            weave("S", "wv", 0, 1)
+            weave("S", "wv", 0, 1, 1, 2)
+            weave("S", "wv", 1, 1, 1, 2)
             weigh(1, 0)
             weigh(1, 1)
             quant_go(1)
@@ -348,10 +349,10 @@ def tile_multiheadattention_pb_v_kernel(tc, values, logw, Wv, Wo, pool_w, grad_o
             dattn(1, 1, 1)
             turn_go(2, 6)
             turn_go(3, 7)
-            weave("V", "wv", 1, 1, 1, 2)
-            quant_staged("wv", 0, 1)
-            quant_half("wv", 1, 1, 1, False)
-            quant_half("wv", 1, 1, 0, True)
+            weave("V", "wv", 1, 1, 0, 2)
+            quant_half("wv", 0, 1, 0, True)
+            quant_half("wv", 0, 1, 1, False)
+            quant_staged("wv", 1, 1)
             copy_turned("S", 1, 0)
             copy_turned("S", 1, 1)
             empty("S", "o0", 0, 0, 0)
@@ -359,7 +360,7 @@ def tile_multiheadattention_pb_v_kernel(tc, values, logw, Wv, Wo, pool_w, grad_o
             quant_turned(1)
             copy_go("S", 2)
             copy_go("S", 3)
-            side_weave("side", "x", 0, 0, 0, 1)
+            side_weave("swap1", "x", 0, 0, 0, 1)
             weigh(2, 0)
             weigh(2, 1)
             weigh(3, 0)
@@ -395,7 +396,7 @@ def tile_multiheadattention_pb_v_kernel(tc, values, logw, Wv, Wo, pool_w, grad_o
                 if 2 <= k < 7:
                     quant_turned(k)
                 if 2 <= k < 6:
-                    side_weave("side", "x", k // 2 + 1, 0, k % 2)
+                    side_weave("swap%d" % (k % 3), "x", k // 2 + 1, 0, k % 2)
                     weigh(k + 2, 0)
                     weigh(k + 2, 1)
                 if k == 3:
@@ -450,7 +451,7 @@ def tile_multiheadattention_pb_v_kernel(tc, values, logw, Wv, Wo, pool_w, grad_o
                 for h in range(2):
                     product1(1, q, h, 2 * q + h)
                     empty("S", "o1", 1, q, h)
-                store("o1", 1, q)
+                    store("o1", 1, q, h, h + 1)
             product1(1, 3, 0, 6)
             empty("V", "o1", 1, 3, 0)
             store("o1", 1, 3, 0, 1)

@@ -19,6 +19,7 @@ STAGES = 6
 TURNED = 3
 ROWS = 7
 CODES = 6
+RUN = {"V": 4, "S": 2}
 
 
 def tile_multiheadattention_pb_v_kernel(tc, values, logw, Wv, Wo, pool_w, grad_out, out_0, out_1):
@@ -103,24 +104,26 @@ def tile_multiheadattention_pb_v_kernel(tc, values, logw, Wv, Wo, pool_w, grad_o
             lo, hi = HALF // parts * part, HALF // parts * (part + count)
             src = raw[name, a, h][:, :, lo:hi]
             dst = stage((name, a, h))
+            run = RUN[engine]
             if name == "wo":
                 dst = dst[:].rearrange("p (u r) t -> p u r t", u=2)[:, :, lo // 2 : hi // 2, :]
+                walk = "p r t l u" if run == 4 else "p r u t l"
                 copy_on(
                     engine,
-                    dst.rearrange("p u (r l) t -> p r t l u", l=2),
-                    src.rearrange("p t (r l u) -> p r t l u", l=2, u=2),
+                    dst.rearrange("p u (r l) t -> " + walk, l=2),
+                    src.rearrange("p t (r l u) -> " + walk, l=2, u=2),
                 )
             elif name == "wv":
                 copy_on(
                     engine,
-                    dst[:, lo:hi, :].rearrange("p (c i) (u e) -> p c u e i", i=4, u=2),
-                    src.rearrange("p (e u) (c i) -> p c u e i", i=4, u=2),
+                    dst[:, lo:hi, :].rearrange("p (c i) (u e) -> p c u e i", i=run, u=2),
+                    src.rearrange("p (e u) (c i) -> p c u e i", i=run, u=2),
                 )
             else:
                 copy_on(
                     engine,
-                    dst[:, lo:hi, :].rearrange("p (c i) t -> p c t i", i=4),
-                    src.rearrange("p t (c i) -> p c t i", i=4),
+                    dst[:, lo:hi, :].rearrange("p (c i) t -> p c t i", i=run),
+                    src.rearrange("p t (c i) -> p c t i", i=run),
                 )
 
         def side_weave(slot, name, a, h, part, parts=2):
@@ -232,7 +235,8 @@ def tile_multiheadattention_pb_v_kernel(tc, values, logw, Wv, Wo, pool_w, grad_o
             n = 4 // parts
             src = dvp[g][:].rearrange("p (i s j) -> p i s j", i=4, s=4)[:, n * part : n * (part + 1), :, P * q : P * (q + 1)]
             dst = stage(("d", g, q))[:].rearrange("p (i j) s -> p i j s", i=4)[:, n * part : n * (part + 1)]
-            copy_on(engine, dst.rearrange("p i (c l) s -> p i c s l", l=4), src.rearrange("p i s (c l) -> p i c s l", l=4))
+            run = RUN[engine]
+            copy_on(engine, dst.rearrange("p i (c l) s -> p i c s l", l=run), src.rearrange("p i s (c l) -> p i c s l", l=run))
 
         def pass1(g, q, h, i, n, last=3):
             if i == 0:

@@ -15,7 +15,7 @@ E5 = mybir.dt.float8_e5m2_x4
 MULT = mybir.AluOpType.mult
 P = 128
 HALF = 512
-STAGES = 6
+STAGES = 5
 TURNED = 3
 ROWS = 7
 CODES = 6
@@ -33,7 +33,8 @@ def tile_multiheadattention_pb_v_kernel(tc, values, logw, Wv, Wo, pool_w, grad_o
         make_identity(nc, ident[:])
         pw = [keep.tile([P, 4, 16], F32, name="pw%d" % i) for i in range(4)]
         go_raw = {}
-        dvp = [keep.tile([P, 4 * 4 * HALF], BF16, name="dvp%d" % g, align_bytes=64) for g in range(2)]
+        woven = [keep.tile([P, 4 * HALF], BF16, name="woven%d" % q, align_bytes=64) for q in range(4)]
+        planes = keep.tile([P, 4 * 4 * HALF], BF16, name="planes", align_bytes=64)
         raw = {}
         codes = {}
         scales = {}
@@ -126,11 +127,10 @@ def tile_multiheadattention_pb_v_kernel(tc, values, logw, Wv, Wo, pool_w, grad_o
                     src.rearrange("p t (c i) -> p c t i", i=run),
                 )
 
-        def side_weave(slot, name, a, h, part, parts=2):
-            n = HALF // parts
-            staged["side", name, a, h, part] = work.tile([P, n, 4], BF16, name=slot, align_bytes=64)
-            src = raw[name, a, h][:, :, n * part : n * (part + 1)]
-            dst = staged["side", name, a, h, part][:]
+        def side_weave(slot, name, a, h, lo, hi):
+            staged["side", name, a, h, lo] = work.tile([P, hi - lo, 4], BF16, name=slot, align_bytes=64)
+            src = raw[name, a, h][:, :, lo:hi]
+            dst = staged["side", name, a, h, lo][:]
             if name == "wv":
                 src = src.rearrange("p (e u) c -> p c u e", u=2)
                 dst = dst.rearrange("p c (u e) -> p c u e", u=2)
@@ -138,15 +138,15 @@ def tile_multiheadattention_pb_v_kernel(tc, values, logw, Wv, Wo, pool_w, grad_o
                 src = src.rearrange("p t c -> p c t")
             nc.gpsimd.tensor_scalar(out=dst, in0=src, scalar1=1.0, scalar2=0.0, op0=MULT, op1=mybir.AluOpType.add)
 
-        def quant_half(name, a, h, part, side, parts=2):
-            n = HALF // parts
+        def quant_part(name, a, h, lo, hi):
             if (name, a, h) not in codes:
                 codes[name, a, h] = keep.tile([P, HALF], U32, name="q_%s%d%d" % (name, a, h), align_bytes=64)
                 scales[name, a, h] = keep.tile([P, HALF], U8, name="s_%s%d%d" % (name, a, h), align_bytes=64)
-            src = staged["side", name, a, h, part][:] if side else staged[name, a, h][:, n * part : n * (part + 1), :]
+            side = ("side", name, a, h, lo)
+            src = staged[side][:] if side in staged else staged[name, a, h][:, lo:hi, :]
             nc.vector.quantize_mx(
-                out=codes[name, a, h][:, n * part : n * (part + 1)].bitcast(E4),
-                scales=scales[name, a, h][:, n * part : n * (part + 1)],
+                out=codes[name, a, h][:, lo:hi].bitcast(E4),
+                scales=scales[name, a, h][:, lo:hi],
                 in_=src.rearrange("p c t -> p (c t)"),
             )
 
@@ -164,8 +164,8 @@ def tile_multiheadattention_pb_v_kernel(tc, values, logw, Wv, Wo, pool_w, grad_o
             staged["go", i] = work.tile([P, HALF], F32, name="go_turned", bufs=2, align_bytes=64)
             copy_on(
                 engine,
-                staged["go", i][:].rearrange("p (a b u) -> p a b u", a=2, u=2),
-                banks["go", i][:].rearrange("p (a u) b -> p a b u", u=2),
+                staged["go", i][:].rearrange("p (a b l u) -> p a b u l", a=2, u=2, l=2),
+                banks["go", i][:].rearrange("p (a u) (b l) -> p a b u l", u=2, l=2),
             )
 
         def quant_go(i):
@@ -185,34 +185,59 @@ def tile_multiheadattention_pb_v_kernel(tc, values, logw, Wv, Wo, pool_w, grad_o
                     stop=(a == 1),
                 )
 
-        def plane(i, g, s):
-            return dvp[g][:, HALF * (4 * i + s) : HALF * (4 * i + s + 1)]
+        def plane(i, s):
+            return planes[:, HALF * (4 * i + s) : HALF * (4 * i + s + 1)]
 
-        def weigh(k, g):
+        def weigh_woven(i, u):
+            for e in range(2):
+                column = banks["da", i, 0][:, 256 * u + e : 256 * (u + 1) : 2]
+                nc.vector.tensor_tensor(
+                    out=woven[2 * u + e][:, HALF * i : HALF * (i + 1)].rearrange("p (h j s) -> p h j s", h=8, s=4),
+                    in0=pw[i][:, :, 0:8].rearrange("p s h -> p h s").unsqueeze(2).to_broadcast([P, 8, 16, 4]),
+                    in1=column.rearrange("p (h j) -> p h j", h=8).unsqueeze(3).to_broadcast([P, 8, 16, 4]),
+                    op=MULT,
+                )
+
+        def weigh_planes(k):
             i = k // 2
             for s in (2 * (k % 2), 2 * (k % 2) + 1):
                 nc.vector.tensor_tensor(
-                    out=plane(i, g, s).rearrange("p (u h j) -> p u h j", u=2, h=8),
-                    in1=banks["da", i, g][:].rearrange("p (u h j) -> p u h j", u=2, h=8),
-                    in0=pw[i][:, s, 8 * g : 8 * g + 8].unsqueeze(1).unsqueeze(3).to_broadcast([P, 2, 8, 32]),
+                    out=plane(i, s).rearrange("p (u h j) -> p u h j", u=2, h=8),
+                    in0=pw[i][:, s, 8:16].unsqueeze(1).unsqueeze(3).to_broadcast([P, 2, 8, 32]),
+                    in1=banks["da", i, 1][:].rearrange("p (u h j) -> p u h j", u=2, h=8),
                     op=MULT,
                 )
 
         def turn(k, g, n):
             banks["t", k, g] = bank(n, [P, 4, P])
-            for e in range(2):
-                words = plane(k // 2, g, 2 * (k % 2) + e).bitcast(F32)
-                for u in range(2):
-                    nc.tensor.transpose(banks["t", k, g][:, 2 * e + u, :], words[:, P * u : P * (u + 1)], ident[:])
+            i, pair = divmod(k, 2)
+            for q in range(4):
+                if g == 0:
+                    words = woven[q][:].bitcast(F32)[:, 256 * i + pair : 256 * (i + 1) : 2]
+                else:
+                    words = plane(i, 2 * pair + q // 2).bitcast(F32)[:, P * (q % 2) : P * (q % 2 + 1)]
+                nc.tensor.transpose(banks["t", k, g][:, q, :], words, ident[:])
 
         def copy_turned(engine, k, g):
             if ("t", k) not in staged:
                 staged["t", k] = work.tile([P, 2 * HALF], F32, name="swap%d" % (k % TURNED), align_bytes=64)
-            copy_on(
-                engine,
-                staged["t", k][:, HALF * g : HALF * (g + 1)].rearrange("p (e b u) -> p e b u", e=2, u=2),
-                banks["t", k, g][:].rearrange("p (e u) b -> p e b u", u=2),
-            )
+            dst = staged["t", k][:, HALF * g : HALF * (g + 1)]
+            src = banks["t", k, g][:]
+            if g == 0:
+                copy_on(
+                    engine,
+                    dst.bitcast(BF16).rearrange("p (e b q) -> p e b q", e=2, q=4),
+                    src.rearrange("p q b -> p (q b)").bitcast(BF16).rearrange("p (q b e) -> p e b q", q=4, e=2),
+                )
+            else:
+                copy_on(
+                    engine,
+                    dst.rearrange("p (e b u) -> p e b u", e=2, u=2),
+                    src.rearrange("p (e u) b -> p e b u", u=2),
+                )
+
+        def quant_woven(q):
+            quantise(("d", 0, q), woven[q][:], E5)
 
         def quant_turned(k):
             quantise(("t", k, 0), staged["t", k][:].bitcast(BF16), E5)
@@ -233,7 +258,7 @@ def tile_multiheadattention_pb_v_kernel(tc, values, logw, Wv, Wo, pool_w, grad_o
 
         def weave_d(engine, g, q, part=0, parts=1):
             n = 4 // parts
-            src = dvp[g][:].rearrange("p (i s j) -> p i s j", i=4, s=4)[:, n * part : n * (part + 1), :, P * q : P * (q + 1)]
+            src = planes[:].rearrange("p (i s j) -> p i s j", i=4, s=4)[:, n * part : n * (part + 1), :, P * q : P * (q + 1)]
             dst = stage(("d", g, q))[:].rearrange("p (i j) s -> p i j s", i=4)[:, n * part : n * (part + 1)]
             run = RUN[engine]
             copy_on(engine, dst.rearrange("p i (c l) s -> p i c s l", l=run), src.rearrange("p i s (c l) -> p i c s l", l=run))
@@ -283,6 +308,8 @@ def tile_multiheadattention_pb_v_kernel(tc, values, logw, Wv, Wo, pool_w, grad_o
             cols = slice(HALF * lo, HALF * hi)
             if name == "o0":
                 dst = out_0[2 * (a % 2) + b, P * (a // 2) : P * (a // 2 + 1), cols]
+            elif a == 0:
+                dst = out_1[0:HALF, cols].rearrange("(m t) d -> t m d", t=4)[2 * (b % 2) + b // 2]
             else:
                 first = HALF * a + 256 * (b % 2)
                 dst = out_1[first : first + 256, cols].rearrange("(r u) d -> u r d", u=2)[b // 2]
@@ -323,52 +350,51 @@ def tile_multiheadattention_pb_v_kernel(tc, values, logw, Wv, Wo, pool_w, grad_o
             quant_staged("wo", 0, 1)
             quant_staged("wo", 1, 1)
             dattn(0, 1, 1)
-            side_weave("swap2", "wv", 0, 0, 0)
-            weave("S", "wv", 0, 0, 1, 2)
-            weigh(0, 0)
-            weigh(0, 1)
+            side_weave("swap2", "wv", 0, 0, 0, 384)
+            weave("S", "wv", 0, 0, 3, 4)
+            weigh_woven(0, 0)
+            weigh_woven(0, 1)
+            weigh_planes(0)
+            turn_go(1, 7)
             turn(0, 0, 2)
             turn(0, 1, 3)
-            turn_go(1, 7)
-            weave("S", "wv", 1, 0, 3, 8, 5)
-            weave("V", "wv", 1, 0, 0, 8, 3)
+            weave("S", "wv", 1, 0, 1, 4, 3)
+            copy_go("S", 1)
+            weave("V", "wv", 1, 0, 0, 4)
             copy_turned("S", 0, 0)
             copy_turned("S", 0, 1)
-            quant_half("wv", 0, 0, 1, False)
-            quant_staged("wv", 1, 0)
-            quant_half("wv", 0, 0, 0, True)
-            quant_turned(0)
-            side_weave("swap0", "wv", 0, 1, 0)
-            copy_go("S", 1)
-            weave("S", "wv", 0, 1, 1, 2)
-            weave("S", "wv", 1, 1, 1, 2)
-            weigh(1, 0)
-            weigh(1, 1)
             quant_go(1)
+            dattn(1, 0, 0)
+            quant_part("wv", 0, 0, 384, 512)
+            quant_staged("wv", 1, 0)
+            quant_part("wv", 0, 0, 0, 384)
+            quant_turned(0)
+            side_weave("swap0", "wv", 0, 1, 256 * (0), 256 * (0) + 256)
+            weave("S", "wv", 0, 1, 1, 2)
+            weave("S", "wv", 1, 1, 3, 8, 5)
+            turn(1, 0, 2)
+            weigh_planes(1)
+            weigh_woven(1, 0)
+            copy_turned("S", 1, 0)
             product0(0, 0, 0, 4)
             product0(0, 1, 0, 5)
-            turn(1, 0, 2)
             turn(1, 1, 3)
-            dattn(1, 0, 0)
-            dattn(1, 1, 1)
             turn_go(2, 6)
             turn_go(3, 7)
-            weave("V", "wv", 1, 1, 0, 2)
-            quant_half("wv", 0, 1, 0, True)
-            quant_half("wv", 0, 1, 1, False)
-            quant_staged("wv", 1, 1)
-            copy_turned("S", 1, 0)
+            dattn(1, 1, 1)
+            weave("V", "wv", 1, 1, 0, 8, 3)
             copy_turned("S", 1, 1)
+            quant_part("wv", 0, 1, 256 * (0), 256 * (0) + 256)
+            quant_part("wv", 0, 1, 256 * (1), 256 * (1) + 256)
+            quant_staged("wv", 1, 1)
             empty("S", "o0", 0, 0, 0)
             empty("S", "o0", 0, 1, 0)
-            quant_turned(1)
             copy_go("S", 2)
+            quant_turned(1)
             copy_go("S", 3)
-            side_weave("swap1", "x", 0, 0, 0, 1)
-            weigh(2, 0)
-            weigh(2, 1)
-            weigh(3, 0)
-            weigh(3, 1)
+            side_weave("swap1", "x", 0, 0, 256 * (0), 256 * (0) + 256)
+            weigh_woven(1, 1)
+            weigh_planes(2)
             quant_go(2)
             acc = 0
             for k in range(8):
@@ -377,64 +403,59 @@ def tile_multiheadattention_pb_v_kernel(tc, values, logw, Wv, Wo, pool_w, grad_o
                     load_pw(3, nc.sync)
                 if 2 <= k < 6:
                     load_x_half(k - 2, 1)
-                if k in (2, 4):
-                    dattn(k // 2 + 1, 0, 0)
-                    dattn(k // 2 + 1, 1, 1)
+                if k == 1:
+                    for e in range(2):
+                        product0(k, e, 0, 4 + acc % 4)
+                        acc = acc + 1
+                        empty("S", "o0", k, e, 0)
                 if 1 <= k < 7:
                     turn(k + 1, 0, 2)
                     turn(k + 1, 1, 3)
-                if k == 2:
-                    weave("S", "x", 1, 0, 0, 2)
-                if k == 4:
-                    weave("S", "x", 0, 1, 0, 2)
+                if 1 <= k < 5:
+                    dattn((k + 3) // 2, (k + 1) % 2, (k + 1) % 2)
                 if 1 <= k < 7:
                     copy_turned("S", k + 1, 0)
                     copy_turned("S", k + 1, 1)
                 if k == 2:
                     quant_go(3)
-                    quant_half("x", 0, 0, 0, True, 1)
-                if k == 4:
-                    quant_staged("x", 1, 0)
-                if 3 <= k < 7:
-                    quant_half("x", (k + 1) // 2, 0, (k - 1) % 2, True)
+                if 1 <= k < 7:
+                    quant_part("x", (k - 1) // 2, 0, 256 * ((k - 1) % 2), 256 * ((k - 1) % 2) + 256)
                 if 2 <= k < 7:
                     quant_turned(k)
-                if 2 <= k < 6:
-                    side_weave("swap%d" % (k % 3), "x", k // 2 + 1, 0, k % 2)
-                    weigh(k + 2, 0)
-                    weigh(k + 2, 1)
-                if k == 3:
-                    weave("S", "x", 1, 0, 1, 2)
-                if k == 5:
-                    weave("S", "x", 0, 1, 1, 2)
+                if 1 <= k < 6:
+                    side_weave("swap%d" % (k % 3), "x", k // 2, 0, 256 * (k % 2), 256 * (k % 2) + 256)
+                    if k % 2 == 1:
+                        weigh_planes(k + 2)
+                        if k < 5:
+                            weigh_woven((k + 3) // 2, 0)
+                    else:
+                        weigh_woven((k + 2) // 2, 1)
+                        weigh_planes(k + 2)
                 if k == 6:
-                    weave_d("V", 0, 0)
+                    weave("V", "x", 3, 0)
                     quant_turned(7)
-                    quant_staged("d", 0, 0)
-                    weave_d("V", 0, 1)
+                    quant_staged("x", 3, 0)
+                    quant_woven(0)
+                    weave("V", "x", 0, 1)
                 if k == 7:
-                    weave_d("V", 0, 2)
-                    quant_staged("d", 0, 1)
+                    for q in range(1, 4):
+                        quant_woven(q)
+                    weave("V", "x", 1, 1)
+                    quant_staged("x", 0, 1)
                 for e, h in ((0, 0), (1, 0), (0, 1), (1, 1)):
-                    if k > 0 or h == 1:
+                    if k > 1 or h == 1:
                         product0(k, e, h, 4 + acc % 4)
                         acc = acc + 1
-                        empty("V" if (e, h) == (0, 0) and 2 <= k < 6 else "S", "o0", k, e, h)
+                        empty("V" if (e, h) == (0, 0) and k in (2, 3, 5) or (k, e, h) == (5, 1, 0) else "S", "o0", k, e, h)
                         if h == 1:
                             store("o0", k, e)
-            weave_d("S", 0, 3, 1, 2)
-            weave_d("V", 0, 3, 0, 2)
-            quant_staged("d", 0, 2)
-            quant_staged("x", 0, 1)
-            quant_staged("d", 0, 3)
-            weave("S", "x", 1, 1)
-            weave("V", "x", 2, 1)
+            weave("S", "x", 2, 1)
             weave("S", "x", 3, 1)
             quant_staged("x", 1, 1)
-            weave_d("V", 1, 0)
             quant_staged("x", 2, 1)
-            quant_staged("d", 1, 0)
+            weave_d("V", 1, 0)
             quant_staged("x", 3, 1)
+            quant_staged("d", 1, 0)
             for q in range(4):
                 product1(0, q, 0, q)
             for q in range(4):

@@ -31,7 +31,10 @@ def tile_multiheadattention_pb_v_kernel(tc, values, logw, Wv, Wo, pool_w, grad_o
 
         ident = keep.tile([P, P], F32, name="ident")
         make_identity(nc, ident[:])
-        pw = [keep.tile([P, 4, 16], F32, name="pw%d" % i) for i in range(4)]
+        pw_all = keep.tile([P, 4, 4, 16], F32, name="pw_all")
+        by_head_all = keep.tile([P, 4, 8, 4], F32, name="by_head_all")
+        pw = [pw_all[:, i] for i in range(4)]
+        by_head = [by_head_all[:, i] for i in range(4)]
         go_raw = {}
         woven = [keep.tile([P, 4 * HALF], BF16, name="woven%d" % q, align_bytes=64) for q in range(4)]
         planes = keep.tile([P, 4 * 4 * HALF], BF16, name="planes", align_bytes=64)
@@ -70,7 +73,10 @@ def tile_multiheadattention_pb_v_kernel(tc, values, logw, Wv, Wo, pool_w, grad_o
             return staged[key]
 
         def load_pw(i, queue):
-            queue.dma_start(out=pw[i][:], in_=pool_w[:, P * i : P * (i + 1), :].rearrange("s p h -> p s h"))
+            queue.dma_start(out=pw[i], in_=pool_w[:, P * i : P * (i + 1), :].rearrange("s p h -> p s h"))
+
+        def sort_pw(lo, hi):
+            nc.scalar.copy(out=by_head_all[:, lo:hi], in_=pw_all[:, lo:hi, :, 0:8].rearrange("p i s h -> p i h s"))
 
         def load_go(first, n):
             both = keep.tile([P, n, 1024], BF16, name="go_raw%d" % first)
@@ -193,7 +199,7 @@ def tile_multiheadattention_pb_v_kernel(tc, values, logw, Wv, Wo, pool_w, grad_o
                 column = banks["da", i, 0][:, 256 * u + e : 256 * (u + 1) : 2]
                 nc.vector.tensor_tensor(
                     out=woven[2 * u + e][:, HALF * i : HALF * (i + 1)].rearrange("p (h j s) -> p h j s", h=8, s=4),
-                    in0=pw[i][:, :, 0:8].rearrange("p s h -> p h s").unsqueeze(2).to_broadcast([P, 8, 16, 4]),
+                    in0=by_head[i].unsqueeze(2).to_broadcast([P, 8, 16, 4]),
                     in1=column.rearrange("p (h j) -> p h j", h=8).unsqueeze(3).to_broadcast([P, 8, 16, 4]),
                     op=MULT,
                 )
@@ -328,9 +334,10 @@ def tile_multiheadattention_pb_v_kernel(tc, values, logw, Wv, Wo, pool_w, grad_o
             load_w("wv", 1, 1)
             load_pw(1, nc.sync)
             load_go(2, 2)
+            load_pw(2, nc.sync)
+            load_pw(3, nc.sync)
             load_x_half(0, 0)
             load_x_half(1, 0)
-            load_pw(2, nc.sync)
             load_x_half(2, 0)
             turn_go(0, 7)
             weave("V", "wo", 0, 0, 0, 8, 5)
@@ -351,6 +358,7 @@ def tile_multiheadattention_pb_v_kernel(tc, values, logw, Wv, Wo, pool_w, grad_o
             quant_staged("wo", 1, 1)
             dattn(0, 1, 1)
             side_weave("swap2", "wv", 0, 0, 0, 384)
+            sort_pw(0, 1)
             weave("S", "wv", 0, 0, 3, 4)
             weigh_woven(0, 0)
             weigh_woven(0, 1)
@@ -371,6 +379,7 @@ def tile_multiheadattention_pb_v_kernel(tc, values, logw, Wv, Wo, pool_w, grad_o
             quant_turned(0)
             side_weave("swap0", "wv", 0, 1, 256 * (0), 256 * (0) + 256)
             weave("S", "wv", 0, 1, 1, 2)
+            sort_pw(1, 2)
             weave("S", "wv", 1, 1, 3, 8, 5)
             turn(1, 0, 2)
             weigh_planes(1)
@@ -392,6 +401,7 @@ def tile_multiheadattention_pb_v_kernel(tc, values, logw, Wv, Wo, pool_w, grad_o
             copy_go("S", 2)
             quant_turned(1)
             copy_go("S", 3)
+            sort_pw(2, 4)
             side_weave("swap1", "x", 0, 0, 256 * (0), 256 * (0) + 256)
             weigh_woven(1, 1)
             weigh_planes(2)
@@ -400,7 +410,6 @@ def tile_multiheadattention_pb_v_kernel(tc, values, logw, Wv, Wo, pool_w, grad_o
             for k in range(8):
                 if k == 1:
                     load_x_half(3, 0)
-                    load_pw(3, nc.sync)
                 if 2 <= k < 6:
                     load_x_half(k - 2, 1)
                 if k == 1:

@@ -13,17 +13,31 @@ U8 = mybir.dt.uint8
 E4 = mybir.dt.float8_e4m3fn_x4
 E5 = mybir.dt.float8_e5m2_x4
 MULT = mybir.AluOpType.mult
+ADD = mybir.AluOpType.add
+
 P = 128
 HALF = 512
-STAGES = 5
-TURNED = 3
-ROWS = 7
-CODES = 6
-RUN = {"V": 4, "S": 2}
+QUARTER = 256
+STEPS = 8
+RUN = 2
+
+WEAVE_BUFS = 5
+SWAP_BUFS = 3
+ROW_BUFS = 7
+DVP_CODE_BUFS = 6
+
+LARGE, SMALL = 320, 192
+FIRST_WINDOW = 384
+BEFORE_FIRST_TURN = 128
+
+DATTN_BANKS = (0, 1)
+TURN_BANKS = (2, 3)
+SUM_BANKS = (4, 5, 6, 7)
 
 
 def tile_multiheadattention_pb_v_kernel(tc, values, logw, Wv, Wo, pool_w, grad_out, out_0, out_1):
     nc = tc.nc
+    vector, scalar = nc.vector.tensor_copy, nc.scalar.copy
     with ExitStack() as ctx:
         keep = ctx.enter_context(tc.tile_pool(name="keep", bufs=1))
         work = ctx.enter_context(tc.tile_pool(name="work", bufs=1))
@@ -31,463 +45,444 @@ def tile_multiheadattention_pb_v_kernel(tc, values, logw, Wv, Wo, pool_w, grad_o
 
         ident = keep.tile([P, P], F32, name="ident")
         make_identity(nc, ident[:])
-        pw_all = keep.tile([P, 4, 4, 16], F32, name="pw_all")
-        by_head_all = keep.tile([P, 4, 8, 4], F32, name="by_head_all")
-        pw = [pw_all[:, i] for i in range(4)]
-        by_head = [by_head_all[:, i] for i in range(4)]
-        go_raw = {}
+        pw = keep.tile([P, 4, 4, 16], F32, name="pw")
+        pw_by_head = keep.tile([P, 4, 8, 4], F32, name="pw_by_head")
         woven = [keep.tile([P, 4 * HALF], BF16, name="woven%d" % q, align_bytes=64) for q in range(4)]
         planes = keep.tile([P, 4 * 4 * HALF], BF16, name="planes", align_bytes=64)
         raw = {}
+        staged = {}
         codes = {}
         scales = {}
-        staged = {}
         banks = {}
         rows = {}
-
-        def copy_on(engine, out, in_):
-            if engine == "V":
-                nc.vector.tensor_copy(out=out, in_=in_)
-            else:
-                nc.scalar.copy(out=out, in_=in_)
-
-        def quantise(key, src, fmt):
-            width = src.shape[1] // 4
-            if key[0] in ("t", "d"):
-                codes[key] = work.tile([P, width], U32, name="q_dvp", bufs=CODES, align_bytes=64)
-                scales[key] = work.tile([P, width], U8, name="s_dvp", bufs=CODES, align_bytes=64)
-            else:
-                codes[key] = keep.tile([P, width], U32, name="q_%s%d%d" % key, align_bytes=64)
-                scales[key] = keep.tile([P, width], U8, name="s_%s%d%d" % key, align_bytes=64)
-            nc.vector.quantize_mx(out=codes[key][:].bitcast(fmt), scales=scales[key][:], in_=src)
 
         def bank(n, shape):
             return psum.tile(shape, F32, name="bank%d" % n)
 
-        def stage(key, slot=None):
+        def swap(n, shape, dtype):
+            return work.tile(shape, dtype, name="swap%d" % (n % SWAP_BUFS), align_bytes=64)
+
+        def stage(key):
             if key not in staged:
-                if slot is None:
-                    staged[key] = work.tile([P, HALF, 4], BF16, name="stage", bufs=STAGES, align_bytes=64)
-                else:
-                    staged[key] = work.tile([P, HALF, 4], BF16, name=slot, align_bytes=64)
+                staged[key] = work.tile([P, HALF, 4], BF16, name="stage", bufs=WEAVE_BUFS, align_bytes=64)
             return staged[key]
 
-        def load_pw(i, queue):
-            queue.dma_start(out=pw[i], in_=pool_w[:, P * i : P * (i + 1), :].rearrange("s p h -> p s h"))
 
-        def sort_pw(lo, hi):
-            nc.scalar.copy(out=by_head_all[:, lo:hi], in_=pw_all[:, lo:hi, :, 0:8].rearrange("p i s h -> p i h s"))
+        def load_pw(i):
+            nc.sync.dma_start(out=pw[:, i], in_=pool_w[:, P * i : P * (i + 1), :].rearrange("s p h -> p s h"))
 
         def load_go(first, n):
-            both = keep.tile([P, n, 1024], BF16, name="go_raw%d" % first)
-            nc.sync.dma_start(out=both[:], in_=grad_out[P * first : P * (first + n), :].rearrange("(i p) o -> p i o", p=P))
+            tiles = keep.tile([P, n, 2 * HALF], BF16, name="go_raw%d" % first)
+            src = grad_out[P * first : P * (first + n), :]
+            nc.sync.dma_start(out=tiles[:], in_=src.rearrange("(i p) o -> p i o", p=P))
             for i in range(n):
-                go_raw[first + i] = both[:, i, :]
+                raw["go", first + i] = tiles[:, i, :]
 
-        def load_w(name, a, h):
-            weight = Wo if name == "wo" else Wv
-            half = keep.tile([P, 4, HALF], BF16, name="raw_%s%d%d" % (name, a, h))
-            raw[name, a, h] = half[:]
-            nc.sync.dma_start(
-                out=half[:],
-                in_=weight[HALF * a : HALF * (a + 1), HALF * h : HALF * (h + 1)].rearrange("(p j) c -> p j c", j=4),
-            )
+        def load_weight(name, a, h):
+            tile = keep.tile([P, 4, HALF], BF16, name="raw_%s%d%d" % (name, a, h))
+            src = {"wo": Wo, "wv": Wv}[name][HALF * a : HALF * (a + 1), HALF * h : HALF * (h + 1)]
+            nc.sync.dma_start(out=tile[:], in_=src.rearrange("(p j) c -> p j c", j=4))
+            raw[name, a, h] = tile[:]
 
-        def load_w_whole(name, a):
-            weight = Wo if name == "wo" else Wv
-            whole = keep.tile([P, 4, 2 * HALF], BF16, name="raw_%s%d" % (name, a))
-            nc.sync.dma_start(out=whole[:], in_=weight[HALF * a : HALF * (a + 1), :].rearrange("(p j) c -> p j c", j=4))
+        def load_first_rows_of_wo():
+            tile = keep.tile([P, 4, 2 * HALF], BF16, name="raw_wo0")
+            nc.sync.dma_start(out=tile[:], in_=Wo[0:HALF, :].rearrange("(p j) c -> p j c", j=4))
             for h in range(2):
-                raw[name, a, h] = whole[:, :, HALF * h : HALF * (h + 1)]
+                raw["wo", 0, h] = tile[:, :, HALF * h : HALF * (h + 1)]
 
-        def load_x_half(i, h):
-            half = keep.tile([P, 4, HALF], BF16, name="raw_x%d%d" % (i, h))
-            raw["x", i, h] = half[:]
-            nc.sync.dma_start(
-                out=half[:], in_=values[:, P * i : P * (i + 1), HALF * h : HALF * (h + 1)].rearrange("s p d -> p s d")
-            )
+        def load_values(i, h):
+            tile = keep.tile([P, 4, HALF], BF16, name="raw_x%d%d" % (i, h))
+            src = values[:, P * i : P * (i + 1), HALF * h : HALF * (h + 1)]
+            nc.sync.dma_start(out=tile[:], in_=src.rearrange("s p d -> p s d"))
+            raw["x", i, h] = tile[:]
 
-        def weave(engine, name, a, h, part=0, parts=1, count=1):
-            lo, hi = HALF // parts * part, HALF // parts * (part + count)
+
+        def sort_pw(lo, hi):
+            scalar(out=pw_by_head[:, lo:hi], in_=pw[:, lo:hi, :, 0:8].rearrange("p i s h -> p i h s"))
+
+        def weave(copy, name, a, h, lo=0, hi=HALF):
             src = raw[name, a, h][:, :, lo:hi]
             dst = stage((name, a, h))
-            run = RUN[engine]
             if name == "wo":
                 dst = dst[:].rearrange("p (u r) t -> p u r t", u=2)[:, :, lo // 2 : hi // 2, :]
-                walk = "p r t l u" if run == 4 else "p r u t l"
-                copy_on(
-                    engine,
-                    dst.rearrange("p u (r l) t -> " + walk, l=2),
-                    src.rearrange("p t (r l u) -> " + walk, l=2, u=2),
+                copy(
+                    out=dst.rearrange("p u (r l) t -> p r u t l", l=RUN),
+                    in_=src.rearrange("p t (r l u) -> p r u t l", l=RUN, u=2),
                 )
             elif name == "wv":
-                copy_on(
-                    engine,
-                    dst[:, lo:hi, :].rearrange("p (c i) (u e) -> p c u e i", i=run, u=2),
-                    src.rearrange("p (e u) (c i) -> p c u e i", i=run, u=2),
+                copy(
+                    out=dst[:, lo:hi, :].rearrange("p (c l) (u e) -> p c u e l", l=RUN, u=2),
+                    in_=src.rearrange("p (e u) (c l) -> p c u e l", l=RUN, u=2),
                 )
             else:
-                copy_on(
-                    engine,
-                    dst[:, lo:hi, :].rearrange("p (c i) t -> p c t i", i=run),
-                    src.rearrange("p t (c i) -> p c t i", i=run),
+                copy(
+                    out=dst[:, lo:hi, :].rearrange("p (c l) s -> p c s l", l=RUN),
+                    in_=src.rearrange("p s (c l) -> p c s l", l=RUN),
                 )
 
-        def side_weave(slot, name, a, h, lo, hi):
-            staged["side", name, a, h, lo] = work.tile([P, hi - lo, 4], BF16, name=slot, align_bytes=64)
+        def weave_in_window(n, name, a, h, lo, hi):
+            staged["window", name, a, h, lo] = swap(n, [P, hi - lo, 4], BF16)
             src = raw[name, a, h][:, :, lo:hi]
-            dst = staged["side", name, a, h, lo][:]
+            dst = staged["window", name, a, h, lo][:]
             if name == "wv":
                 src = src.rearrange("p (e u) c -> p c u e", u=2)
                 dst = dst.rearrange("p c (u e) -> p c u e", u=2)
             else:
-                src = src.rearrange("p t c -> p c t")
-            nc.gpsimd.tensor_scalar(out=dst, in0=src, scalar1=1.0, scalar2=0.0, op0=MULT, op1=mybir.AluOpType.add)
+                src = src.rearrange("p s c -> p c s")
+            nc.gpsimd.tensor_scalar(out=dst, in0=src, scalar1=1.0, scalar2=0.0, op0=MULT, op1=ADD)
+
+        def weave_chunk(q):
+            src = planes[:].rearrange("p (i s j) -> p i s j", i=4, s=4)[:, :, :, P * q : P * (q + 1)]
+            dst = stage(("chunk", 1, q))[:].rearrange("p (i j) s -> p i j s", i=4)
+            vector(
+                out=dst.rearrange("p i (c l) s -> p i c s l", l=RUN),
+                in_=src.rearrange("p i s (c l) -> p i c s l", l=RUN),
+            )
+
+        def new_operand(key, width):
+            if key[0] in ("step", "chunk"):
+                codes[key] = work.tile([P, width], U32, name="q_dvp", bufs=DVP_CODE_BUFS, align_bytes=64)
+                scales[key] = work.tile([P, width], U8, name="s_dvp", bufs=DVP_CODE_BUFS, align_bytes=64)
+            else:
+                tag = "_".join(str(part) for part in key)
+                codes[key] = keep.tile([P, width], U32, name="q_" + tag, align_bytes=64)
+                scales[key] = keep.tile([P, width], U8, name="s_" + tag, align_bytes=64)
+
+        def quantise(key, src, fmt):
+            new_operand(key, src.shape[1] // 4)
+            nc.vector.quantize_mx(out=codes[key][:].bitcast(fmt), scales=scales[key][:], in_=src)
+
+        def quant_staged(name, a, h):
+            quantise((name, a, h), staged[name, a, h][:].rearrange("p c t -> p (c t)"), E5 if name == "chunk" else E4)
 
         def quant_part(name, a, h, lo, hi):
             if (name, a, h) not in codes:
-                codes[name, a, h] = keep.tile([P, HALF], U32, name="q_%s%d%d" % (name, a, h), align_bytes=64)
-                scales[name, a, h] = keep.tile([P, HALF], U8, name="s_%s%d%d" % (name, a, h), align_bytes=64)
-            side = ("side", name, a, h, lo)
-            src = staged[side][:] if side in staged else staged[name, a, h][:, lo:hi, :]
+                new_operand((name, a, h), HALF)
+            piece = ("window", name, a, h, lo)
+            src = staged[piece][:] if piece in staged else staged[name, a, h][:, lo:hi, :]
             nc.vector.quantize_mx(
                 out=codes[name, a, h][:, lo:hi].bitcast(E4),
                 scales=scales[name, a, h][:, lo:hi],
                 in_=src.rearrange("p c t -> p (c t)"),
             )
 
-        def quant_staged(name, a, h):
-            quantise((name, a, h), staged[name, a, h][:].rearrange("p c t -> p (c t)"), E5 if name == "d" else E4)
+        def quant_woven(q):
+            quantise(("chunk", 0, q), woven[q][:], E5)
+
+        def quant_step(k):
+            quantise(("step", k), staged["step", k][:].bitcast(BF16), E5)
+
+        def mx_pass(out, left, m, right, cols, start, stop):
+            window = slice(P * m, P * (m + 1))
+            nc.tensor.matmul_mx(
+                out=out,
+                lhsT=codes[left][:, window].bitcast(E5),
+                lhsT_scale=scales[left][:, window],
+                rhs=codes[right][:, cols].bitcast(E4),
+                rhs_scale=scales[right][:, cols],
+                start=start,
+                stop=stop,
+            )
+
+        every = slice(0, HALF)
+
 
         def turn_go(i, n):
             banks["go", i] = bank(n, [P, 4, P])
-            words = go_raw[i].bitcast(F32)
+            words = raw["go", i].bitcast(F32)
             for a in range(2):
                 for u in range(2):
-                    nc.tensor.transpose(banks["go", i][:, 2 * a + u, :], words[:, 256 * a + u : 256 * a + 256 : 2], ident[:])
+                    src = words[:, QUARTER * a + u : QUARTER * (a + 1) : 2]
+                    nc.tensor.transpose(banks["go", i][:, 2 * a + u, :], src, ident[:])
 
-        def copy_go(engine, i):
+        def copy_go(i):
             staged["go", i] = work.tile([P, HALF], F32, name="go_turned", bufs=2, align_bytes=64)
-            copy_on(
-                engine,
-                staged["go", i][:].rearrange("p (a b l u) -> p a b u l", a=2, u=2, l=2),
-                banks["go", i][:].rearrange("p (a u) (b l) -> p a b u l", u=2, l=2),
+            scalar(
+                out=staged["go", i][:].rearrange("p (a b l u) -> p a b u l", a=2, u=2, l=RUN),
+                in_=banks["go", i][:].rearrange("p (a u) (b l) -> p a b u l", u=2, l=RUN),
             )
 
         def quant_go(i):
-            quantise(("go", i, 0), staged["go", i][:].bitcast(BF16), E5)
+            quantise(("go", i), staged["go", i][:].bitcast(BF16), E5)
 
-        def dattn(i, g, n):
-            banks["da", i, g] = bank(n, [P, HALF])
+        def dattn(i, g):
+            banks["dattn", i, g] = bank(DATTN_BANKS[g], [P, HALF])
             for a in range(2):
-                m = slice(P * a, P * (a + 1))
-                nc.tensor.matmul_mx(
-                    out=banks["da", i, g][:],
-                    lhsT=codes["go", i, 0][:, m].bitcast(E5),
-                    lhsT_scale=scales["go", i, 0][:, m],
-                    rhs=codes["wo", a, g][:].bitcast(E4),
-                    rhs_scale=scales["wo", a, g][:],
-                    start=(a == 0),
-                    stop=(a == 1),
-                )
+                mx_pass(banks["dattn", i, g][:], ("go", i), a, ("wo", a, g), every, a == 0, a == 1)
+
 
         def plane(i, s):
             return planes[:, HALF * (4 * i + s) : HALF * (4 * i + s + 1)]
 
         def weigh_woven(i, u):
+            shape = [P, 8, 16, 4]
             for e in range(2):
-                column = banks["da", i, 0][:, 256 * u + e : 256 * (u + 1) : 2]
+                column = banks["dattn", i, 0][:, QUARTER * u + e : QUARTER * (u + 1) : 2]
                 nc.vector.tensor_tensor(
-                    out=woven[2 * u + e][:, HALF * i : HALF * (i + 1)].rearrange("p (h j s) -> p h j s", h=8, s=4),
-                    in0=by_head[i].unsqueeze(2).to_broadcast([P, 8, 16, 4]),
-                    in1=column.rearrange("p (h j) -> p h j", h=8).unsqueeze(3).to_broadcast([P, 8, 16, 4]),
+                    out=woven[2 * u + e][:, HALF * i : HALF * (i + 1)].rearrange("p (h m s) -> p h m s", h=8, s=4),
+                    in0=pw_by_head[:, i].unsqueeze(2).to_broadcast(shape),
+                    in1=column.rearrange("p (h m) -> p h m", h=8).unsqueeze(3).to_broadcast(shape),
                     op=MULT,
                 )
 
         def weigh_planes(k):
-            i = k // 2
-            for s in (2 * (k % 2), 2 * (k % 2) + 1):
+            i, pair = divmod(k, 2)
+            for s in (2 * pair, 2 * pair + 1):
                 nc.vector.tensor_tensor(
-                    out=plane(i, s).rearrange("p (u h j) -> p u h j", u=2, h=8),
-                    in0=pw[i][:, s, 8:16].unsqueeze(1).unsqueeze(3).to_broadcast([P, 2, 8, 32]),
-                    in1=banks["da", i, 1][:].rearrange("p (u h j) -> p u h j", u=2, h=8),
+                    out=plane(i, s).rearrange("p (u h r) -> p u h r", u=2, h=8),
+                    in0=pw[:, i, s, 8:16].unsqueeze(1).unsqueeze(3).to_broadcast([P, 2, 8, 32]),
+                    in1=banks["dattn", i, 1][:].rearrange("p (u h r) -> p u h r", u=2, h=8),
                     op=MULT,
                 )
 
-        def turn(k, g, n):
-            banks["t", k, g] = bank(n, [P, 4, P])
+        def turn(k, g):
+            banks["turn", k, g] = bank(TURN_BANKS[g], [P, 4, P])
             i, pair = divmod(k, 2)
             for q in range(4):
                 if g == 0:
-                    words = woven[q][:].bitcast(F32)[:, 256 * i + pair : 256 * (i + 1) : 2]
+                    words = woven[q][:].bitcast(F32)[:, QUARTER * i + pair : QUARTER * (i + 1) : 2]
                 else:
                     words = plane(i, 2 * pair + q // 2).bitcast(F32)[:, P * (q % 2) : P * (q % 2 + 1)]
-                nc.tensor.transpose(banks["t", k, g][:, q, :], words, ident[:])
+                nc.tensor.transpose(banks["turn", k, g][:, q, :], words, ident[:])
 
-        def copy_turned(engine, k, g):
-            if ("t", k) not in staged:
-                staged["t", k] = work.tile([P, 2 * HALF], F32, name="swap%d" % (k % TURNED), align_bytes=64)
-            dst = staged["t", k][:, HALF * g : HALF * (g + 1)]
-            src = banks["t", k, g][:]
+        def copy_turned(k, g):
             if g == 0:
-                copy_on(
-                    engine,
-                    dst.bitcast(BF16).rearrange("p (e b q) -> p e b q", e=2, q=4),
-                    src.rearrange("p q b -> p (q b)").bitcast(BF16).rearrange("p (q b e) -> p e b q", q=4, e=2),
+                staged["step", k] = swap(k, [P, 2 * HALF], F32)
+            dst = staged["step", k][:, HALF * g : HALF * (g + 1)]
+            src = banks["turn", k, g][:]
+            if g == 0:
+                scalar(
+                    out=dst.bitcast(BF16).rearrange("p (s b q) -> p s b q", s=2, q=4),
+                    in_=src.rearrange("p q b -> p (q b)").bitcast(BF16).rearrange("p (q b s) -> p s b q", q=4, s=2),
                 )
             else:
-                copy_on(
-                    engine,
-                    dst.rearrange("p (e b u) -> p e b u", e=2, u=2),
-                    src.rearrange("p (e u) b -> p e b u", u=2),
+                scalar(
+                    out=dst.rearrange("p (s b u) -> p s b u", s=2, u=2),
+                    in_=src.rearrange("p (s u) b -> p s b u", u=2),
                 )
 
-        def quant_woven(q):
-            quantise(("d", 0, q), woven[q][:], E5)
 
-        def quant_turned(k):
-            quantise(("t", k, 0), staged["t", k][:].bitcast(BF16), E5)
-
-        def product0(k, e, h, n):
-            banks["o0", k, e, h] = bank(n, [P, HALF])
+        def product0(k, s, h, n):
+            banks["o0", k, s, h] = bank(n, [P, HALF])
             for g in range(2):
-                m = slice(P * (2 * g + e), P * (2 * g + e + 1))
-                nc.tensor.matmul_mx(
-                    out=banks["o0", k, e, h][:],
-                    lhsT=codes["t", k, 0][:, m].bitcast(E5),
-                    lhsT_scale=scales["t", k, 0][:, m],
-                    rhs=codes["wv", g, h][:].bitcast(E4),
-                    rhs_scale=scales["wv", g, h][:],
-                    start=(g == 0),
-                    stop=(g == 1),
-                )
+                mx_pass(banks["o0", k, s, h][:], ("step", k), 2 * g + s, ("wv", g, h), every, g == 0, g == 1)
 
-        def weave_d(engine, g, q, part=0, parts=1):
-            n = 4 // parts
-            src = planes[:].rearrange("p (i s j) -> p i s j", i=4, s=4)[:, n * part : n * (part + 1), :, P * q : P * (q + 1)]
-            dst = stage(("d", g, q))[:].rearrange("p (i j) s -> p i j s", i=4)[:, n * part : n * (part + 1)]
-            run = RUN[engine]
-            copy_on(engine, dst.rearrange("p i (c l) s -> p i c s l", l=run), src.rearrange("p i s (c l) -> p i c s l", l=run))
-
-        def pass1(g, q, h, i, n, last=3):
+        def pass1(g, q, h, i, n):
             if i == 0:
                 banks["o1", g, q, h] = bank(n, [P, HALF])
-            nc.tensor.matmul_mx(
-                out=banks["o1", g, q, h][:],
-                lhsT=codes["d", g, q][:, P * i : P * (i + 1)].bitcast(E5),
-                lhsT_scale=scales["d", g, q][:, P * i : P * (i + 1)],
-                rhs=codes["x", i, h][:].bitcast(E4),
-                rhs_scale=scales["x", i, h][:],
-                start=(i == 0),
-                stop=(i == last),
-            )
-
-        def last_product1(engine, g, q, quarter, n):
-            acc = bank(n, [P, HALF // 2])
-            h, cols = quarter // 2, slice(256 * (quarter % 2), 256 * (quarter % 2 + 1))
-            for i in range(4):
-                nc.tensor.matmul_mx(
-                    out=acc[:],
-                    lhsT=codes["d", g, q][:, P * i : P * (i + 1)].bitcast(E5),
-                    lhsT_scale=scales["d", g, q][:, P * i : P * (i + 1)],
-                    rhs=codes["x", i, h][:, cols].bitcast(E4),
-                    rhs_scale=scales["x", i, h][:, cols],
-                    start=(i == 0),
-                    stop=(i == 3),
-                )
-            part = work.tile([P, HALF // 2], F32, name="last%d" % quarter)
-            copy_on(engine, part[:], acc[:])
-            first = HALF * g + 256 * (q % 2)
-            dst = out_1[first : first + 256, 256 * quarter : 256 * (quarter + 1)]
-            nc.sync.dma_start(out=dst.rearrange("(r u) d -> u r d", u=2)[q // 2], in_=part[:])
+            mx_pass(banks["o1", g, q, h][:], ("chunk", g, q), i, ("x", i, h), every, i == 0, i == 3)
 
         def product1(g, q, h, n):
             for i in range(4):
                 pass1(g, q, h, i, n)
 
-        def empty(engine, name, a, b, h):
-            if (name, a, b) not in rows:
-                rows[name, a, b] = work.tile([P, 2 * HALF], F32, name="rows", bufs=ROWS)
-            copy_on(engine, rows[name, a, b][:, HALF * h : HALF * (h + 1)], banks[name, a, b, h][:])
+        def rows_of_out_1(g, q):
+            if g == 0:
+                return out_1[0:HALF, :].rearrange("(m t) d -> t m d", t=4)[2 * (q % 2) + q // 2]
+            first = HALF + QUARTER * (q % 2)
+            return out_1[first : first + QUARTER, :].rearrange("(r u) d -> u r d", u=2)[q // 2]
 
-        def store(name, a, b, lo=0, hi=2):
-            cols = slice(HALF * lo, HALF * hi)
-            if name == "o0":
-                dst = out_0[2 * (a % 2) + b, P * (a // 2) : P * (a // 2 + 1), cols]
-            elif a == 0:
-                dst = out_1[0:HALF, cols].rearrange("(m t) d -> t m d", t=4)[2 * (b % 2) + b // 2]
-            else:
-                first = HALF * a + 256 * (b % 2)
-                dst = out_1[first : first + 256, cols].rearrange("(r u) d -> u r d", u=2)[b // 2]
-            nc.sync.dma_start(out=dst, in_=rows[name, a, b][:, cols])
+        def empty(copy, name, a, b, h):
+            if (name, a, b) not in rows:
+                rows[name, a, b] = work.tile([P, 2 * HALF], F32, name="rows", bufs=ROW_BUFS)
+            copy(out=rows[name, a, b][:, HALF * h : HALF * (h + 1)], in_=banks[name, a, b, h][:])
+
+        def store0(k, s):
+            i, pair = divmod(k, 2)
+            nc.sync.dma_start(out=out_0[2 * pair + s, P * i : P * (i + 1), :], in_=rows["o0", k, s][:])
+
+        def store1(g, q, h):
+            cols = slice(HALF * h, HALF * (h + 1))
+            nc.sync.dma_start(out=rows_of_out_1(g, q)[:, cols], in_=rows["o1", g, q][:, cols])
+
+        def last_quarter(copy, part, n):
+            acc = bank(n, [P, QUARTER])
+            cols = slice(QUARTER * part, QUARTER * (part + 1))
+            for i in range(4):
+                mx_pass(acc[:], ("chunk", 1, 3), i, ("x", i, 1), cols, i == 0, i == 3)
+            piece = work.tile([P, QUARTER], F32, name="last%d" % part)
+            copy(out=piece[:], in_=acc[:])
+            first = HALF + QUARTER * part
+            nc.sync.dma_start(out=rows_of_out_1(1, 3)[:, first : first + QUARTER], in_=piece[:])
 
         with tc.manual_schedule():
-            load_w_whole("wo", 0)
+            load_first_rows_of_wo()
             load_go(0, 1)
-            load_w("wo", 1, 0)
-            load_w("wo", 1, 1)
-            load_w("wv", 0, 0)
-            load_pw(0, nc.sync)
-            load_w("wv", 1, 0)
+            load_weight("wo", 1, 0)
+            load_weight("wo", 1, 1)
+            load_weight("wv", 0, 0)
+            load_pw(0)
+            load_weight("wv", 1, 0)
             load_go(1, 1)
-            load_w("wv", 0, 1)
-            load_w("wv", 1, 1)
-            load_pw(1, nc.sync)
+            load_weight("wv", 0, 1)
+            load_weight("wv", 1, 1)
+            load_pw(1)
             load_go(2, 2)
-            load_pw(2, nc.sync)
-            load_pw(3, nc.sync)
-            load_x_half(0, 0)
-            load_x_half(1, 0)
-            load_x_half(2, 0)
-            turn_go(0, 7)
-            weave("V", "wo", 0, 0, 0, 8, 5)
-            weave("S", "wo", 0, 0, 5, 8, 3)
-            weave("V", "wo", 0, 1, 0, 8, 3)
-            weave("S", "wo", 0, 1, 3, 8, 5)
+            load_pw(2)
+            load_pw(3)
+            for i in range(3):
+                load_values(i, 0)
+
+            turn_go(0, SUM_BANKS[3])
+            weave(vector, "wo", 0, 0, 0, LARGE)
+            weave(scalar, "wo", 0, 0, LARGE, HALF)
+            weave(vector, "wo", 0, 1, 0, SMALL)
+            weave(scalar, "wo", 0, 1, SMALL, HALF)
             quant_staged("wo", 0, 0)
-            copy_go("S", 0)
-            weave("V", "wo", 1, 0, 0, 8, 5)
-            weave("S", "wo", 1, 0, 5, 8, 3)
+            copy_go(0)
+            weave(vector, "wo", 1, 0, 0, LARGE)
+            weave(scalar, "wo", 1, 0, LARGE, HALF)
             quant_go(0)
             quant_staged("wo", 1, 0)
-            dattn(0, 0, 0)
-            stage(("wo", 1, 1), "swap2")
-            weave("V", "wo", 1, 1, 0, 8, 3)
-            weave("S", "wo", 1, 1, 3, 8, 5)
+            dattn(0, 0)
+            staged["wo", 1, 1] = swap(2, [P, HALF, 4], BF16)
+            weave(vector, "wo", 1, 1, 0, SMALL)
+            weave(scalar, "wo", 1, 1, SMALL, HALF)
             quant_staged("wo", 0, 1)
             quant_staged("wo", 1, 1)
-            dattn(0, 1, 1)
-            side_weave("swap2", "wv", 0, 0, 0, 384)
+            dattn(0, 1)
+
+            weave_in_window(2, "wv", 0, 0, 0, FIRST_WINDOW)
             sort_pw(0, 1)
-            weave("S", "wv", 0, 0, 3, 4)
+            weave(scalar, "wv", 0, 0, FIRST_WINDOW, HALF)
             weigh_woven(0, 0)
             weigh_woven(0, 1)
             weigh_planes(0)
-            turn_go(1, 7)
-            turn(0, 0, 2)
-            turn(0, 1, 3)
-            weave("S", "wv", 1, 0, 1, 4, 3)
-            copy_go("S", 1)
-            weave("V", "wv", 1, 0, 0, 4)
-            copy_turned("S", 0, 0)
-            copy_turned("S", 0, 1)
+            turn_go(1, SUM_BANKS[3])
+            turn(0, 0)
+            turn(0, 1)
+            weave(scalar, "wv", 1, 0, BEFORE_FIRST_TURN, HALF)
+            copy_go(1)
+            weave(vector, "wv", 1, 0, 0, BEFORE_FIRST_TURN)
+            copy_turned(0, 0)
+            copy_turned(0, 1)
             quant_go(1)
-            dattn(1, 0, 0)
-            quant_part("wv", 0, 0, 384, 512)
+            dattn(1, 0)
+            quant_part("wv", 0, 0, FIRST_WINDOW, HALF)
             quant_staged("wv", 1, 0)
-            quant_part("wv", 0, 0, 0, 384)
-            quant_turned(0)
-            side_weave("swap0", "wv", 0, 1, 256 * (0), 256 * (0) + 256)
-            weave("S", "wv", 0, 1, 1, 2)
+            quant_part("wv", 0, 0, 0, FIRST_WINDOW)
+            quant_step(0)
+
+            weave_in_window(0, "wv", 0, 1, 0, QUARTER)
+            weave(scalar, "wv", 0, 1, QUARTER, HALF)
             sort_pw(1, 2)
-            weave("S", "wv", 1, 1, 3, 8, 5)
-            turn(1, 0, 2)
+            weave(scalar, "wv", 1, 1, SMALL, HALF)
+            turn(1, 0)
             weigh_planes(1)
             weigh_woven(1, 0)
-            copy_turned("S", 1, 0)
-            product0(0, 0, 0, 4)
-            product0(0, 1, 0, 5)
-            turn(1, 1, 3)
-            turn_go(2, 6)
-            turn_go(3, 7)
-            dattn(1, 1, 1)
-            weave("V", "wv", 1, 1, 0, 8, 3)
-            copy_turned("S", 1, 1)
-            quant_part("wv", 0, 1, 256 * (0), 256 * (0) + 256)
-            quant_part("wv", 0, 1, 256 * (1), 256 * (1) + 256)
+            copy_turned(1, 0)
+            product0(0, 0, 0, SUM_BANKS[0])
+            product0(0, 1, 0, SUM_BANKS[1])
+            turn(1, 1)
+            turn_go(2, SUM_BANKS[2])
+            turn_go(3, SUM_BANKS[3])
+            dattn(1, 1)
+            weave(vector, "wv", 1, 1, 0, SMALL)
+            copy_turned(1, 1)
+            quant_part("wv", 0, 1, 0, QUARTER)
+            quant_part("wv", 0, 1, QUARTER, HALF)
             quant_staged("wv", 1, 1)
-            empty("S", "o0", 0, 0, 0)
-            empty("S", "o0", 0, 1, 0)
-            copy_go("S", 2)
-            quant_turned(1)
-            copy_go("S", 3)
+            empty(scalar, "o0", 0, 0, 0)
+            empty(scalar, "o0", 0, 1, 0)
+            copy_go(2)
+            quant_step(1)
+            copy_go(3)
             sort_pw(2, 4)
-            side_weave("swap1", "x", 0, 0, 256 * (0), 256 * (0) + 256)
+
+            def piece(n):
+                return "x", n // 2, 0, QUARTER * (n % 2), QUARTER * (n % 2 + 1)
+
+            done = []
+
+            def group0(k, s, h):
+                product0(k, s, h, SUM_BANKS[len(done) % 4])
+                done.append((k, s, h))
+                in_window = 2 <= k <= 5 and h == 0 and (s == 0 or k == 5)
+                empty(vector if in_window else scalar, "o0", k, s, h)
+                if h == 1:
+                    store0(k, s)
+
+            weave_in_window(1, *piece(0))
             weigh_woven(1, 1)
             weigh_planes(2)
             quant_go(2)
-            acc = 0
-            for k in range(8):
+            for s in range(2):
+                group0(0, s, 1)
+
+            for k in range(1, STEPS):
                 if k == 1:
-                    load_x_half(3, 0)
-                if 2 <= k < 6:
-                    load_x_half(k - 2, 1)
-                if k == 1:
-                    for e in range(2):
-                        product0(k, e, 0, 4 + acc % 4)
-                        acc = acc + 1
-                        empty("S", "o0", k, e, 0)
-                if 1 <= k < 7:
-                    turn(k + 1, 0, 2)
-                    turn(k + 1, 1, 3)
-                if 1 <= k < 5:
-                    dattn((k + 3) // 2, (k + 1) % 2, (k + 1) % 2)
-                if 1 <= k < 7:
-                    copy_turned("S", k + 1, 0)
-                    copy_turned("S", k + 1, 1)
+                    load_values(3, 0)
+                    for s in range(2):
+                        group0(1, s, 0)
+                if 2 <= k <= 5:
+                    load_values(k - 2, 1)
+                if k + 1 < STEPS:
+                    turn(k + 1, 0)
+                    turn(k + 1, 1)
+                if k <= 4:
+                    dattn((k + 3) // 2, (k + 1) % 2)
+                if k + 1 < STEPS:
+                    copy_turned(k + 1, 0)
+                    copy_turned(k + 1, 1)
                 if k == 2:
                     quant_go(3)
-                if 1 <= k < 7:
-                    quant_part("x", (k - 1) // 2, 0, 256 * ((k - 1) % 2), 256 * ((k - 1) % 2) + 256)
-                if 2 <= k < 7:
-                    quant_turned(k)
-                if 1 <= k < 6:
-                    side_weave("swap%d" % (k % 3), "x", k // 2, 0, 256 * (k % 2), 256 * (k % 2) + 256)
-                    if k % 2 == 1:
-                        weigh_planes(k + 2)
-                        if k < 5:
-                            weigh_woven((k + 3) // 2, 0)
-                    else:
-                        weigh_woven((k + 2) // 2, 1)
-                        weigh_planes(k + 2)
-                if k == 6:
-                    weave("V", "x", 3, 0)
-                    quant_turned(7)
+                if k + 1 < STEPS:
+                    quant_part(*piece(k - 1))
+                if 2 <= k < STEPS - 1:
+                    quant_step(k)
+                if k + 2 < STEPS:
+                    weave_in_window(k, *piece(k))
+                    if k % 2 == 0:
+                        weigh_woven(k // 2 + 1, 1)
+                    weigh_planes(k + 2)
+                    if k % 2 == 1 and k + 3 < STEPS:
+                        weigh_woven((k + 3) // 2, 0)
+                if k == STEPS - 2:
+                    weave(vector, "x", 3, 0)
+                    quant_step(STEPS - 1)
                     quant_staged("x", 3, 0)
                     quant_woven(0)
-                    weave("V", "x", 0, 1)
-                if k == 7:
+                    weave(vector, "x", 0, 1)
+                if k == STEPS - 1:
                     for q in range(1, 4):
                         quant_woven(q)
-                    weave("V", "x", 1, 1)
+                    weave(vector, "x", 1, 1)
                     quant_staged("x", 0, 1)
-                for e, h in ((0, 0), (1, 0), (0, 1), (1, 1)):
-                    if k > 1 or h == 1:
-                        product0(k, e, h, 4 + acc % 4)
-                        acc = acc + 1
-                        empty("V" if (e, h) == (0, 0) and k in (2, 3, 5) or (k, e, h) == (5, 1, 0) else "S", "o0", k, e, h)
-                        if h == 1:
-                            store("o0", k, e)
-            weave("S", "x", 2, 1)
-            weave("S", "x", 3, 1)
+                for h in range(1 if k == 1 else 0, 2):
+                    for s in range(2):
+                        group0(k, s, h)
+
+            weave(scalar, "x", 2, 1)
+            weave(scalar, "x", 3, 1)
             quant_staged("x", 1, 1)
             quant_staged("x", 2, 1)
-            weave_d("V", 1, 0)
+            weave_chunk(0)
             quant_staged("x", 3, 1)
-            quant_staged("d", 1, 0)
+            quant_staged("chunk", 1, 0)
             for q in range(4):
                 product1(0, q, 0, q)
             for q in range(4):
-                empty("S", "o1", 0, q, 0)
-                store("o1", 0, q, 0, 1)
+                empty(scalar, "o1", 0, q, 0)
+                store1(0, q, 0)
             for i in range(4):
                 for q in range(4):
-                    pass1(0, q, 1, i, 4 + q)
+                    pass1(0, q, 1, i, SUM_BANKS[q])
+
             for q in range(1, 4):
-                weave_d("V", 1, q)
+                weave_chunk(q)
                 if q > 1:
-                    quant_staged("d", 1, q - 1)
-            quant_staged("d", 1, 3)
+                    quant_staged("chunk", 1, q - 1)
+            quant_staged("chunk", 1, 3)
             for q in range(4):
-                empty("S", "o1", 0, q, 1)
-                store("o1", 0, q, 1, 2)
+                empty(scalar, "o1", 0, q, 1)
+                store1(0, q, 1)
             for q in range(3):
                 for h in range(2):
                     product1(1, q, h, 2 * q + h)
-                    empty("S", "o1", 1, q, h)
-                    store("o1", 1, q, h, h + 1)
+                    empty(scalar, "o1", 1, q, h)
+                    store1(1, q, h)
             product1(1, 3, 0, 6)
-            empty("V", "o1", 1, 3, 0)
-            store("o1", 1, 3, 0, 1)
-            last_product1("S", 1, 3, 2, 7)
-            last_product1("V", 1, 3, 3, 0)
+            empty(vector, "o1", 1, 3, 0)
+            store1(1, 3, 0)
+            last_quarter(scalar, 0, 7)
+            last_quarter(vector, 1, 0)

@@ -23,12 +23,11 @@ RUN = 2
 
 WEAVE_BUFS = 5
 SWAP_BUFS = 3
-ROW_BUFS = 7
+ROW_BUFS = 8
 DVP_CODE_BUFS = 6
 
-LARGE, SMALL = 320, 192
-FIRST_WINDOW = 384
-BEFORE_FIRST_TURN = 128
+LARGE = 320
+WINDOW = 384
 
 DATTN_BANKS = (0, 1)
 TURN_BANKS = (2, 3)
@@ -45,10 +44,10 @@ def tile_multiheadattention_pb_v_kernel(tc, values, logw, Wv, Wo, pool_w, grad_o
 
         ident = keep.tile([P, P], F32, name="ident")
         make_identity(nc, ident[:])
+        ident_bf16 = keep.tile([P, P], BF16, name="ident_bf16")
+        make_identity(nc, ident_bf16[:])
         pw = keep.tile([P, 4, 4, 16], F32, name="pw")
-        pw_by_head = keep.tile([P, 4, 8, 4], F32, name="pw_by_head")
-        woven = [keep.tile([P, 4 * HALF], BF16, name="woven%d" % q, align_bytes=64) for q in range(4)]
-        planes = keep.tile([P, 4 * 4 * HALF], BF16, name="planes", align_bytes=64)
+        planes = [keep.tile([P, 4 * 4 * HALF], BF16, name="planes%d" % g, align_bytes=64) for g in range(2)]
         raw = {}
         staged = {}
         codes = {}
@@ -56,8 +55,8 @@ def tile_multiheadattention_pb_v_kernel(tc, values, logw, Wv, Wo, pool_w, grad_o
         banks = {}
         rows = {}
 
-        def bank(n, shape):
-            return psum.tile(shape, F32, name="bank%d" % n)
+        def bank(n, shape, dtype=F32):
+            return psum.tile(shape, dtype, name="bank%d" % n)
 
         def swap(n, shape, dtype):
             return work.tile(shape, dtype, name="swap%d" % (n % SWAP_BUFS), align_bytes=64)
@@ -66,7 +65,6 @@ def tile_multiheadattention_pb_v_kernel(tc, values, logw, Wv, Wo, pool_w, grad_o
             if key not in staged:
                 staged[key] = work.tile([P, HALF, 4], BF16, name="stage", bufs=WEAVE_BUFS, align_bytes=64)
             return staged[key]
-
 
         def load_pw(i):
             nc.sync.dma_start(out=pw[:, i], in_=pool_w[:, P * i : P * (i + 1), :].rearrange("s p h -> p s h"))
@@ -79,26 +77,22 @@ def tile_multiheadattention_pb_v_kernel(tc, values, logw, Wv, Wo, pool_w, grad_o
                 raw["go", first + i] = tiles[:, i, :]
 
         def load_weight(name, a, h):
-            tile = keep.tile([P, 4, HALF], BF16, name="raw_%s%d%d" % (name, a, h))
+            tile = keep.tile([P, 4, HALF], BF16, name="raw_%s%d" % (name, 2 * h + a))
             src = {"wo": Wo, "wv": Wv}[name][HALF * a : HALF * (a + 1), HALF * h : HALF * (h + 1)]
             nc.sync.dma_start(out=tile[:], in_=src.rearrange("(p j) c -> p j c", j=4))
             raw[name, a, h] = tile[:]
 
-        def load_first_rows_of_wo():
-            tile = keep.tile([P, 4, 2 * HALF], BF16, name="raw_wo0")
-            nc.sync.dma_start(out=tile[:], in_=Wo[0:HALF, :].rearrange("(p j) c -> p j c", j=4))
+        def load_rows_of_wo(a):
+            tile = keep.tile([P, 4, 2 * HALF], BF16, name="rows_wo%d" % a)
+            nc.sync.dma_start(out=tile[:], in_=Wo[HALF * a : HALF * (a + 1), :].rearrange("(p j) c -> p j c", j=4))
             for h in range(2):
-                raw["wo", 0, h] = tile[:, :, HALF * h : HALF * (h + 1)]
+                raw["wo", a, h] = tile[:, :, HALF * h : HALF * (h + 1)]
 
         def load_values(i, h):
-            tile = keep.tile([P, 4, HALF], BF16, name="raw_x%d%d" % (i, h))
+            tile = keep.tile([P, 4, HALF], BF16, name="raw_%s%d" % ("wv" if h else "x", i))
             src = values[:, P * i : P * (i + 1), HALF * h : HALF * (h + 1)]
             nc.sync.dma_start(out=tile[:], in_=src.rearrange("s p d -> p s d"))
             raw["x", i, h] = tile[:]
-
-
-        def sort_pw(lo, hi):
-            scalar(out=pw_by_head[:, lo:hi], in_=pw[:, lo:hi, :, 0:8].rearrange("p i s h -> p i h s"))
 
         def weave(copy, name, a, h, lo=0, hi=HALF):
             src = raw[name, a, h][:, :, lo:hi]
@@ -120,21 +114,52 @@ def tile_multiheadattention_pb_v_kernel(tc, values, logw, Wv, Wo, pool_w, grad_o
                     in_=src.rearrange("p s (c l) -> p c s l", l=RUN),
                 )
 
+        def weave_parity(copy, a, h, u):
+            src = raw["wo", a, h].rearrange("p t (r l u) -> p u r t l", l=RUN, u=2)[:, u]
+            dst = stage(("wo", a, h))[:, QUARTER * u : QUARTER * (u + 1), :]
+            copy(out=dst.rearrange("p (r l) t -> p r t l", l=RUN), in_=src)
+
+        def spin(name, a, h, part, n):
+            banks["spun", name, a, h, part] = bank(n, [P, 2, HALF], BF16)
+            for m in range(2):
+                first = QUARTER * part + P * m
+                src = raw[name, a, h]
+                dst = banks["spun", name, a, h, part][:, m, :]
+                if name == "wo":
+                    src = src.rearrange("p t (r u) -> p u r t", u=2)[:, part, P * m : P * (m + 1), :]
+                    dst = dst.rearrange("p (r t) -> p r t", t=4)
+                else:
+                    src = src[:, :, first : first + P].rearrange("p (e u) c -> p c u e", u=2)
+                    dst = dst.rearrange("p (c u e) -> p c u e", u=2, e=2)
+                nc.tensor.matmul(dst, lhsT=ident_bf16[:], rhs=src, start=True, stop=True)
+
+        def copy_spun(copy, name, a, h, part):
+            dst = stage((name, a, h))[:, QUARTER * part : QUARTER * (part + 1), :]
+            copy(
+                out=dst.rearrange("p c t -> p (c t)").bitcast(F32),
+                in_=banks["spun", name, a, h, part][:].rearrange("p m c -> p (m c)").bitcast(F32),
+            )
+
         def weave_in_window(n, name, a, h, lo, hi):
-            staged["window", name, a, h, lo] = swap(n, [P, hi - lo, 4], BF16)
+            if n is None:
+                staged["window", name, a, h, lo] = work.tile([P, hi - lo, 4], BF16, name="piece", align_bytes=64)
+            else:
+                staged["window", name, a, h, lo] = swap(n, [P, hi - lo, 4], BF16)
             src = raw[name, a, h][:, :, lo:hi]
             dst = staged["window", name, a, h, lo][:]
-            if name == "wv":
+            if name == "wo":
+                src = raw[name, a, h].rearrange("p t (r u) -> p u r t", u=2)[:, lo // QUARTER]
+            elif name == "wv":
                 src = src.rearrange("p (e u) c -> p c u e", u=2)
                 dst = dst.rearrange("p c (u e) -> p c u e", u=2)
             else:
                 src = src.rearrange("p s c -> p c s")
             nc.gpsimd.tensor_scalar(out=dst, in0=src, scalar1=1.0, scalar2=0.0, op0=MULT, op1=ADD)
 
-        def weave_chunk(q):
-            src = planes[:].rearrange("p (i s j) -> p i s j", i=4, s=4)[:, :, :, P * q : P * (q + 1)]
-            dst = stage(("chunk", 1, q))[:].rearrange("p (i j) s -> p i j s", i=4)
-            vector(
+        def weave_chunk(copy, g, q, lo=0, hi=4):
+            src = planes[g][:].rearrange("p (i s j) -> p i s j", i=4, s=4)[:, lo:hi, :, P * q : P * (q + 1)]
+            dst = stage(("chunk", g, q))[:].rearrange("p (i j) s -> p i j s", i=4)[:, lo:hi]
+            copy(
                 out=dst.rearrange("p i (c l) s -> p i c s l", l=RUN),
                 in_=src.rearrange("p i s (c l) -> p i c s l", l=RUN),
             )
@@ -166,9 +191,6 @@ def tile_multiheadattention_pb_v_kernel(tc, values, logw, Wv, Wo, pool_w, grad_o
                 in_=src.rearrange("p c t -> p (c t)"),
             )
 
-        def quant_woven(q):
-            quantise(("chunk", 0, q), woven[q][:], E5)
-
         def quant_step(k):
             quantise(("step", k), staged["step", k][:].bitcast(BF16), E5)
 
@@ -186,7 +208,6 @@ def tile_multiheadattention_pb_v_kernel(tc, values, logw, Wv, Wo, pool_w, grad_o
 
         every = slice(0, HALF)
 
-
         def turn_go(i, n):
             banks["go", i] = bank(n, [P, 4, P])
             words = raw["go", i].bitcast(F32)
@@ -195,9 +216,9 @@ def tile_multiheadattention_pb_v_kernel(tc, values, logw, Wv, Wo, pool_w, grad_o
                     src = words[:, QUARTER * a + u : QUARTER * (a + 1) : 2]
                     nc.tensor.transpose(banks["go", i][:, 2 * a + u, :], src, ident[:])
 
-        def copy_go(i):
+        def copy_go(i, copy=scalar):
             staged["go", i] = work.tile([P, HALF], F32, name="go_turned", bufs=2, align_bytes=64)
-            scalar(
+            copy(
                 out=staged["go", i][:].rearrange("p (a b l u) -> p a b u l", a=2, u=2, l=RUN),
                 in_=banks["go", i][:].rearrange("p (a u) (b l) -> p a b u l", u=2, l=RUN),
             )
@@ -210,28 +231,16 @@ def tile_multiheadattention_pb_v_kernel(tc, values, logw, Wv, Wo, pool_w, grad_o
             for a in range(2):
                 mx_pass(banks["dattn", i, g][:], ("go", i), a, ("wo", a, g), every, a == 0, a == 1)
 
+        def plane(g, i, s):
+            return planes[g][:, HALF * (4 * i + s) : HALF * (4 * i + s + 1)]
 
-        def plane(i, s):
-            return planes[:, HALF * (4 * i + s) : HALF * (4 * i + s + 1)]
-
-        def weigh_woven(i, u):
-            shape = [P, 8, 16, 4]
-            for e in range(2):
-                column = banks["dattn", i, 0][:, QUARTER * u + e : QUARTER * (u + 1) : 2]
-                nc.vector.tensor_tensor(
-                    out=woven[2 * u + e][:, HALF * i : HALF * (i + 1)].rearrange("p (h m s) -> p h m s", h=8, s=4),
-                    in0=pw_by_head[:, i].unsqueeze(2).to_broadcast(shape),
-                    in1=column.rearrange("p (h m) -> p h m", h=8).unsqueeze(3).to_broadcast(shape),
-                    op=MULT,
-                )
-
-        def weigh_planes(k):
+        def weigh(k, g):
             i, pair = divmod(k, 2)
             for s in (2 * pair, 2 * pair + 1):
                 nc.vector.tensor_tensor(
-                    out=plane(i, s).rearrange("p (u h r) -> p u h r", u=2, h=8),
-                    in0=pw[:, i, s, 8:16].unsqueeze(1).unsqueeze(3).to_broadcast([P, 2, 8, 32]),
-                    in1=banks["dattn", i, 1][:].rearrange("p (u h r) -> p u h r", u=2, h=8),
+                    out=plane(g, i, s).rearrange("p (u h r) -> p u h r", u=2, h=8),
+                    in0=pw[:, i, s, 8 * g : 8 * (g + 1)].unsqueeze(1).unsqueeze(3).to_broadcast([P, 2, 8, 32]),
+                    in1=banks["dattn", i, g][:].rearrange("p (u h r) -> p u h r", u=2, h=8),
                     op=MULT,
                 )
 
@@ -239,28 +248,17 @@ def tile_multiheadattention_pb_v_kernel(tc, values, logw, Wv, Wo, pool_w, grad_o
             banks["turn", k, g] = bank(TURN_BANKS[g], [P, 4, P])
             i, pair = divmod(k, 2)
             for q in range(4):
-                if g == 0:
-                    words = woven[q][:].bitcast(F32)[:, QUARTER * i + pair : QUARTER * (i + 1) : 2]
-                else:
-                    words = plane(i, 2 * pair + q // 2).bitcast(F32)[:, P * (q % 2) : P * (q % 2 + 1)]
+                words = plane(g, i, 2 * pair + q // 2).bitcast(F32)[:, P * (q % 2) : P * (q % 2 + 1)]
                 nc.tensor.transpose(banks["turn", k, g][:, q, :], words, ident[:])
 
-        def copy_turned(k, g):
+        def copy_turned(k, g, copy=scalar):
             if g == 0:
                 staged["step", k] = swap(k, [P, 2 * HALF], F32)
             dst = staged["step", k][:, HALF * g : HALF * (g + 1)]
-            src = banks["turn", k, g][:]
-            if g == 0:
-                scalar(
-                    out=dst.bitcast(BF16).rearrange("p (s b q) -> p s b q", s=2, q=4),
-                    in_=src.rearrange("p q b -> p (q b)").bitcast(BF16).rearrange("p (q b s) -> p s b q", q=4, s=2),
-                )
-            else:
-                scalar(
-                    out=dst.rearrange("p (s b u) -> p s b u", s=2, u=2),
-                    in_=src.rearrange("p (s u) b -> p s b u", u=2),
-                )
-
+            copy(
+                out=dst.rearrange("p (s b u) -> p s b u", s=2, u=2),
+                in_=banks["turn", k, g][:].rearrange("p (s u) b -> p s b u", u=2),
+            )
 
         def product0(k, s, h, n):
             banks["o0", k, s, h] = bank(n, [P, HALF])
@@ -277,9 +275,7 @@ def tile_multiheadattention_pb_v_kernel(tc, values, logw, Wv, Wo, pool_w, grad_o
                 pass1(g, q, h, i, n)
 
         def rows_of_out_1(g, q):
-            if g == 0:
-                return out_1[0:HALF, :].rearrange("(m t) d -> t m d", t=4)[2 * (q % 2) + q // 2]
-            first = HALF + QUARTER * (q % 2)
+            first = HALF * g + QUARTER * (q % 2)
             return out_1[first : first + QUARTER, :].rearrange("(r u) d -> u r d", u=2)[q // 2]
 
         def empty(copy, name, a, b, h):
@@ -306,170 +302,194 @@ def tile_multiheadattention_pb_v_kernel(tc, values, logw, Wv, Wo, pool_w, grad_o
             nc.sync.dma_start(out=rows_of_out_1(1, 3)[:, first : first + QUARTER], in_=piece[:])
 
         with tc.manual_schedule():
-            load_first_rows_of_wo()
+            done = []
+
+            def group0(k, s, h, copy=scalar):
+                product0(k, s, h, SUM_BANKS[len(done) % 4])
+                done.append((k, s, h))
+                empty(copy, "o0", k, s, h)
+                if h == 1:
+                    store0(k, s)
+
+            def piece(n):
+                return "x", n % 4, n // 4
+
+            load_rows_of_wo(0)
             load_go(0, 1)
-            load_weight("wo", 1, 0)
-            load_weight("wo", 1, 1)
-            load_weight("wv", 0, 0)
+            load_rows_of_wo(1)
             load_pw(0)
+            load_weight("wv", 0, 0)
             load_weight("wv", 1, 0)
             load_go(1, 1)
             load_weight("wv", 0, 1)
             load_weight("wv", 1, 1)
             load_pw(1)
             load_go(2, 2)
+            load_values(0, 0)
             load_pw(2)
+            load_values(1, 0)
             load_pw(3)
-            for i in range(3):
-                load_values(i, 0)
+            load_values(2, 0)
+            load_values(3, 0)
 
-            turn_go(0, SUM_BANKS[3])
             weave(vector, "wo", 0, 0, 0, LARGE)
             weave(scalar, "wo", 0, 0, LARGE, HALF)
-            weave(vector, "wo", 0, 1, 0, SMALL)
-            weave(scalar, "wo", 0, 1, SMALL, HALF)
+            spin("wo", 0, 1, 0, 4)
+            turn_go(0, 6)
             quant_staged("wo", 0, 0)
-            copy_go(0)
-            weave(vector, "wo", 1, 0, 0, LARGE)
-            weave(scalar, "wo", 1, 0, LARGE, HALF)
+            spin("wo", 0, 1, 1, 5)
+            copy_go(0, vector)
+            copy_spun(scalar, "wo", 0, 1, 0)
+            staged["wo", 1, 1] = swap(2, [P, HALF, 4], BF16)
+            spin("wo", 1, 1, 0, 7)
+            spin("wo", 1, 1, 1, 4)
+            weave(vector, "wo", 1, 0, 0, WINDOW)
+            weave(scalar, "wo", 1, 0, WINDOW, HALF)
+            copy_spun(scalar, "wo", 0, 1, 1)
             quant_go(0)
             quant_staged("wo", 1, 0)
+            copy_spun(scalar, "wo", 1, 1, 0)
+            copy_spun(scalar, "wo", 1, 1, 1)
             dattn(0, 0)
-            staged["wo", 1, 1] = swap(2, [P, HALF, 4], BF16)
-            weave(vector, "wo", 1, 1, 0, SMALL)
-            weave(scalar, "wo", 1, 1, SMALL, HALF)
             quant_staged("wo", 0, 1)
             quant_staged("wo", 1, 1)
             dattn(0, 1)
-
-            weave_in_window(2, "wv", 0, 0, 0, FIRST_WINDOW)
-            sort_pw(0, 1)
-            weave(scalar, "wv", 0, 0, FIRST_WINDOW, HALF)
-            weigh_woven(0, 0)
-            weigh_woven(0, 1)
-            weigh_planes(0)
-            turn_go(1, SUM_BANKS[3])
+            weave_in_window(2, "wv", 0, 0, 0, HALF)
+            spin("wv", 1, 0, 0, 6)
+            weave(scalar, "wv", 1, 0, QUARTER, HALF)
+            copy_spun(scalar, "wv", 1, 0, 0)
+            weigh(0, 0)
+            weigh(0, 1)
+            weigh(1, 0)
             turn(0, 0)
-            turn(0, 1)
-            weave(scalar, "wv", 1, 0, BEFORE_FIRST_TURN, HALF)
-            copy_go(1)
-            weave(vector, "wv", 1, 0, 0, BEFORE_FIRST_TURN)
+            turn_go(1, 4)
             copy_turned(0, 0)
+            copy_go(1)
+            spin("wv", 0, 1, 0, 5)
+            spin("wv", 0, 1, 1, 6)
+            turn(0, 1)
+            turn(1, 0)
+            copy_spun(scalar, "wv", 0, 1, 0)
             copy_turned(0, 1)
             quant_go(1)
-            dattn(1, 0)
-            quant_part("wv", 0, 0, FIRST_WINDOW, HALF)
             quant_staged("wv", 1, 0)
-            quant_part("wv", 0, 0, 0, FIRST_WINDOW)
+            quant_part("wv", 0, 0, 0, HALF)
+            spin("wv", 1, 1, 1, 7)
+            dattn(1, 0)
             quant_step(0)
-
-            weave_in_window(0, "wv", 0, 1, 0, QUARTER)
-            weave(scalar, "wv", 0, 1, QUARTER, HALF)
-            sort_pw(1, 2)
-            weave(scalar, "wv", 1, 1, SMALL, HALF)
-            turn(1, 0)
-            weigh_planes(1)
-            weigh_woven(1, 0)
+            copy_spun(scalar, "wv", 0, 1, 1)
             copy_turned(1, 0)
-            product0(0, 0, 0, SUM_BANKS[0])
-            product0(0, 1, 0, SUM_BANKS[1])
+            copy_spun(scalar, "wv", 1, 1, 1)
+            weave_in_window(0, "wv", 1, 1, 0, P)
+            weave(scalar, "wv", 1, 1, P, QUARTER)
+            weigh(1, 1)
+            group0(0, 0, 0)
+            group0(0, 1, 0)
             turn(1, 1)
-            turn_go(2, SUM_BANKS[2])
-            turn_go(3, SUM_BANKS[3])
+            turn_go(2, SUM_BANKS[len(done) % 4])
+            done.append(None)
             dattn(1, 1)
-            weave(vector, "wv", 1, 1, 0, SMALL)
             copy_turned(1, 1)
-            quant_part("wv", 0, 1, 0, QUARTER)
-            quant_part("wv", 0, 1, QUARTER, HALF)
-            quant_staged("wv", 1, 1)
-            empty(scalar, "o0", 0, 0, 0)
-            empty(scalar, "o0", 0, 1, 0)
             copy_go(2)
+            quant_staged("wv", 0, 1)
+            quant_part("wv", 1, 1, P, HALF)
+            quant_part("wv", 1, 1, 0, P)
+            weave_in_window(0, "x", 0, 0, WINDOW, HALF)
+            weigh(2, 0)
             quant_step(1)
-            copy_go(3)
-            sort_pw(2, 4)
-
-            def piece(n):
-                return "x", n // 2, 0, QUARTER * (n % 2), QUARTER * (n % 2 + 1)
-
-            done = []
-
-            def group0(k, s, h):
-                product0(k, s, h, SUM_BANKS[len(done) % 4])
-                done.append((k, s, h))
-                in_window = 2 <= k <= 5 and h == 0 and (s == 0 or k == 5)
-                empty(vector if in_window else scalar, "o0", k, s, h)
-                if h == 1:
-                    store0(k, s)
-
-            weave_in_window(1, *piece(0))
-            weigh_woven(1, 1)
-            weigh_planes(2)
+            group0(0, 0, 1)
+            group0(0, 1, 1)
+            weave_in_window(1, "x", 0, 0, 0, WINDOW)
+            weigh(2, 1)
+            weigh(3, 0)
+            group0(1, 0, 0)
+            group0(1, 1, 0)
+            turn(2, 0)
+            turn(2, 1)
             quant_go(2)
-            for s in range(2):
-                group0(0, s, 1)
+            quant_part("x", 0, 0, WINDOW, HALF)
+            weave_in_window(0, "x", 1, 0, WINDOW, HALF)
+            copy_turned(2, 0)
+            copy_turned(2, 1)
+            weigh(3, 1)
+            group0(1, 0, 1)
+            group0(1, 1, 1)
+            dattn(2, 0)
+            weave(scalar, "x", 2, 0, WINDOW, HALF)
+            quant_part("x", 0, 0, 0, WINDOW)
+            quant_part("x", 1, 0, WINDOW, HALF)
+            quant_step(2)
 
-            for k in range(1, STEPS):
-                if k == 1:
-                    load_values(3, 0)
-                    for s in range(2):
-                        group0(1, s, 0)
-                if 2 <= k <= 5:
+            for k in range(2, STEPS):
+                if k <= 5:
                     load_values(k - 2, 1)
                 if k + 1 < STEPS:
                     turn(k + 1, 0)
                     turn(k + 1, 1)
-                if k <= 4:
-                    dattn((k + 3) // 2, (k + 1) % 2)
+                if k == 2:
+                    turn_go(3, SUM_BANKS[len(done) % 4])
+                    done.append(None)
+                    dattn(2, 1)
                 if k + 1 < STEPS:
                     copy_turned(k + 1, 0)
                     copy_turned(k + 1, 1)
                 if k == 2:
-                    quant_go(3)
-                if k + 1 < STEPS:
-                    quant_part(*piece(k - 1))
-                if 2 <= k < STEPS - 1:
-                    quant_step(k)
+                    copy_go(3)
                 if k + 2 < STEPS:
-                    weave_in_window(k, *piece(k))
-                    if k % 2 == 0:
-                        weigh_woven(k // 2 + 1, 1)
-                    weigh_planes(k + 2)
-                    if k % 2 == 1 and k + 3 < STEPS:
-                        weigh_woven((k + 3) // 2, 0)
-                if k == STEPS - 2:
-                    weave(vector, "x", 3, 0)
-                    quant_step(STEPS - 1)
-                    quant_staged("x", 3, 0)
-                    quant_woven(0)
-                    weave(vector, "x", 0, 1)
-                if k == STEPS - 1:
-                    for q in range(1, 4):
-                        quant_woven(q)
+                    weave_in_window(k, *piece(k - 1), 0, WINDOW)
+                    weigh(k + 2, 0)
+                    weigh(k + 2, 1)
+                if k == 2:
+                    quant_go(3)
+                if k in (2, 3):
+                    quant_part(*piece(k), WINDOW, HALF)
+                if k == 5:
+                    weave(vector, *piece(4), WINDOW, HALF)
+                if 3 <= k <= 5:
+                    quant_part(*piece(k - 2), 0, WINDOW)
+                if k == 5:
+                    quant_part(*piece(4), WINDOW, HALF)
+                if k == 6:
+                    weave_chunk(vector, 0, 0)
+                    quant_part(*piece(4), 0, WINDOW)
+                if k + 1 < STEPS:
+                    quant_step(k + 1)
+                if k == 6:
+                    weave_chunk(vector, 0, 1)
+                    quant_staged("chunk", 0, 0)
+                    quant_staged("chunk", 0, 1)
+                    weave_chunk(vector, 0, 2)
+                    weave_chunk(vector, 0, 3)
+                    quant_staged("chunk", 0, 2)
+                    quant_staged("chunk", 0, 3)
                     weave(vector, "x", 1, 1)
-                    quant_staged("x", 0, 1)
-                for h in range(1 if k == 1 else 0, 2):
+                for h in range(2):
                     for s in range(2):
                         group0(k, s, h)
+                    if k == 3:
+                        dattn(3, h)
+                if k == 2:
+                    weave(scalar, *piece(3), WINDOW, HALF)
 
             weave(scalar, "x", 2, 1)
             weave(scalar, "x", 3, 1)
-            quant_staged("x", 1, 1)
             quant_staged("x", 2, 1)
-            weave_chunk(0)
+            quant_staged("x", 1, 1)
+            weave_chunk(vector, 1, 0)
             quant_staged("x", 3, 1)
             quant_staged("chunk", 1, 0)
             for q in range(4):
                 product1(0, q, 0, q)
+                pass1(0, q, 1, 0, SUM_BANKS[q])
             for q in range(4):
                 empty(scalar, "o1", 0, q, 0)
                 store1(0, q, 0)
-            for i in range(4):
+            weave_chunk(scalar, 1, 1, 3, 4)
+            for i in (2, 1, 3):
                 for q in range(4):
                     pass1(0, q, 1, i, SUM_BANKS[q])
-
             for q in range(1, 4):
-                weave_chunk(q)
+                weave_chunk(vector, 1, q, 0, 3 if q == 1 else 4)
                 if q > 1:
                     quant_staged("chunk", 1, q - 1)
             quant_staged("chunk", 1, 3)

@@ -19,6 +19,7 @@ P = 128
 HALF = 512
 QUARTER = 256
 STEPS = 8
+EARLY = 2
 RUN = 2
 
 WEAVE_BUFS = 5
@@ -47,7 +48,11 @@ def tile_multiheadattention_pb_v_kernel(tc, values, logw, Wv, Wo, pool_w, grad_o
         ident_bf16 = keep.tile([P, P], BF16, name="ident_bf16")
         make_identity(nc, ident_bf16[:])
         pw = keep.tile([P, 4, 4, 16], F32, name="pw")
-        planes = [keep.tile([P, 4 * 4 * HALF], BF16, name="planes%d" % g, align_bytes=64) for g in range(2)]
+        pw_by_head = keep.tile([P, 4 - EARLY, 8, 4], F32, name="pw_by_head")
+        woven = [keep.tile([P, 4 * HALF], BF16, name="woven%d" % q, align_bytes=64) for q in range(4)]
+        planes = [
+            keep.tile([P, n * 4 * HALF], BF16, name="planes%d" % g, align_bytes=64) for g, n in enumerate((EARLY, 4))
+        ]
         raw = {}
         staged = {}
         codes = {}
@@ -114,9 +119,9 @@ def tile_multiheadattention_pb_v_kernel(tc, values, logw, Wv, Wo, pool_w, grad_o
                     in_=src.rearrange("p s (c l) -> p c s l", l=RUN),
                 )
 
-        def weave_parity(copy, a, h, u):
-            src = raw["wo", a, h].rearrange("p t (r l u) -> p u r t l", l=RUN, u=2)[:, u]
-            dst = stage(("wo", a, h))[:, QUARTER * u : QUARTER * (u + 1), :]
+        def weave_parity(copy, a, h, u, lo=0, hi=QUARTER):
+            src = raw["wo", a, h].rearrange("p t (r l u) -> p u r t l", l=RUN, u=2)[:, u, lo // RUN : hi // RUN]
+            dst = stage(("wo", a, h))[:, QUARTER * u + lo : QUARTER * u + hi, :]
             copy(out=dst.rearrange("p (r l) t -> p r t l", l=RUN), in_=src)
 
         def spin(name, a, h, part, n):
@@ -155,6 +160,29 @@ def tile_multiheadattention_pb_v_kernel(tc, values, logw, Wv, Wo, pool_w, grad_o
             else:
                 src = src.rearrange("p s c -> p c s")
             nc.gpsimd.tensor_scalar(out=dst, in0=src, scalar1=1.0, scalar2=0.0, op0=MULT, op1=ADD)
+
+        def sort_pw():
+            scalar(out=pw_by_head[:], in_=pw[:, EARLY:, :, 0:8].rearrange("p i s h -> p i h s"))
+
+        def weave_early(copy, q):
+            u, e = divmod(q, 2)
+            src = planes[0][:].rearrange("p (i s u m e) -> p i s u m e", i=EARLY, s=4, u=2, e=2)[:, :, :, u, :, e]
+            dst = woven[q][:, 0 : EARLY * HALF].rearrange("p (i c l s) -> p i c s l", i=EARLY, l=RUN, s=4)
+            copy(out=dst, in_=src.rearrange("p i s (c l) -> p i c s l", l=RUN))
+
+        def quant_woven(q):
+            quantise(("chunk", 0, q), woven[q][:], E5)
+
+        def weigh_woven(i, u):
+            shape = [P, 8, 16, 4]
+            for e in range(2):
+                column = banks["dattn", i, 0][:, QUARTER * u + e : QUARTER * (u + 1) : 2]
+                nc.vector.tensor_tensor(
+                    out=woven[2 * u + e][:, HALF * i : HALF * (i + 1)].rearrange("p (h m s) -> p h m s", h=8, s=4),
+                    in0=pw_by_head[:, i - EARLY].unsqueeze(2).to_broadcast(shape),
+                    in1=column.rearrange("p (h m) -> p h m", h=8).unsqueeze(3).to_broadcast(shape),
+                    op=MULT,
+                )
 
         def weave_chunk(copy, g, q, lo=0, hi=4):
             src = planes[g][:].rearrange("p (i s j) -> p i s j", i=4, s=4)[:, lo:hi, :, P * q : P * (q + 1)]
@@ -216,8 +244,11 @@ def tile_multiheadattention_pb_v_kernel(tc, values, logw, Wv, Wo, pool_w, grad_o
                     src = words[:, QUARTER * a + u : QUARTER * (a + 1) : 2]
                     nc.tensor.transpose(banks["go", i][:, 2 * a + u, :], src, ident[:])
 
-        def copy_go(i, copy=scalar):
-            staged["go", i] = work.tile([P, HALF], F32, name="go_turned", bufs=2, align_bytes=64)
+        def copy_go(i, copy=scalar, n=None):
+            if n is None:
+                staged["go", i] = work.tile([P, HALF], F32, name="go_turned", bufs=2, align_bytes=64)
+            else:
+                staged["go", i] = swap(n, [P, HALF], F32)
             copy(
                 out=staged["go", i][:].rearrange("p (a b l u) -> p a b u l", a=2, u=2, l=RUN),
                 in_=banks["go", i][:].rearrange("p (a u) (b l) -> p a b u l", u=2, l=RUN),
@@ -226,9 +257,10 @@ def tile_multiheadattention_pb_v_kernel(tc, values, logw, Wv, Wo, pool_w, grad_o
         def quant_go(i):
             quantise(("go", i), staged["go", i][:].bitcast(BF16), E5)
 
-        def dattn(i, g):
-            banks["dattn", i, g] = bank(DATTN_BANKS[g], [P, HALF])
-            for a in range(2):
+        def dattn(i, g, passes=(0, 1)):
+            if 0 in passes:
+                banks["dattn", i, g] = bank(DATTN_BANKS[g], [P, HALF])
+            for a in passes:
                 mx_pass(banks["dattn", i, g][:], ("go", i), a, ("wo", a, g), every, a == 0, a == 1)
 
         def plane(g, i, s):
@@ -244,21 +276,31 @@ def tile_multiheadattention_pb_v_kernel(tc, values, logw, Wv, Wo, pool_w, grad_o
                     op=MULT,
                 )
 
-        def turn(k, g):
-            banks["turn", k, g] = bank(TURN_BANKS[g], [P, 4, P])
+        def turn(k, g, n=None):
+            banks["turn", k, g] = bank(TURN_BANKS[g] if n is None else n, [P, 4, P])
             i, pair = divmod(k, 2)
             for q in range(4):
-                words = plane(g, i, 2 * pair + q // 2).bitcast(F32)[:, P * (q % 2) : P * (q % 2 + 1)]
+                if g == 0 and i >= EARLY:
+                    words = woven[q][:].bitcast(F32)[:, QUARTER * i + pair : QUARTER * (i + 1) : 2]
+                else:
+                    words = plane(g, i, 2 * pair + q // 2).bitcast(F32)[:, P * (q % 2) : P * (q % 2 + 1)]
                 nc.tensor.transpose(banks["turn", k, g][:, q, :], words, ident[:])
 
         def copy_turned(k, g, copy=scalar):
             if g == 0:
                 staged["step", k] = swap(k, [P, 2 * HALF], F32)
             dst = staged["step", k][:, HALF * g : HALF * (g + 1)]
-            copy(
-                out=dst.rearrange("p (s b u) -> p s b u", s=2, u=2),
-                in_=banks["turn", k, g][:].rearrange("p (s u) b -> p s b u", u=2),
-            )
+            src = banks["turn", k, g][:]
+            if g == 0 and k // 2 >= EARLY:
+                copy(
+                    out=dst.bitcast(BF16).rearrange("p (s b q) -> p s b q", s=2, q=4),
+                    in_=src.rearrange("p q b -> p (q b)").bitcast(BF16).rearrange("p (q b s) -> p s b q", q=4, s=2),
+                )
+            else:
+                copy(
+                    out=dst.rearrange("p (s b u) -> p s b u", s=2, u=2),
+                    in_=src.rearrange("p (s u) b -> p s b u", u=2),
+                )
 
         def product0(k, s, h, n):
             banks["o0", k, s, h] = bank(n, [P, HALF])
@@ -275,7 +317,9 @@ def tile_multiheadattention_pb_v_kernel(tc, values, logw, Wv, Wo, pool_w, grad_o
                 pass1(g, q, h, i, n)
 
         def rows_of_out_1(g, q):
-            first = HALF * g + QUARTER * (q % 2)
+            if g == 0:
+                return out_1[0:HALF, :].rearrange("(m t) d -> t m d", t=4)[2 * (q % 2) + q // 2]
+            first = HALF + QUARTER * (q % 2)
             return out_1[first : first + QUARTER, :].rearrange("(r u) d -> u r d", u=2)[q // 2]
 
         def empty(copy, name, a, b, h):
@@ -307,24 +351,36 @@ def tile_multiheadattention_pb_v_kernel(tc, values, logw, Wv, Wo, pool_w, grad_o
             def group0(k, s, h, copy=scalar):
                 product0(k, s, h, SUM_BANKS[len(done) % 4])
                 done.append((k, s, h))
-                empty(copy, "o0", k, s, h)
+                empty(vector if (k, h) == (5, 0) else scalar, "o0", k, s, h)
                 if h == 1:
                     store0(k, s)
 
             def piece(n):
                 return "x", n % 4, n // 4
 
+            def pair0(k, h):
+                for s in range(2):
+                    banks["o0", k, s, h] = bank(SUM_BANKS[len(done) % 4], [P, HALF])
+                    done.append((k, s, h))
+                for g in range(2):
+                    for s in range(2):
+                        mx_pass(banks["o0", k, s, h][:], ("step", k), 2 * g + s, ("wv", g, h), every, g == 0, g == 1)
+                for s in range(2):
+                    empty(scalar, "o0", k, s, h)
+                    store0(k, s)
+
             load_rows_of_wo(0)
             load_go(0, 1)
-            load_rows_of_wo(1)
+            load_weight("wo", 1, 0)
+            load_weight("wo", 1, 1)
+            load_go(1, 1)
             load_pw(0)
+            load_go(2, 2)
             load_weight("wv", 0, 0)
             load_weight("wv", 1, 0)
-            load_go(1, 1)
             load_weight("wv", 0, 1)
             load_weight("wv", 1, 1)
             load_pw(1)
-            load_go(2, 2)
             load_values(0, 0)
             load_pw(2)
             load_values(1, 0)
@@ -336,89 +392,84 @@ def tile_multiheadattention_pb_v_kernel(tc, values, logw, Wv, Wo, pool_w, grad_o
             weave(scalar, "wo", 0, 0, LARGE, HALF)
             spin("wo", 0, 1, 0, 4)
             turn_go(0, 6)
-            quant_staged("wo", 0, 0)
             spin("wo", 0, 1, 1, 5)
-            copy_go(0, vector)
+            quant_staged("wo", 0, 0)
             copy_spun(scalar, "wo", 0, 1, 0)
-            staged["wo", 1, 1] = swap(2, [P, HALF, 4], BF16)
-            spin("wo", 1, 1, 0, 7)
-            spin("wo", 1, 1, 1, 4)
-            weave(vector, "wo", 1, 0, 0, WINDOW)
-            weave(scalar, "wo", 1, 0, WINDOW, HALF)
+            weave(vector, "wo", 1, 0, 0, LARGE)
+            weave(scalar, "wo", 1, 0, LARGE, HALF)
+            copy_go(0, vector)
             copy_spun(scalar, "wo", 0, 1, 1)
-            quant_go(0)
+            spin("wo", 1, 1, 0, 7)
             quant_staged("wo", 1, 0)
-            copy_spun(scalar, "wo", 1, 1, 0)
-            copy_spun(scalar, "wo", 1, 1, 1)
+            quant_go(0)
+            weave_parity(scalar, 1, 1, 1)
             dattn(0, 0)
             quant_staged("wo", 0, 1)
-            quant_staged("wo", 1, 1)
-            dattn(0, 1)
-            weave_in_window(2, "wv", 0, 0, 0, HALF)
-            spin("wv", 1, 0, 0, 6)
-            weave(scalar, "wv", 1, 0, QUARTER, HALF)
-            copy_spun(scalar, "wv", 1, 0, 0)
-            weigh(0, 0)
-            weigh(0, 1)
-            weigh(1, 0)
-            turn(0, 0)
+            copy_spun(scalar, "wo", 1, 1, 0)
+            dattn(0, 1, (0,))
             turn_go(1, 4)
-            copy_turned(0, 0)
-            copy_go(1)
-            spin("wv", 0, 1, 0, 5)
-            spin("wv", 0, 1, 1, 6)
-            turn(0, 1)
-            turn(1, 0)
-            copy_spun(scalar, "wv", 0, 1, 0)
-            copy_turned(0, 1)
+            copy_go(1, scalar, 2)
+            weigh(0, 0)
+            turn_go(2, 5)
+            turn_go(3, 6)
+            copy_go(2)
+            copy_go(3)
+            quant_staged("wo", 1, 1)
             quant_go(1)
+            dattn(0, 1, (1,))
+            turn(0, 0)
+            spin("wv", 1, 0, 0, 4)
+            copy_turned(0, 0)
+            weave(scalar, "wv", 1, 0, QUARTER, HALF)
+            weave_in_window(2, "wv", 0, 0, 0, HALF)
+            weigh(1, 0)
+            weigh(0, 1)
+            weigh(1, 1)
+            copy_spun(scalar, "wv", 1, 0, 0)
+            turn(0, 1)
+            turn(1, 0, 5)
+            dattn(1, 0)
+            copy_turned(0, 1)
+            turn(1, 1, 2)
+            spin("wv", 0, 1, 0, 6)
+            copy_turned(1, 0)
+            copy_turned(1, 1)
             quant_staged("wv", 1, 0)
             quant_part("wv", 0, 0, 0, HALF)
-            spin("wv", 1, 1, 1, 7)
-            dattn(1, 0)
             quant_step(0)
-            copy_spun(scalar, "wv", 0, 1, 1)
-            copy_turned(1, 0)
-            copy_spun(scalar, "wv", 1, 1, 1)
-            weave_in_window(0, "wv", 1, 1, 0, P)
-            weave(scalar, "wv", 1, 1, P, QUARTER)
-            weigh(1, 1)
-            group0(0, 0, 0)
-            group0(0, 1, 0)
-            turn(1, 1)
-            turn_go(2, SUM_BANKS[len(done) % 4])
-            done.append(None)
-            dattn(1, 1)
-            copy_turned(1, 1)
-            copy_go(2)
-            quant_staged("wv", 0, 1)
-            quant_part("wv", 1, 1, P, HALF)
-            quant_part("wv", 1, 1, 0, P)
-            weave_in_window(0, "x", 0, 0, WINDOW, HALF)
-            weigh(2, 0)
+            weave(scalar, "wv", 0, 1, QUARTER, HALF)
+            copy_spun(scalar, "wv", 0, 1, 0)
+            weave(scalar, "wv", 1, 1, WINDOW, HALF)
             quant_step(1)
-            group0(0, 0, 1)
-            group0(0, 1, 1)
-            weave_in_window(1, "x", 0, 0, 0, WINDOW)
+            quant_go(2)
+            done.extend([None, None, None])
+            group0(0, 0, 0)
+            dattn(1, 1)
+            weave_in_window(1, "wv", 1, 1, 0, WINDOW)
+            weigh(2, 0)
             weigh(2, 1)
-            weigh(3, 0)
+            group0(0, 1, 0)
             group0(1, 0, 0)
             group0(1, 1, 0)
             turn(2, 0)
             turn(2, 1)
-            quant_go(2)
-            quant_part("x", 0, 0, WINDOW, HALF)
-            weave_in_window(0, "x", 1, 0, WINDOW, HALF)
+            quant_staged("wv", 0, 1)
+            quant_part("wv", 1, 1, 0, WINDOW)
+            quant_part("wv", 1, 1, WINDOW, HALF)
             copy_turned(2, 0)
             copy_turned(2, 1)
+            sort_pw()
+            weave_in_window(1, "x", 0, 0, 0, WINDOW)
+            weigh(3, 0)
             weigh(3, 1)
+            pair0(0, 1)
             group0(1, 0, 1)
-            group0(1, 1, 1)
             dattn(2, 0)
-            weave(scalar, "x", 2, 0, WINDOW, HALF)
-            quant_part("x", 0, 0, 0, WINDOW)
-            quant_part("x", 1, 0, WINDOW, HALF)
+            group0(1, 1, 1)
+            dattn(2, 1)
+            quant_go(3)
             quant_step(2)
+            quant_part("x", 0, 0, 0, WINDOW)
 
             for k in range(2, STEPS):
                 if k <= 5:
@@ -426,56 +477,61 @@ def tile_multiheadattention_pb_v_kernel(tc, values, logw, Wv, Wo, pool_w, grad_o
                 if k + 1 < STEPS:
                     turn(k + 1, 0)
                     turn(k + 1, 1)
-                if k == 2:
-                    turn_go(3, SUM_BANKS[len(done) % 4])
-                    done.append(None)
-                    dattn(2, 1)
-                if k + 1 < STEPS:
                     copy_turned(k + 1, 0)
-                    copy_turned(k + 1, 1)
-                if k == 2:
-                    copy_go(3)
+                    if k < 6:
+                        copy_turned(k + 1, 1)
                 if k + 2 < STEPS:
-                    weave_in_window(k, *piece(k - 1), 0, WINDOW)
-                    weigh(k + 2, 0)
-                    weigh(k + 2, 1)
+                    weave_in_window(k, *piece(k - 1), 0, HALF if k == 2 else WINDOW)
                 if k == 2:
-                    quant_go(3)
-                if k in (2, 3):
-                    quant_part(*piece(k), WINDOW, HALF)
+                    weigh_woven(2, 0)
+                    weigh_woven(2, 1)
+                    weigh(4, 1)
+                if k == 3:
+                    weigh(5, 1)
+                    weigh_woven(3, 0)
+                if k == 4:
+                    weigh_woven(3, 1)
+                    weigh(6, 1)
                 if k == 5:
-                    weave(vector, *piece(4), WINDOW, HALF)
-                if 3 <= k <= 5:
-                    quant_part(*piece(k - 2), 0, WINDOW)
-                if k == 5:
-                    quant_part(*piece(4), WINDOW, HALF)
+                    weigh(7, 1)
                 if k == 6:
-                    weave_chunk(vector, 0, 0)
+                    quant_step(6)
                     quant_part(*piece(4), 0, WINDOW)
-                if k + 1 < STEPS:
+                    copy_turned(7, 1, vector)
+                    weave_early(vector, 0)
+                if k == 3:
+                    for n in (2, 3):
+                        weave(vector, *piece(n), WINDOW, HALF)
+                if k + 1 < STEPS and k != 5:
                     quant_step(k + 1)
+                if k <= 4:
+                    quant_part(*piece(k - 1), 0, HALF if k == 2 else WINDOW)
                 if k == 6:
-                    weave_chunk(vector, 0, 1)
-                    quant_staged("chunk", 0, 0)
-                    quant_staged("chunk", 0, 1)
-                    weave_chunk(vector, 0, 2)
-                    weave_chunk(vector, 0, 3)
-                    quant_staged("chunk", 0, 2)
-                    quant_staged("chunk", 0, 3)
+                    for n in (0, 2, 3):
+                        quant_part(*piece(n), WINDOW, HALF)
+                    weave_early(vector, 1)
+                    quant_woven(0)
+                    weave(vector, *piece(4), WINDOW, HALF)
+                    quant_woven(1)
+                    quant_part(*piece(4), WINDOW, HALF)
+                    weave_early(vector, 2)
+                    weave_early(vector, 3)
+                    quant_woven(2)
                     weave(vector, "x", 1, 1)
+                    quant_woven(3)
                 for h in range(2):
                     for s in range(2):
                         group0(k, s, h)
-                    if k == 3:
-                        dattn(3, h)
+                    if (k, h) in ((2, 1), (3, 1)):
+                        dattn(3, k - 2)
                 if k == 2:
-                    weave(scalar, *piece(3), WINDOW, HALF)
+                    weave(scalar, *piece(0), WINDOW, HALF)
 
             weave(scalar, "x", 2, 1)
             weave(scalar, "x", 3, 1)
-            quant_staged("x", 2, 1)
             quant_staged("x", 1, 1)
             weave_chunk(vector, 1, 0)
+            quant_staged("x", 2, 1)
             quant_staged("x", 3, 1)
             quant_staged("chunk", 1, 0)
             for q in range(4):
@@ -484,12 +540,11 @@ def tile_multiheadattention_pb_v_kernel(tc, values, logw, Wv, Wo, pool_w, grad_o
             for q in range(4):
                 empty(scalar, "o1", 0, q, 0)
                 store1(0, q, 0)
-            weave_chunk(scalar, 1, 1, 3, 4)
-            for i in (2, 1, 3):
+            for i in range(1, 4):
                 for q in range(4):
                     pass1(0, q, 1, i, SUM_BANKS[q])
             for q in range(1, 4):
-                weave_chunk(vector, 1, q, 0, 3 if q == 1 else 4)
+                weave_chunk(vector, 1, q)
                 if q > 1:
                     quant_staged("chunk", 1, q - 1)
             quant_staged("chunk", 1, 3)

@@ -124,9 +124,10 @@ def tile_multiheadattention_pb_v_kernel(tc, values, logw, Wv, Wo, pool_w, grad_o
             dst = stage(("wo", a, h))[:, QUARTER * u + lo : QUARTER * u + hi, :]
             copy(out=dst.rearrange("p (r l) t -> p r t l", l=RUN), in_=src)
 
-        def spin(name, a, h, part, n):
-            banks["spun", name, a, h, part] = bank(n, [P, 2, HALF], BF16)
-            for m in range(2):
+        def spin(name, a, h, part, n, quarters=(0, 1)):
+            if 0 in quarters:
+                banks["spun", name, a, h, part] = bank(n, [P, 2, HALF], BF16)
+            for m in quarters:
                 first = QUARTER * part + P * m
                 src = raw[name, a, h]
                 dst = banks["spun", name, a, h, part][:, m, :]
@@ -371,8 +372,7 @@ def tile_multiheadattention_pb_v_kernel(tc, values, logw, Wv, Wo, pool_w, grad_o
 
             load_rows_of_wo(0)
             load_go(0, 1)
-            load_weight("wo", 1, 0)
-            load_weight("wo", 1, 1)
+            load_rows_of_wo(1)
             load_go(1, 1)
             load_pw(0)
             load_go(2, 2)
@@ -395,19 +395,19 @@ def tile_multiheadattention_pb_v_kernel(tc, values, logw, Wv, Wo, pool_w, grad_o
             spin("wo", 0, 1, 1, 5)
             quant_staged("wo", 0, 0)
             copy_spun(scalar, "wo", 0, 1, 0)
+            copy_go(0, vector)
             weave(vector, "wo", 1, 0, 0, LARGE)
             weave(scalar, "wo", 1, 0, LARGE, HALF)
-            copy_go(0, vector)
             copy_spun(scalar, "wo", 0, 1, 1)
             spin("wo", 1, 1, 0, 7)
-            quant_staged("wo", 1, 0)
             quant_go(0)
+            quant_staged("wo", 1, 0)
             weave_parity(scalar, 1, 1, 1)
             dattn(0, 0)
             quant_staged("wo", 0, 1)
             copy_spun(scalar, "wo", 1, 1, 0)
-            dattn(0, 1, (0,))
             turn_go(1, 4)
+            dattn(0, 1, (0,))
             copy_go(1, scalar, 2)
             weigh(0, 0)
             turn_go(2, 5)
@@ -417,21 +417,22 @@ def tile_multiheadattention_pb_v_kernel(tc, values, logw, Wv, Wo, pool_w, grad_o
             quant_staged("wo", 1, 1)
             quant_go(1)
             dattn(0, 1, (1,))
-            turn(0, 0)
             spin("wv", 1, 0, 0, 4)
-            copy_turned(0, 0)
             weave(scalar, "wv", 1, 0, QUARTER, HALF)
             weave_in_window(2, "wv", 0, 0, 0, HALF)
             weigh(1, 0)
             weigh(0, 1)
             weigh(1, 1)
             copy_spun(scalar, "wv", 1, 0, 0)
+            dattn(1, 0)
+            turn(0, 0)
             turn(0, 1)
             turn(1, 0, 5)
-            dattn(1, 0)
+            copy_turned(0, 0)
             copy_turned(0, 1)
-            turn(1, 1, 2)
+            turn(1, 1, 7)
             spin("wv", 0, 1, 0, 6)
+            dattn(1, 1)
             copy_turned(1, 0)
             copy_turned(1, 1)
             quant_staged("wv", 1, 0)
@@ -440,17 +441,18 @@ def tile_multiheadattention_pb_v_kernel(tc, values, logw, Wv, Wo, pool_w, grad_o
             weave(scalar, "wv", 0, 1, QUARTER, HALF)
             copy_spun(scalar, "wv", 0, 1, 0)
             weave(scalar, "wv", 1, 1, WINDOW, HALF)
-            quant_step(1)
             quant_go(2)
-            done.extend([None, None, None])
+            quant_step(1)
             group0(0, 0, 0)
-            dattn(1, 1)
             weave_in_window(1, "wv", 1, 1, 0, WINDOW)
             weigh(2, 0)
             weigh(2, 1)
             group0(0, 1, 0)
+            done.append(None)
             group0(1, 0, 0)
+            done.extend([None, None])
             group0(1, 1, 0)
+            done.append(None)
             turn(2, 0)
             turn(2, 1)
             quant_staged("wv", 0, 1)
@@ -467,9 +469,8 @@ def tile_multiheadattention_pb_v_kernel(tc, values, logw, Wv, Wo, pool_w, grad_o
             dattn(2, 0)
             group0(1, 1, 1)
             dattn(2, 1)
-            quant_go(3)
             quant_step(2)
-            quant_part("x", 0, 0, 0, WINDOW)
+            quant_go(3)
 
             for k in range(2, STEPS):
                 if k <= 5:
@@ -495,26 +496,27 @@ def tile_multiheadattention_pb_v_kernel(tc, values, logw, Wv, Wo, pool_w, grad_o
                 if k == 5:
                     weigh(7, 1)
                 if k == 6:
-                    quant_step(6)
-                    quant_part(*piece(4), 0, WINDOW)
-                    copy_turned(7, 1, vector)
                     weave_early(vector, 0)
+                    quant_step(6)
+                    quant_part(*piece(3), 0, WINDOW)
+                    copy_turned(7, 1, vector)
+                    weave_early(vector, 1)
                 if k == 3:
                     for n in (2, 3):
                         weave(vector, *piece(n), WINDOW, HALF)
                 if k + 1 < STEPS and k != 5:
                     quant_step(k + 1)
                 if k <= 4:
-                    quant_part(*piece(k - 1), 0, HALF if k == 2 else WINDOW)
+                    quant_part(*piece(k - 2), 0, HALF if k == 3 else WINDOW)
                 if k == 6:
                     for n in (0, 2, 3):
                         quant_part(*piece(n), WINDOW, HALF)
-                    weave_early(vector, 1)
                     quant_woven(0)
                     weave(vector, *piece(4), WINDOW, HALF)
-                    quant_woven(1)
+                    quant_part(*piece(4), 0, WINDOW)
                     quant_part(*piece(4), WINDOW, HALF)
                     weave_early(vector, 2)
+                    quant_woven(1)
                     weave_early(vector, 3)
                     quant_woven(2)
                     weave(vector, "x", 1, 1)

@@ -49,7 +49,8 @@ def tile_multiheadattention_pb_v_kernel(tc, values, logw, Wv, Wo, pool_w, grad_o
         make_identity(nc, ident_bf16[:])
         pw = keep.tile([P, 4, 4, 16], F32, name="pw")
         pw_by_head = keep.tile([P, 4 - EARLY, 8, 4], F32, name="pw_by_head")
-        woven = [keep.tile([P, 4 * HALF], BF16, name="woven%d" % q, align_bytes=64) for q in range(4)]
+        all_woven = keep.tile([P, 4 * 4 * HALF], BF16, name="woven", align_bytes=64)
+        woven = [all_woven[:, 4 * HALF * q : 4 * HALF * (q + 1)] for q in range(4)]
         planes = [
             keep.tile([P, n * 4 * HALF], BF16, name="planes%d" % g, align_bytes=64) for g, n in enumerate((EARLY, 4))
         ]
@@ -119,11 +120,6 @@ def tile_multiheadattention_pb_v_kernel(tc, values, logw, Wv, Wo, pool_w, grad_o
                     in_=src.rearrange("p s (c l) -> p c s l", l=RUN),
                 )
 
-        def weave_parity(copy, a, h, u, lo=0, hi=QUARTER):
-            src = raw["wo", a, h].rearrange("p t (r l u) -> p u r t l", l=RUN, u=2)[:, u, lo // RUN : hi // RUN]
-            dst = stage(("wo", a, h))[:, QUARTER * u + lo : QUARTER * u + hi, :]
-            copy(out=dst.rearrange("p (r l) t -> p r t l", l=RUN), in_=src)
-
         def spin(name, a, h, part, n, quarters=(0, 1)):
             if 0 in quarters:
                 banks["spun", name, a, h, part] = bank(n, [P, 2, HALF], BF16)
@@ -132,7 +128,7 @@ def tile_multiheadattention_pb_v_kernel(tc, values, logw, Wv, Wo, pool_w, grad_o
                 src = raw[name, a, h]
                 dst = banks["spun", name, a, h, part][:, m, :]
                 if name == "wo":
-                    src = src.rearrange("p t (r u) -> p u r t", u=2)[:, part, P * m : P * (m + 1), :]
+                    src = src.rearrange("p t (r u) -> p u r t", u=2)[:, m, P * part : P * (part + 1), :]
                     dst = dst.rearrange("p (r t) -> p r t", t=4)
                 else:
                     src = src[:, :, first : first + P].rearrange("p (e u) c -> p c u e", u=2)
@@ -140,11 +136,12 @@ def tile_multiheadattention_pb_v_kernel(tc, values, logw, Wv, Wo, pool_w, grad_o
                 nc.tensor.matmul(dst, lhsT=ident_bf16[:], rhs=src, start=True, stop=True)
 
         def copy_spun(copy, name, a, h, part):
-            dst = stage((name, a, h))[:, QUARTER * part : QUARTER * (part + 1), :]
-            copy(
-                out=dst.rearrange("p c t -> p (c t)").bitcast(F32),
-                in_=banks["spun", name, a, h, part][:].rearrange("p m c -> p (m c)").bitcast(F32),
-            )
+            dst = stage((name, a, h))[:].rearrange("p c t -> p (c t)").bitcast(F32)
+            if name == "wo":
+                dst = dst.rearrange("p (u part w) -> p part u w", u=2, part=2)[:, part]
+            else:
+                dst = dst.rearrange("p (part m w) -> p part m w", part=2, m=2)[:, part]
+            copy(out=dst, in_=banks["spun", name, a, h, part][:].bitcast(F32))
 
         def weave_in_window(n, name, a, h, lo, hi):
             if n is None:
@@ -165,14 +162,13 @@ def tile_multiheadattention_pb_v_kernel(tc, values, logw, Wv, Wo, pool_w, grad_o
         def sort_pw():
             scalar(out=pw_by_head[:], in_=pw[:, EARLY:, :, 0:8].rearrange("p i s h -> p i h s"))
 
-        def weave_early(copy, q):
-            u, e = divmod(q, 2)
-            src = planes[0][:].rearrange("p (i s u m e) -> p i s u m e", i=EARLY, s=4, u=2, e=2)[:, :, :, u, :, e]
-            dst = woven[q][:, 0 : EARLY * HALF].rearrange("p (i c l s) -> p i c s l", i=EARLY, l=RUN, s=4)
-            copy(out=dst, in_=src.rearrange("p i s (c l) -> p i c s l", l=RUN))
+        def weave_early(copy, i, u):
+            src = planes[0][:].rearrange("p (i s u c l e) -> p i u c e s l", i=EARLY, s=4, u=2, l=RUN, e=2)
+            dst = all_woven[:].rearrange("p (u e i c l s) -> p i u c e s l", u=2, e=2, i=4, l=RUN, s=4)
+            copy(out=dst[:, i, u], in_=src[:, i, u])
 
         def quant_woven(q):
-            quantise(("chunk", 0, q), woven[q][:], E5)
+            quantise(("chunk", 0, q), woven[q], E5)
 
         def weigh_woven(i, u):
             shape = [P, 8, 16, 4]
@@ -282,7 +278,7 @@ def tile_multiheadattention_pb_v_kernel(tc, values, logw, Wv, Wo, pool_w, grad_o
             i, pair = divmod(k, 2)
             for q in range(4):
                 if g == 0 and i >= EARLY:
-                    words = woven[q][:].bitcast(F32)[:, QUARTER * i + pair : QUARTER * (i + 1) : 2]
+                    words = woven[q].bitcast(F32)[:, QUARTER * i + pair : QUARTER * (i + 1) : 2]
                 else:
                     words = plane(g, i, 2 * pair + q // 2).bitcast(F32)[:, P * (q % 2) : P * (q % 2 + 1)]
                 nc.tensor.transpose(banks["turn", k, g][:, q, :], words, ident[:])
@@ -402,7 +398,7 @@ def tile_multiheadattention_pb_v_kernel(tc, values, logw, Wv, Wo, pool_w, grad_o
             spin("wo", 1, 1, 0, 7)
             quant_go(0)
             quant_staged("wo", 1, 0)
-            weave_parity(scalar, 1, 1, 1)
+            weave(scalar, "wo", 1, 1, QUARTER, HALF)
             dattn(0, 0)
             quant_staged("wo", 0, 1)
             copy_spun(scalar, "wo", 1, 1, 0)
@@ -496,11 +492,12 @@ def tile_multiheadattention_pb_v_kernel(tc, values, logw, Wv, Wo, pool_w, grad_o
                 if k == 5:
                     weigh(7, 1)
                 if k == 6:
-                    weave_early(vector, 0)
+                    for n in (0, 2, 3):
+                        quant_part(*piece(n), WINDOW, HALF)
                     quant_step(6)
                     quant_part(*piece(3), 0, WINDOW)
                     copy_turned(7, 1, vector)
-                    weave_early(vector, 1)
+                    weave_early(vector, 0, 0)
                 if k == 3:
                     for n in (2, 3):
                         weave(vector, *piece(n), WINDOW, HALF)
@@ -509,18 +506,17 @@ def tile_multiheadattention_pb_v_kernel(tc, values, logw, Wv, Wo, pool_w, grad_o
                 if k <= 4:
                     quant_part(*piece(k - 2), 0, HALF if k == 3 else WINDOW)
                 if k == 6:
-                    for n in (0, 2, 3):
-                        quant_part(*piece(n), WINDOW, HALF)
+                    weave_early(vector, 1, 0)
+                    weave_early(vector, 0, 1)
                     quant_woven(0)
-                    weave(vector, *piece(4), WINDOW, HALF)
-                    quant_part(*piece(4), 0, WINDOW)
-                    quant_part(*piece(4), WINDOW, HALF)
-                    weave_early(vector, 2)
                     quant_woven(1)
-                    weave_early(vector, 3)
+                    weave_early(vector, 1, 1)
+                    quant_part(*piece(4), 0, WINDOW)
                     quant_woven(2)
-                    weave(vector, "x", 1, 1)
+                    weave(vector, *piece(4), WINDOW, HALF)
                     quant_woven(3)
+                    weave(vector, "x", 1, 1)
+                    quant_part(*piece(4), WINDOW, HALF)
                 for h in range(2):
                     for s in range(2):
                         group0(k, s, h)
@@ -532,21 +528,21 @@ def tile_multiheadattention_pb_v_kernel(tc, values, logw, Wv, Wo, pool_w, grad_o
             weave(scalar, "x", 2, 1)
             weave(scalar, "x", 3, 1)
             quant_staged("x", 1, 1)
-            weave_chunk(vector, 1, 0)
             quant_staged("x", 2, 1)
+            weave_chunk(vector, 1, 0)
             quant_staged("x", 3, 1)
             quant_staged("chunk", 1, 0)
             for q in range(4):
                 product1(0, q, 0, q)
-                pass1(0, q, 1, 0, SUM_BANKS[q])
             for q in range(4):
                 empty(scalar, "o1", 0, q, 0)
                 store1(0, q, 0)
-            for i in range(1, 4):
+            weave_chunk(scalar, 1, 1, 2, 4)
+            for i in range(4):
                 for q in range(4):
                     pass1(0, q, 1, i, SUM_BANKS[q])
             for q in range(1, 4):
-                weave_chunk(vector, 1, q)
+                weave_chunk(vector, 1, q, 0, 2 if q == 1 else 4)
                 if q > 1:
                     quant_staged("chunk", 1, q - 1)
             quant_staged("chunk", 1, 3)

@@ -135,13 +135,13 @@ def tile_multiheadattention_pb_v_kernel(tc, values, logw, Wv, Wo, pool_w, grad_o
                     dst = dst.rearrange("p (c u e) -> p c u e", u=2, e=2)
                 nc.tensor.matmul(dst, lhsT=ident_bf16[:], rhs=src, start=True, stop=True)
 
-        def copy_spun(copy, name, a, h, part):
+        def copy_spun(copy, name, a, h, part, quarters=2):
             dst = stage((name, a, h))[:].rearrange("p c t -> p (c t)").bitcast(F32)
             if name == "wo":
                 dst = dst.rearrange("p (u part w) -> p part u w", u=2, part=2)[:, part]
             else:
                 dst = dst.rearrange("p (part m w) -> p part m w", part=2, m=2)[:, part]
-            copy(out=dst, in_=banks["spun", name, a, h, part][:].bitcast(F32))
+            copy(out=dst[:, 0:quarters], in_=banks["spun", name, a, h, part][:, 0:quarters].bitcast(F32))
 
         def weave_in_window(n, name, a, h, lo, hi):
             if n is None:
@@ -332,22 +332,17 @@ def tile_multiheadattention_pb_v_kernel(tc, values, logw, Wv, Wo, pool_w, grad_o
             cols = slice(HALF * h, HALF * (h + 1))
             nc.sync.dma_start(out=rows_of_out_1(g, q)[:, cols], in_=rows["o1", g, q][:, cols])
 
-        def last_quarter(copy, part, n):
-            acc = bank(n, [P, QUARTER])
-            cols = slice(QUARTER * part, QUARTER * (part + 1))
+        def last_part(copy, lo, hi, n):
+            acc = bank(n, [P, hi - lo])
             for i in range(4):
-                mx_pass(acc[:], ("chunk", 1, 3), i, ("x", i, 1), cols, i == 0, i == 3)
-            piece = work.tile([P, QUARTER], F32, name="last%d" % part)
+                mx_pass(acc[:], ("chunk", 1, 3), i, ("x", i, lo // HALF), slice(lo % HALF, (hi - 1) % HALF + 1), i == 0, i == 3)
+            piece = work.tile([P, hi - lo], F32, name="last%d" % lo)
             copy(out=piece[:], in_=acc[:])
-            first = HALF + QUARTER * part
-            nc.sync.dma_start(out=rows_of_out_1(1, 3)[:, first : first + QUARTER], in_=piece[:])
+            nc.sync.dma_start(out=rows_of_out_1(1, 3)[:, lo:hi], in_=piece[:])
 
         with tc.manual_schedule():
-            done = []
-
-            def group0(k, s, h, copy=scalar):
-                product0(k, s, h, SUM_BANKS[len(done) % 4])
-                done.append((k, s, h))
+            def group0(k, s, h, n=None):
+                product0(k, s, h, SUM_BANKS[(2 * h + s + (k > 0)) % 4] if n is None else n)
                 empty(vector if (k, h) == (5, 0) else scalar, "o0", k, s, h)
                 if h == 1:
                     store0(k, s)
@@ -355,10 +350,9 @@ def tile_multiheadattention_pb_v_kernel(tc, values, logw, Wv, Wo, pool_w, grad_o
             def piece(n):
                 return "x", n % 4, n // 4
 
-            def pair0(k, h):
+            def pair0(k, h, numbers):
                 for s in range(2):
-                    banks["o0", k, s, h] = bank(SUM_BANKS[len(done) % 4], [P, HALF])
-                    done.append((k, s, h))
+                    banks["o0", k, s, h] = bank(numbers[s], [P, HALF])
                 for g in range(2):
                     for s in range(2):
                         mx_pass(banks["o0", k, s, h][:], ("step", k), 2 * g + s, ("wv", g, h), every, g == 0, g == 1)
@@ -369,14 +363,14 @@ def tile_multiheadattention_pb_v_kernel(tc, values, logw, Wv, Wo, pool_w, grad_o
             load_rows_of_wo(0)
             load_go(0, 1)
             load_rows_of_wo(1)
-            load_go(1, 1)
+            load_go(1, 2)
             load_pw(0)
-            load_go(2, 2)
             load_weight("wv", 0, 0)
             load_weight("wv", 1, 0)
             load_weight("wv", 0, 1)
             load_weight("wv", 1, 1)
             load_pw(1)
+            load_go(3, 1)
             load_values(0, 0)
             load_pw(2)
             load_values(1, 0)
@@ -407,63 +401,63 @@ def tile_multiheadattention_pb_v_kernel(tc, values, logw, Wv, Wo, pool_w, grad_o
             copy_go(1, scalar, 2)
             weigh(0, 0)
             turn_go(2, 5)
-            turn_go(3, 6)
+            turn(0, 0)
             copy_go(2)
-            copy_go(3)
+            copy_turned(0, 0)
             quant_staged("wo", 1, 1)
             quant_go(1)
             dattn(0, 1, (1,))
+            spin("wv", 0, 0, 0, 6, (0,))
             spin("wv", 1, 0, 0, 4)
             weave(scalar, "wv", 1, 0, QUARTER, HALF)
-            weave_in_window(2, "wv", 0, 0, 0, HALF)
+            copy_spun(scalar, "wv", 0, 0, 0, 1)
+            weave_in_window(2, "wv", 0, 0, P, HALF)
             weigh(1, 0)
             weigh(0, 1)
             weigh(1, 1)
             copy_spun(scalar, "wv", 1, 0, 0)
-            dattn(1, 0)
-            turn(0, 0)
-            turn(0, 1)
             turn(1, 0, 5)
-            copy_turned(0, 0)
+            turn(0, 1)
+            dattn(1, 0)
+            copy_turned(1, 0)
             copy_turned(0, 1)
             turn(1, 1, 7)
             spin("wv", 0, 1, 0, 6)
             dattn(1, 1)
-            copy_turned(1, 0)
             copy_turned(1, 1)
             quant_staged("wv", 1, 0)
-            quant_part("wv", 0, 0, 0, HALF)
+            quant_part("wv", 0, 0, 0, P)
+            quant_part("wv", 0, 0, P, HALF)
             quant_step(0)
             weave(scalar, "wv", 0, 1, QUARTER, HALF)
             copy_spun(scalar, "wv", 0, 1, 0)
             weave(scalar, "wv", 1, 1, WINDOW, HALF)
-            quant_go(2)
             quant_step(1)
+            quant_go(2)
             group0(0, 0, 0)
             weave_in_window(1, "wv", 1, 1, 0, WINDOW)
             weigh(2, 0)
             weigh(2, 1)
             group0(0, 1, 0)
-            done.append(None)
-            group0(1, 0, 0)
-            done.extend([None, None])
-            group0(1, 1, 0)
-            done.append(None)
+            group0(1, 0, 0, 7)
+            group0(1, 1, 0, 6)
             turn(2, 0)
+            turn_go(3, 4)
             turn(2, 1)
             quant_staged("wv", 0, 1)
             quant_part("wv", 1, 1, 0, WINDOW)
             quant_part("wv", 1, 1, WINDOW, HALF)
             copy_turned(2, 0)
             copy_turned(2, 1)
+            copy_go(3)
             sort_pw()
             weave_in_window(1, "x", 0, 0, 0, WINDOW)
             weigh(3, 0)
             weigh(3, 1)
-            pair0(0, 1)
-            group0(1, 0, 1)
+            pair0(0, 1, (5, 7))
+            group0(1, 0, 1, 6)
             dattn(2, 0)
-            group0(1, 1, 1)
+            group0(1, 1, 1, 4)
             dattn(2, 1)
             quant_step(2)
             quant_go(3)
@@ -492,10 +486,10 @@ def tile_multiheadattention_pb_v_kernel(tc, values, logw, Wv, Wo, pool_w, grad_o
                 if k == 5:
                     weigh(7, 1)
                 if k == 6:
+                    quant_part(*piece(3), 0, WINDOW)
+                    quant_step(6)
                     for n in (0, 2, 3):
                         quant_part(*piece(n), WINDOW, HALF)
-                    quant_step(6)
-                    quant_part(*piece(3), 0, WINDOW)
                     copy_turned(7, 1, vector)
                     weave_early(vector, 0, 0)
                 if k == 3:
@@ -554,8 +548,7 @@ def tile_multiheadattention_pb_v_kernel(tc, values, logw, Wv, Wo, pool_w, grad_o
                     product1(1, q, h, 2 * q + h)
                     empty(scalar, "o1", 1, q, h)
                     store1(1, q, h)
-            product1(1, 3, 0, 6)
-            empty(vector, "o1", 1, 3, 0)
-            store1(1, 3, 0)
-            last_quarter(scalar, 0, 7)
-            last_quarter(vector, 1, 0)
+            last_part(vector, 0, 256, 6)
+            last_part(scalar, 256, 512, 7)
+            last_part(vector, 512, 768, 0)
+            last_part(scalar, 768, 1024, 1)

@@ -135,6 +135,10 @@ def tile_multiheadattention_pb_v_kernel(tc, values, logw, Wv, Wo, pool_w, grad_o
                     dst = dst.rearrange("p (c u e) -> p c u e", u=2, e=2)
                 nc.tensor.matmul(dst, lhsT=ident_bf16[:], rhs=src, start=True, stop=True)
 
+        def warm_up(n=TURN_BANKS[1]):
+            unread = bank(n, [P, HALF])
+            nc.tensor.matmul(unread[:], lhsT=ident_bf16[:], rhs=raw["wo", 0, 0][:, 0, :], start=True, stop=True)
+
         def copy_spun(copy, name, a, h, part, quarters=2):
             dst = stage((name, a, h))[:].rearrange("p c t -> p (c t)").bitcast(F32)
             if name == "wo":
@@ -382,14 +386,16 @@ def tile_multiheadattention_pb_v_kernel(tc, values, logw, Wv, Wo, pool_w, grad_o
             weave(scalar, "wo", 0, 0, LARGE, HALF)
             spin("wo", 0, 1, 0, 4)
             turn_go(0, 6)
-            spin("wo", 0, 1, 1, 5)
+            warm_up()
+            warm_up()
             quant_staged("wo", 0, 0)
+            weave(scalar, "wo", 0, 1, QUARTER, HALF)
             copy_spun(scalar, "wo", 0, 1, 0)
             copy_go(0, vector)
             weave(vector, "wo", 1, 0, 0, LARGE)
             weave(scalar, "wo", 1, 0, LARGE, HALF)
-            copy_spun(scalar, "wo", 0, 1, 1)
             spin("wo", 1, 1, 0, 7)
+            warm_up()
             quant_go(0)
             quant_staged("wo", 1, 0)
             weave(scalar, "wo", 1, 1, QUARTER, HALF)
@@ -407,27 +413,28 @@ def tile_multiheadattention_pb_v_kernel(tc, values, logw, Wv, Wo, pool_w, grad_o
             quant_staged("wo", 1, 1)
             quant_go(1)
             dattn(0, 1, (1,))
-            spin("wv", 0, 0, 0, 6, (0,))
-            spin("wv", 1, 0, 0, 4)
+            spin("wv", 1, 0, 0, 4, (0,))
+            warm_up()
+            spin("wv", 1, 0, 0, 4, (1,))
             weave(scalar, "wv", 1, 0, QUARTER, HALF)
-            copy_spun(scalar, "wv", 0, 0, 0, 1)
-            weave_in_window(2, "wv", 0, 0, P, HALF)
+            weave_in_window(2, "wv", 0, 0, 0, HALF)
             weigh(1, 0)
             weigh(0, 1)
             weigh(1, 1)
             copy_spun(scalar, "wv", 1, 0, 0)
+            dattn(1, 0, (0,))
             turn(1, 0, 5)
             turn(0, 1)
-            dattn(1, 0)
+            dattn(1, 0, (1,))
             copy_turned(1, 0)
             copy_turned(0, 1)
+            spin("wv", 0, 1, 0, 6, (0,))
             turn(1, 1, 7)
-            spin("wv", 0, 1, 0, 6)
             dattn(1, 1)
+            spin("wv", 0, 1, 0, 6, (1,))
             copy_turned(1, 1)
             quant_staged("wv", 1, 0)
-            quant_part("wv", 0, 0, 0, P)
-            quant_part("wv", 0, 0, P, HALF)
+            quant_part("wv", 0, 0, 0, HALF)
             quant_step(0)
             weave(scalar, "wv", 0, 1, QUARTER, HALF)
             copy_spun(scalar, "wv", 0, 1, 0)

from contextlib import ExitStack

import concourse.mybir as mybir
from concourse.masks import make_identity

FLOPS = 2 * 512 * 1024 * 1024 + 2 * 2 * 2048 * 1024 * 1024
BYTES = 2 * (4 * 512 * 1024 + 2 * 1024 * 1024 + 512 * 1024) + 4 * 4 * 512 * 16 + 4 * (2048 * 1024 + 1024 * 1024)

F32 = mybir.dt.float32
BF16 = mybir.dt.bfloat16
U32 = mybir.dt.uint32
U8 = mybir.dt.uint8
E4 = mybir.dt.float8_e4m3fn_x4
E5 = mybir.dt.float8_e5m2_x4
MULT = mybir.AluOpType.mult
ADD = mybir.AluOpType.add

P = 128
HALF = 512
QUARTER = 256
STEPS = 8
EARLY = 2
RUN = 2

WEAVE_BUFS = 5
SWAP_BUFS = 3
ROW_BUFS = 8
DVP_CODE_BUFS = 6

LARGE = 320
WINDOW = 384

DATTN_BANKS = (0, 1)
TURN_BANKS = (2, 3)
SUM_BANKS = (4, 5, 6, 7)


def tile_multiheadattention_pb_v_kernel(tc, values, logw, Wv, Wo, pool_w, grad_out, out_0, out_1):
    nc = tc.nc
    vector, scalar = nc.vector.tensor_copy, nc.scalar.copy
    with ExitStack() as ctx:
        keep = ctx.enter_context(tc.tile_pool(name="keep", bufs=1))
        work = ctx.enter_context(tc.tile_pool(name="work", bufs=1))
        psum = ctx.enter_context(tc.psum_pool(name="psum", bufs=1))

        ident = keep.tile([P, P], F32, name="ident")
        make_identity(nc, ident[:])
        ident_bf16 = keep.tile([P, P], BF16, name="ident_bf16")
        make_identity(nc, ident_bf16[:])
        pw = keep.tile([P, 4, 4, 16], F32, name="pw")
        pw_by_head = keep.tile([P, 4 - EARLY, 8, 4], F32, name="pw_by_head")
        all_woven = keep.tile([P, 4 * 4 * HALF], BF16, name="woven", align_bytes=64)
        woven = [all_woven[:, 4 * HALF * q : 4 * HALF * (q + 1)] for q in range(4)]
        planes = [
            keep.tile([P, n * 4 * HALF], BF16, name="planes%d" % g, align_bytes=64) for g, n in enumerate((EARLY, 4))
        ]
        raw = {}
        staged = {}
        codes = {}
        scales = {}
        banks = {}
        rows = {}

        def bank(n, shape, dtype=F32):
            return psum.tile(shape, dtype, name="bank%d" % n)

        def swap(n, shape, dtype):
            return work.tile(shape, dtype, name="swap%d" % (n % SWAP_BUFS), align_bytes=64)

        def stage(key):
            if key not in staged:
                staged[key] = work.tile([P, HALF, 4], BF16, name="stage", bufs=WEAVE_BUFS, align_bytes=64)
            return staged[key]

        def load_pw(i):
            nc.sync.dma_start(out=pw[:, i], in_=pool_w[:, P * i : P * (i + 1), :].rearrange("s p h -> p s h"))

        def load_go(first, n):
            tiles = keep.tile([P, n, 2 * HALF], BF16, name="go_raw%d" % first)
            src = grad_out[P * first : P * (first + n), :]
            nc.sync.dma_start(out=tiles[:], in_=src.rearrange("(i p) o -> p i o", p=P))
            for i in range(n):
                raw["go", first + i] = tiles[:, i, :]

        def load_weight(name, a, h):
            tile = keep.tile([P, 4, HALF], BF16, name="raw_%s%d" % (name, 2 * h + a))
            src = {"wo": Wo, "wv": Wv}[name][HALF * a : HALF * (a + 1), HALF * h : HALF * (h + 1)]
            nc.sync.dma_start(out=tile[:], in_=src.rearrange("(p j) c -> p j c", j=4))
            raw[name, a, h] = tile[:]

        def load_rows_of_wo(a):
            tile = keep.tile([P, 4, 2 * HALF], BF16, name="rows_wo%d" % a)
            nc.sync.dma_start(out=tile[:], in_=Wo[HALF * a : HALF * (a + 1), :].rearrange("(p j) c -> p j c", j=4))
            for h in range(2):
                raw["wo", a, h] = tile[:, :, HALF * h : HALF * (h + 1)]

        def load_values(i, h):
            tile = keep.tile([P, 4, HALF], BF16, name="raw_%s%d" % ("wv" if h else "x", i))
            src = values[:, P * i : P * (i + 1), HALF * h : HALF * (h + 1)]
            nc.sync.dma_start(out=tile[:], in_=src.rearrange("s p d -> p s d"))
            raw["x", i, h] = tile[:]

        def weave(copy, name, a, h, lo=0, hi=HALF):
            src = raw[name, a, h][:, :, lo:hi]
            dst = stage((name, a, h))
            if name == "wo":
                dst = dst[:].rearrange("p (u r) t -> p u r t", u=2)[:, :, lo // 2 : hi // 2, :]
                copy(
                    out=dst.rearrange("p u (r l) t -> p r u t l", l=RUN),
                    in_=src.rearrange("p t (r l u) -> p r u t l", l=RUN, u=2),
                )
            elif name == "wv":
                copy(
                    out=dst[:, lo:hi, :].rearrange("p (c l) (u e) -> p c u e l", l=RUN, u=2),
                    in_=src.rearrange("p (e u) (c l) -> p c u e l", l=RUN, u=2),
                )
            else:
                copy(
                    out=dst[:, lo:hi, :].rearrange("p (c l) s -> p c s l", l=RUN),
                    in_=src.rearrange("p s (c l) -> p c s l", l=RUN),
                )

        def spin(name, a, h, part, n, quarters=(0, 1)):
            if 0 in quarters:
                banks["spun", name, a, h, part] = bank(n, [P, 2, HALF], BF16)
            for m in quarters:
                first = QUARTER * part + P * m
                src = raw[name, a, h]
                dst = banks["spun", name, a, h, part][:, m, :]
                if name == "wo":
                    src = src.rearrange("p t (r u) -> p u r t", u=2)[:, m, P * part : P * (part + 1), :]
                    dst = dst.rearrange("p (r t) -> p r t", t=4)
                else:
                    src = src[:, :, first : first + P].rearrange("p (e u) c -> p c u e", u=2)
                    dst = dst.rearrange("p (c u e) -> p c u e", u=2, e=2)
                nc.tensor.matmul(dst, lhsT=ident_bf16[:], rhs=src, start=True, stop=True)

        def warm_up(n=TURN_BANKS[1]):
            unread = bank(n, [P, HALF])
            nc.tensor.matmul(unread[:], lhsT=ident_bf16[:], rhs=raw["wo", 0, 0][:, 0, :], start=True, stop=True)

        def copy_spun(copy, name, a, h, part, quarters=2):
            dst = stage((name, a, h))[:].rearrange("p c t -> p (c t)").bitcast(F32)
            if name == "wo":
                dst = dst.rearrange("p (u part w) -> p part u w", u=2, part=2)[:, part]
            else:
                dst = dst.rearrange("p (part m w) -> p part m w", part=2, m=2)[:, part]
            copy(out=dst[:, 0:quarters], in_=banks["spun", name, a, h, part][:, 0:quarters].bitcast(F32))

        def weave_in_window(n, name, a, h, lo, hi):
            if n is None:
                staged["window", name, a, h, lo] = work.tile([P, hi - lo, 4], BF16, name="piece", align_bytes=64)
            else:
                staged["window", name, a, h, lo] = swap(n, [P, hi - lo, 4], BF16)
            src = raw[name, a, h][:, :, lo:hi]
            dst = staged["window", name, a, h, lo][:]
            if name == "wo":
                src = raw[name, a, h].rearrange("p t (r u) -> p u r t", u=2)[:, lo // QUARTER]
            elif name == "wv":
                src = src.rearrange("p (e u) c -> p c u e", u=2)
                dst = dst.rearrange("p c (u e) -> p c u e", u=2)
            else:
                src = src.rearrange("p s c -> p c s")
            nc.gpsimd.tensor_scalar(out=dst, in0=src, scalar1=1.0, scalar2=0.0, op0=MULT, op1=ADD)

        def sort_pw():
            scalar(out=pw_by_head[:], in_=pw[:, EARLY:, :, 0:8].rearrange("p i s h -> p i h s"))

        def weave_early(copy, i, u):
            src = planes[0][:].rearrange("p (i s u c l e) -> p i u c e s l", i=EARLY, s=4, u=2, l=RUN, e=2)
            dst = all_woven[:].rearrange("p (u e i c l s) -> p i u c e s l", u=2, e=2, i=4, l=RUN, s=4)
            copy(out=dst[:, i, u], in_=src[:, i, u])

        def quant_woven(q):
            quantise(("chunk", 0, q), woven[q], E5)

        def weigh_woven(i, u):
            shape = [P, 8, 16, 4]
            for e in range(2):
                column = banks["dattn", i, 0][:, QUARTER * u + e : QUARTER * (u + 1) : 2]
                nc.vector.tensor_tensor(
                    out=woven[2 * u + e][:, HALF * i : HALF * (i + 1)].rearrange("p (h m s) -> p h m s", h=8, s=4),
                    in0=pw_by_head[:, i - EARLY].unsqueeze(2).to_broadcast(shape),
                    in1=column.rearrange("p (h m) -> p h m", h=8).unsqueeze(3).to_broadcast(shape),
                    op=MULT,
                )

        def weave_chunk(copy, g, q, lo=0, hi=4):
            src = planes[g][:].rearrange("p (i s j) -> p i s j", i=4, s=4)[:, lo:hi, :, P * q : P * (q + 1)]
            dst = stage(("chunk", g, q))[:].rearrange("p (i j) s -> p i j s", i=4)[:, lo:hi]
            copy(
                out=dst.rearrange("p i (c l) s -> p i c s l", l=RUN),
                in_=src.rearrange("p i s (c l) -> p i c s l", l=RUN),
            )

        def new_operand(key, width):
            if key[0] in ("step", "chunk"):
                codes[key] = work.tile([P, width], U32, name="q_dvp", bufs=DVP_CODE_BUFS, align_bytes=64)
                scales[key] = work.tile([P, width], U8, name="s_dvp", bufs=DVP_CODE_BUFS, align_bytes=64)
            else:
                tag = "_".join(str(part) for part in key)
                codes[key] = keep.tile([P, width], U32, name="q_" + tag, align_bytes=64)
                scales[key] = keep.tile([P, width], U8, name="s_" + tag, align_bytes=64)

        def quantise(key, src, fmt):
            new_operand(key, src.shape[1] // 4)
            nc.vector.quantize_mx(out=codes[key][:].bitcast(fmt), scales=scales[key][:], in_=src)

        def quant_staged(name, a, h):
            quantise((name, a, h), staged[name, a, h][:].rearrange("p c t -> p (c t)"), E5 if name == "chunk" else E4)

        def quant_part(name, a, h, lo, hi):
            if (name, a, h) not in codes:
                new_operand((name, a, h), HALF)
            piece = ("window", name, a, h, lo)
            src = staged[piece][:] if piece in staged else staged[name, a, h][:, lo:hi, :]
            nc.vector.quantize_mx(
                out=codes[name, a, h][:, lo:hi].bitcast(E4),
                scales=scales[name, a, h][:, lo:hi],
                in_=src.rearrange("p c t -> p (c t)"),
            )

        def quant_step(k):
            quantise(("step", k), staged["step", k][:].bitcast(BF16), E5)

        def mx_pass(out, left, m, right, cols, start, stop):
            window = slice(P * m, P * (m + 1))
            nc.tensor.matmul_mx(
                out=out,
                lhsT=codes[left][:, window].bitcast(E5),
                lhsT_scale=scales[left][:, window],
                rhs=codes[right][:, cols].bitcast(E4),
                rhs_scale=scales[right][:, cols],
                start=start,
                stop=stop,
            )

        every = slice(0, HALF)

        def turn_go(i, n):
            banks["go", i] = bank(n, [P, 4, P])
            words = raw["go", i].bitcast(F32)
            for a in range(2):
                for u in range(2):
                    src = words[:, QUARTER * a + u : QUARTER * (a + 1) : 2]
                    nc.tensor.transpose(banks["go", i][:, 2 * a + u, :], src, ident[:])

        def copy_go(i, copy=scalar, n=None):
            if n is None:
                staged["go", i] = work.tile([P, HALF], F32, name="go_turned", bufs=2, align_bytes=64)
            else:
                staged["go", i] = swap(n, [P, HALF], F32)
            copy(
                out=staged["go", i][:].rearrange("p (a b l u) -> p a b u l", a=2, u=2, l=RUN),
                in_=banks["go", i][:].rearrange("p (a u) (b l) -> p a b u l", u=2, l=RUN),
            )

        def quant_go(i):
            quantise(("go", i), staged["go", i][:].bitcast(BF16), E5)

        def dattn(i, g, passes=(0, 1)):
            if 0 in passes:
                banks["dattn", i, g] = bank(DATTN_BANKS[g], [P, HALF])
            for a in passes:
                mx_pass(banks["dattn", i, g][:], ("go", i), a, ("wo", a, g), every, a == 0, a == 1)

        def plane(g, i, s):
            return planes[g][:, HALF * (4 * i + s) : HALF * (4 * i + s + 1)]

        def weigh(k, g):
            i, pair = divmod(k, 2)
            for s in (2 * pair, 2 * pair + 1):
                nc.vector.tensor_tensor(
                    out=plane(g, i, s).rearrange("p (u h r) -> p u h r", u=2, h=8),
                    in0=pw[:, i, s, 8 * g : 8 * (g + 1)].unsqueeze(1).unsqueeze(3).to_broadcast([P, 2, 8, 32]),
                    in1=banks["dattn", i, g][:].rearrange("p (u h r) -> p u h r", u=2, h=8),
                    op=MULT,
                )

        def turn(k, g, n=None):
            banks["turn", k, g] = bank(TURN_BANKS[g] if n is None else n, [P, 4, P])
            i, pair = divmod(k, 2)
            for q in range(4):
                if g == 0 and i >= EARLY:
                    words = woven[q].bitcast(F32)[:, QUARTER * i + pair : QUARTER * (i + 1) : 2]
                else:
                    words = plane(g, i, 2 * pair + q // 2).bitcast(F32)[:, P * (q % 2) : P * (q % 2 + 1)]
                nc.tensor.transpose(banks["turn", k, g][:, q, :], words, ident[:])

        def copy_turned(k, g, copy=scalar):
            if g == 0:
                staged["step", k] = swap(k, [P, 2 * HALF], F32)
            dst = staged["step", k][:, HALF * g : HALF * (g + 1)]
            src = banks["turn", k, g][:]
            if g == 0 and k // 2 >= EARLY:
                copy(
                    out=dst.bitcast(BF16).rearrange("p (s b q) -> p s b q", s=2, q=4),
                    in_=src.rearrange("p q b -> p (q b)").bitcast(BF16).rearrange("p (q b s) -> p s b q", q=4, s=2),
                )
            else:
                copy(
                    out=dst.rearrange("p (s b u) -> p s b u", s=2, u=2),
                    in_=src.rearrange("p (s u) b -> p s b u", u=2),
                )

        def product0(k, s, h, n):
            banks["o0", k, s, h] = bank(n, [P, HALF])
            for g in range(2):
                mx_pass(banks["o0", k, s, h][:], ("step", k), 2 * g + s, ("wv", g, h), every, g == 0, g == 1)

        def pass1(g, q, h, i, n):
            if i == 0:
                banks["o1", g, q, h] = bank(n, [P, HALF])
            mx_pass(banks["o1", g, q, h][:], ("chunk", g, q), i, ("x", i, h), every, i == 0, i == 3)

        def product1(g, q, h, n):
            for i in range(4):
                pass1(g, q, h, i, n)

        def rows_of_out_1(g, q):
            if g == 0:
                return out_1[0:HALF, :].rearrange("(m t) d -> t m d", t=4)[2 * (q % 2) + q // 2]
            first = HALF + QUARTER * (q % 2)
            return out_1[first : first + QUARTER, :].rearrange("(r u) d -> u r d", u=2)[q // 2]

        def empty(copy, name, a, b, h):
            if (name, a, b) not in rows:
                rows[name, a, b] = work.tile([P, 2 * HALF], F32, name="rows", bufs=ROW_BUFS)
            copy(out=rows[name, a, b][:, HALF * h : HALF * (h + 1)], in_=banks[name, a, b, h][:])

        def store0(k, s):
            i, pair = divmod(k, 2)
            nc.sync.dma_start(out=out_0[2 * pair + s, P * i : P * (i + 1), :], in_=rows["o0", k, s][:])

        def store1(g, q, h):
            cols = slice(HALF * h, HALF * (h + 1))
            nc.sync.dma_start(out=rows_of_out_1(g, q)[:, cols], in_=rows["o1", g, q][:, cols])

        def last_part(copy, lo, hi, n):
            acc = bank(n, [P, hi - lo])
            for i in range(4):
                mx_pass(acc[:], ("chunk", 1, 3), i, ("x", i, lo // HALF), slice(lo % HALF, (hi - 1) % HALF + 1), i == 0, i == 3)
            piece = work.tile([P, hi - lo], F32, name="last%d" % lo)
            copy(out=piece[:], in_=acc[:])
            nc.sync.dma_start(out=rows_of_out_1(1, 3)[:, lo:hi], in_=piece[:])

        with tc.manual_schedule():
            def group0(k, s, h, n=None):
                product0(k, s, h, SUM_BANKS[(2 * h + s + (k > 0)) % 4] if n is None else n)
                empty(vector if (k, h) == (5, 0) else scalar, "o0", k, s, h)
                if h == 1:
                    store0(k, s)

            def piece(n):
                return "x", n % 4, n // 4

            def pair0(k, h, numbers):
                for s in range(2):
                    banks["o0", k, s, h] = bank(numbers[s], [P, HALF])
                for g in range(2):
                    for s in range(2):
                        mx_pass(banks["o0", k, s, h][:], ("step", k), 2 * g + s, ("wv", g, h), every, g == 0, g == 1)
                for s in range(2):
                    empty(scalar, "o0", k, s, h)
                    store0(k, s)

            load_rows_of_wo(0)
            load_go(0, 1)
            load_rows_of_wo(1)
            load_go(1, 2)
            load_pw(0)
            load_weight("wv", 0, 0)
            load_weight("wv", 1, 0)
            load_weight("wv", 0, 1)
            load_weight("wv", 1, 1)
            load_pw(1)
            load_go(3, 1)
            load_values(0, 0)
            load_pw(2)
            load_values(1, 0)
            load_pw(3)
            load_values(2, 0)
            load_values(3, 0)

            weave(vector, "wo", 0, 0, 0, LARGE)
            weave(scalar, "wo", 0, 0, LARGE, HALF)
            spin("wo", 0, 1, 0, 4)
            turn_go(0, 6)
            warm_up()
            warm_up()
            quant_staged("wo", 0, 0)
            weave(scalar, "wo", 0, 1, QUARTER, HALF)
            copy_spun(scalar, "wo", 0, 1, 0)
            copy_go(0, vector)
            weave(vector, "wo", 1, 0, 0, LARGE)
            weave(scalar, "wo", 1, 0, LARGE, HALF)
            spin("wo", 1, 1, 0, 7)
            warm_up()
            quant_go(0)
            quant_staged("wo", 1, 0)
            weave(scalar, "wo", 1, 1, QUARTER, HALF)
            dattn(0, 0)
            quant_staged("wo", 0, 1)
            copy_spun(scalar, "wo", 1, 1, 0)
            turn_go(1, 4)
            dattn(0, 1, (0,))
            copy_go(1, scalar, 2)
            weigh(0, 0)
            turn_go(2, 5)
            turn(0, 0)
            copy_go(2)
            copy_turned(0, 0)
            quant_staged("wo", 1, 1)
            quant_go(1)
            dattn(0, 1, (1,))
            spin("wv", 1, 0, 0, 4, (0,))
            warm_up()
            spin("wv", 1, 0, 0, 4, (1,))
            weave(scalar, "wv", 1, 0, QUARTER, HALF)
            weave_in_window(2, "wv", 0, 0, 0, HALF)
            weigh(1, 0)
            weigh(0, 1)
            weigh(1, 1)
            copy_spun(scalar, "wv", 1, 0, 0)
            dattn(1, 0, (0,))
            turn(1, 0, 5)
            turn(0, 1)
            dattn(1, 0, (1,))
            copy_turned(1, 0)
            copy_turned(0, 1)
            spin("wv", 0, 1, 0, 6, (0,))
            turn(1, 1, 7)
            dattn(1, 1)
            spin("wv", 0, 1, 0, 6, (1,))
            copy_turned(1, 1)
            quant_staged("wv", 1, 0)
            quant_part("wv", 0, 0, 0, HALF)
            quant_step(0)
            weave(scalar, "wv", 0, 1, QUARTER, HALF)
            copy_spun(scalar, "wv", 0, 1, 0)
            weave(scalar, "wv", 1, 1, WINDOW, HALF)
            quant_step(1)
            quant_go(2)
            group0(0, 0, 0)
            weave_in_window(1, "wv", 1, 1, 0, WINDOW)
            weigh(2, 0)
            weigh(2, 1)
            group0(0, 1, 0)
            group0(1, 0, 0, 7)
            group0(1, 1, 0, 6)
            turn(2, 0)
            turn_go(3, 4)
            turn(2, 1)
            quant_staged("wv", 0, 1)
            quant_part("wv", 1, 1, 0, WINDOW)
            quant_part("wv", 1, 1, WINDOW, HALF)
            copy_turned(2, 0)
            copy_turned(2, 1)
            copy_go(3)
            sort_pw()
            weave_in_window(1, "x", 0, 0, 0, WINDOW)
            weigh(3, 0)
            weigh(3, 1)
            pair0(0, 1, (5, 7))
            group0(1, 0, 1, 6)
            dattn(2, 0)
            group0(1, 1, 1, 4)
            dattn(2, 1)
            quant_step(2)
            quant_go(3)

            for k in range(2, STEPS):
                if k <= 5:
                    load_values(k - 2, 1)
                if k + 1 < STEPS:
                    turn(k + 1, 0)
                    turn(k + 1, 1)
                    copy_turned(k + 1, 0)
                    if k < 6:
                        copy_turned(k + 1, 1)
                if k + 2 < STEPS:
                    weave_in_window(k, *piece(k - 1), 0, HALF if k == 2 else WINDOW)
                if k == 2:
                    weigh_woven(2, 0)
                    weigh_woven(2, 1)
                    weigh(4, 1)
                if k == 3:
                    weigh(5, 1)
                    weigh_woven(3, 0)
                if k == 4:
                    weigh_woven(3, 1)
                    weigh(6, 1)
                if k == 5:
                    weigh(7, 1)
                if k == 6:
                    quant_part(*piece(3), 0, WINDOW)
                    quant_step(6)
                    for n in (0, 2, 3):
                        quant_part(*piece(n), WINDOW, HALF)
                    copy_turned(7, 1, vector)
                    weave_early(vector, 0, 0)
                if k == 3:
                    for n in (2, 3):
                        weave(vector, *piece(n), WINDOW, HALF)
                if k + 1 < STEPS and k != 5:
                    quant_step(k + 1)
                if k <= 4:
                    quant_part(*piece(k - 2), 0, HALF if k == 3 else WINDOW)
                if k == 6:
                    weave_early(vector, 1, 0)
                    weave_early(vector, 0, 1)
                    quant_woven(0)
                    quant_woven(1)
                    weave_early(vector, 1, 1)
                    quant_part(*piece(4), 0, WINDOW)
                    quant_woven(2)
                    weave(vector, *piece(4), WINDOW, HALF)
                    quant_woven(3)
                    weave(vector, "x", 1, 1)
                    quant_part(*piece(4), WINDOW, HALF)
                for h in range(2):
                    for s in range(2):
                        group0(k, s, h)
                    if (k, h) in ((2, 1), (3, 1)):
                        dattn(3, k - 2)
                if k == 2:
                    weave(scalar, *piece(0), WINDOW, HALF)

            weave(scalar, "x", 2, 1)
            weave(scalar, "x", 3, 1)
            quant_staged("x", 1, 1)
            quant_staged("x", 2, 1)
            weave_chunk(vector, 1, 0)
            quant_staged("x", 3, 1)
            quant_staged("chunk", 1, 0)
            for q in range(4):
                product1(0, q, 0, q)
            for q in range(4):
                empty(scalar, "o1", 0, q, 0)
                store1(0, q, 0)
            weave_chunk(scalar, 1, 1, 2, 4)
            for i in range(4):
                for q in range(4):
                    pass1(0, q, 1, i, SUM_BANKS[q])
            for q in range(1, 4):
                weave_chunk(vector, 1, q, 0, 2 if q == 1 else 4)
                if q > 1:
                    quant_staged("chunk", 1, q - 1)
            quant_staged("chunk", 1, 3)
            for q in range(4):
                empty(scalar, "o1", 0, q, 1)
                store1(0, q, 1)
            for q in range(3):
                for h in range(2):
                    product1(1, q, h, 2 * q + h)
                    empty(scalar, "o1", 1, q, h)
                    store1(1, q, h)
            last_part(vector, 0, 256, 6)
            last_part(scalar, 256, 512, 7)
            last_part(vector, 512, 768, 0)
            last_part(scalar, 768, 1024, 1)
